import numpy as np
import ml_dtypes


def mxq(x, axis, fmt="e4m3"):
    dtype, down = {"e4m3": (ml_dtypes.float8_e4m3fn, 7), "e5m2": (ml_dtypes.float8_e5m2, 14)}[fmt]
    v = np.moveaxis(np.asarray(x, np.float32).astype(ml_dtypes.bfloat16).astype(np.float64), axis, -1)
    blocks = v.reshape(v.shape[:-1] + (-1, 32))
    amax = np.abs(blocks).max(-1, keepdims=True)
    byte = np.maximum(np.where(amax > 0, np.frexp(amax)[1] - 1 + 127, 0) - down, 1)
    scale = np.exp2(byte - 127.0)
    codes = (blocks / scale).astype(np.float32).astype(dtype).astype(np.float64)
    return np.moveaxis((codes * scale).reshape(v.shape), -1, axis)


WIDE = False


def mx_kscale(k):
    if not WIDE:
        return np.ones(k)
    levels = np.array([10, -10, 5, -5, 0])
    a = np.random.permutation(np.resize(levels, k // 512 * 4)).reshape(k // 512, 4)
    idx = np.arange(k)
    return np.exp2(a[idx // 512, idx % 128 // 32])


BF16 = ml_dtypes.bfloat16


def bf(x):
    return np.asarray(x, np.float32).astype(BF16)


def f64(x):
    return np.asarray(x).astype(np.float64)


B, N, C, E = 2, 512, 1024, 1024
EPS_SUM = 1e-7
EPS_NORM = 1e-12


def setup_inputs():
    s = mx_kscale(C)
    r = np.random.uniform(0.5, 1.5, (B, N, 1))
    return {"x": bf(np.random.standard_normal((B, N, C)) * r * s),
            "wk": bf(np.random.standard_normal((C, E)) / np.sqrt(C) / s[:, None]),
            "bk": bf(0.3 + 0.3 * np.random.standard_normal(E)),
            "wv": bf(np.random.standard_normal((C, E)) / np.sqrt(C) / s[:, None]),
            "bv": bf(0.1 * np.random.standard_normal(E))}


def reference(x, wk, bk, wv, bv):
    xq = mxq(f64(x), 2, "e4m3")
    k = (xq @ mxq(f64(wk), 0, "e4m3")) + f64(bk)
    v = (xq @ mxq(f64(wv), 0, "e4m3")) + f64(bv)
    k = k - k.mean(axis=2, keepdims=True)
    k2 = k * k
    k2 = k2 / (k2.sum(axis=2, keepdims=True) + EPS_SUM)
    nrm = np.sqrt((k2 * k2).sum(axis=1, keepdims=True))
    k2 = k2 / np.maximum(nrm, EPS_NORM)
    kv = mxq(k2, 1, "e4m3").transpose(0, 2, 1) @ mxq(v, 1, "e4m3")
    return kv, v

@@ -1,0 +1,321 @@
+from contextlib import ExitStack
+
+import concourse.mybir as mybir
+from concourse.masks import make_identity
+
+F32 = mybir.dt.float32
+BF16 = mybir.dt.bfloat16
+U32 = mybir.dt.uint32
+U8 = mybir.dt.uint8
+FP8X4 = mybir.dt.float8_e4m3fn_x4
+ALU = mybir.AluOpType
+ACT = mybir.ActivationFunctionType
+
+P = 128
+PACK = 4
+B, N, C, E = 2, 512, 1024, 1024
+T = N // P
+PASSES = C // (P * PACK)
+BANK = 512
+HALVES = E // BANK
+CHUNKS = E // P
+EPS_SUM = 1e-7
+EPS_NORM = 1e-12
+
+FLOPS = 2 * (2 * B * N * C * E) + 2 * B * N * E * E
+
+
+def tile_essattn_pa_kernel(tc, x, wk, bk, wv, bv, out_0, out_1):
+    nc = tc.nc
+    with ExitStack() as ctx:
+        const = ctx.enter_context(tc.tile_pool(name="const", bufs=1))
+        keep = ctx.enter_context(tc.tile_pool(name="keep", bufs=1))
+        raw = ctx.enter_context(tc.tile_pool(name="raw", bufs=3))
+        stage = ctx.enter_context(tc.tile_pool(name="stage", bufs=2))
+        work = ctx.enter_context(tc.tile_pool(name="work", bufs=3))
+        small = ctx.enter_context(tc.tile_pool(name="small", bufs=4))
+        rows = ctx.enter_context(tc.tile_pool(name="rows", bufs=4))
+        psum = ctx.enter_context(tc.psum_pool(name="psum", bufs=8))
+        ctx.enter_context(tc.manual_schedule())
+
+        ident = const.tile([P, P], F32)
+        make_identity(nc, ident[:])
+        ones_bf = const.tile([P, P], BF16)
+        nc.vector.memset(ones_bf[:], 1.0)
+        ones_col = const.tile([P, 1], F32)
+        nc.vector.memset(ones_col[:], 1.0)
+        eps_sum = const.tile([P, 1], F32)
+        nc.vector.memset(eps_sum[:], EPS_SUM)
+        warm = const.tile([P, 1], F32)
+        nc.scalar.activation(out=warm[:], in_=ones_col[:], func=ACT.Abs_reciprocal_sqrt)
+
+        x_raw = [keep.tile([P, T, C], BF16, name="x_raw%d" % b) for b in range(B)]
+
+        def load_x(b):
+            tokens = x[b].rearrange("(p t) c -> p t c", t=T)
+            for half in range(2):
+                pair = slice(2 * half, 2 * half + 2)
+                nc.sync.dma_start(out=x_raw[b][:, pair, :], in_=tokens[:, pair, :])
+
+        def load_w(w):
+            tiles = []
+            for g in range(PASSES):
+                w_raw = raw.tile([P, PACK, E], BF16, name="w_raw")
+                for u in range(2):
+                    first = g * P * PACK + u * 2 * P
+                    nc.sync.dma_start(
+                        out=w_raw[:, 2 * u : 2 * u + 2, :],
+                        in_=w[first : first + 2 * P, :].rearrange("(q e) n -> q e n", e=2),
+                    )
+                tiles.append(w_raw)
+            return tiles
+
+        bias_rows = const.tile([P, 2, E], BF16)
+        nc.vector.memset(bias_rows[:], 0.0)
+
+        wk_raw = load_w(wk)
+        load_x(0)
+        nc.sync.dma_start(out=bias_rows[0:1, 0, :], in_=bk.unsqueeze(0))
+        nc.sync.dma_start(out=bias_rows[0:1, 1, :], in_=bv.unsqueeze(0))
+        wv_raw = load_w(wv)
+        load_x(1)
+
+        bias_all = const.tile([P, 2, E], F32)
+
+        def spread_biases():
+            for i in range(2):
+                for h in range(HALVES):
+                    cols = slice(h * BANK, (h + 1) * BANK)
+                    bank = psum.tile([P, BANK], F32, name="bank")
+                    nc.tensor.matmul(out=bank[:], lhsT=ones_bf[:], rhs=bias_rows[:, i, cols], start=True, stop=True)
+                    nc.scalar.copy(out=bias_all[:, i, cols], in_=bank[:])
+
+        x_codes = keep.tile([P, B * T, PASSES * P], U32, align_bytes=64)
+        x_scales = keep.tile([P, B * T, PASSES * P], U8, align_bytes=64)
+
+        def prepare_x(b):
+            words = x_raw[b][:].bitcast(F32)
+            banks = []
+            for t in range(T):
+                bank = psum.tile([P, BANK], F32, name="bank")
+                for q in range(PASSES * 2):
+                    nc.tensor.transpose(bank[:, q * P : (q + 1) * P], words[:, t, q * P : (q + 1) * P], ident[:])
+                banks.append(bank)
+            grouped = []
+            for t in range(T + 1):
+                if t < T:
+                    x_grp = stage.tile([P, PASSES * P * PACK], BF16, align_bytes=64, name="x_grp")
+                    nc.scalar.copy(
+                        out=x_grp[:].bitcast(F32).rearrange("p (g r u) -> p g r u", g=PASSES, u=2),
+                        in_=banks[t][:].rearrange("p (g u r) -> p g r u", g=PASSES, u=2),
+                    )
+                    grouped.append(x_grp)
+                if t > 0:
+                    nc.vector.quantize_mx(
+                        out=x_codes[:, b * T + t - 1, :].bitcast(FP8X4),
+                        scales=x_scales[:, b * T + t - 1, :],
+                        in_=grouped[t - 1][:],
+                    )
+
+        def prepare_w(w_raw, name):
+            codes = keep.tile([P, PASSES, E], U32, align_bytes=64, name=name + "_codes")
+            scales = keep.tile([P, PASSES, E], U8, align_bytes=64, name=name + "_scales")
+            grouped = []
+            for g in range(PASSES):
+                w_grp = stage.tile([P, E, PACK], BF16, align_bytes=64, name="w_grp")
+                for h, copy in enumerate((nc.vector.tensor_copy, nc.scalar.copy)):
+                    cols = slice(h * BANK, (h + 1) * BANK)
+                    copy(
+                        out=w_grp[:, cols, :].rearrange("p (c i) t -> p c t i", i=4),
+                        in_=w_raw[g][:, :, cols].rearrange("p t (c i) -> p c t i", i=4),
+                    )
+                grouped.append(w_grp)
+            for g in range(PASSES):
+                for h in range(HALVES):
+                    cols = slice(h * BANK, (h + 1) * BANK)
+                    nc.vector.quantize_mx(
+                        out=codes[:, g, cols].bitcast(FP8X4),
+                        scales=scales[:, g, cols],
+                        in_=grouped[g][:, cols, :].rearrange("p n t -> p (n t)"),
+                    )
+            return codes, scales
+
+        def project(w_codes, w_scales, tile_index):
+            banks = []
+            for h in range(HALVES):
+                cols = slice(h * BANK, (h + 1) * BANK)
+                bank = psum.tile([P, BANK], F32, name="bank")
+                for g in range(PASSES):
+                    toks = slice(g * P, (g + 1) * P)
+                    nc.tensor.matmul_mx(
+                        out=bank[:],
+                        lhsT=x_codes[:, tile_index, toks].bitcast(FP8X4),
+                        lhsT_scale=x_scales[:, tile_index, toks],
+                        rhs=w_codes[:, g, cols].bitcast(FP8X4),
+                        rhs_scale=w_scales[:, g, cols],
+                        start=(g == 0),
+                        stop=(g == PASSES - 1),
+                    )
+                banks.append(bank)
+            return banks
+
+        g_all = [keep.tile([P, T, E], F32, name="g_all%d" % b) for b in range(B)]
+        pair_sums = [[], []]
+
+        def keys(b, t, banks):
+            feat = g_all[b][:, t, :]
+            row_sum = small.tile([P, HALVES], F32, name="row_sum")
+            for h in range(HALVES):
+                cols = slice(h * BANK, (h + 1) * BANK)
+                nc.vector.scalar_tensor_tensor(
+                    out=feat[:, cols], in0=banks[h][:], scalar=1.0, in1=bias_all[:, 0, cols],
+                    op0=ALU.mult, op1=ALU.add, accum_out=row_sum[:, h : h + 1],
+                )
+            neg_mean = small.tile([P, 1], F32, name="neg_mean")
+            nc.vector.tensor_scalar(
+                out=neg_mean[:], in0=row_sum[:, 0:1], scalar1=row_sum[:, 1:2], scalar2=-1.0 / E,
+                op0=ALU.add, op1=ALU.mult,
+            )
+            f_sum = small.tile([P, 1], F32, name="f_sum")
+            nc.scalar.activation(out=feat, in_=feat, func=ACT.Square, bias=neg_mean[:], scale=1.0, accum_out=f_sum[:])
+            inv_sum = small.tile([P, 1], F32, name="inv_sum")
+            nc.scalar.activation(out=inv_sum[:], in_=f_sum[:], func=ACT.Abs_reciprocal_sqrt, bias=eps_sum[:], scale=1.0)
+            nc.scalar.square(out=inv_sum[:], in_=inv_sum[:])
+            g_sq = work.tile([P, E], F32, name="g_sq", bufs=5)
+            nc.scalar.activation(out=g_sq[:], in_=feat, func=ACT.Square, scale=inv_sum[:])
+            nc.gpsimd.tensor_scalar(out=feat, in0=feat, scalar1=inv_sum[:], scalar2=0.0, op0=ALU.mult, op1=ALU.add)
+            if t % 2 == 0:
+                pair_sums[b].append(g_sq)
+            else:
+                nc.gpsimd.tensor_tensor(out=pair_sums[b][-1][:], in0=pair_sums[b][-1][:], in1=g_sq[:], op=ALU.add)
+
+        def sum_over_tokens(b):
+            bank = psum.tile([P, BANK], F32, name="bank")
+            for j in range(CHUNKS):
+                for i, part in enumerate(pair_sums[b]):
+                    nc.tensor.matmul(
+                        out=bank[:, j : j + 1], lhsT=part[:, j * P : (j + 1) * P], rhs=ones_col[:],
+                        start=(i == 0), stop=(i == len(pair_sums[b]) - 1),
+                    )
+            return bank
+
+        def invert_norms(bank):
+            inv_norm = small.tile([P, CHUNKS], F32, name="inv_norm")
+            nc.vector.tensor_scalar_max(out=inv_norm[:], in0=bank[:, 0:CHUNKS], scalar1=EPS_NORM * EPS_NORM)
+            nc.scalar.activation(out=inv_norm[:], in_=inv_norm[:], func=ACT.Abs_reciprocal_sqrt)
+            return inv_norm
+
+        def spread_norms(inv_norm):
+            banks = []
+            for h in range(HALVES):
+                bank = psum.tile([P, BANK], F32, name="bank")
+                for i in range(BANK // P):
+                    j = h * (BANK // P) + i
+                    nc.tensor.matmul(
+                        out=bank[:, i * P : (i + 1) * P], lhsT=inv_norm[:, j : j + 1].to_broadcast([P, P]),
+                        rhs=ident[:], start=True, stop=True,
+                    )
+                banks.append(bank)
+            return banks
+
+        v_all = [keep.tile([P, T, E], F32, name="v_all%d" % b) for b in range(B)]
+
+        def values(b, t, banks):
+            for h in range(HALVES):
+                cols = slice(h * BANK, (h + 1) * BANK)
+                nc.vector.tensor_tensor(out=v_all[b][:, t, cols], in0=banks[h][:], in1=bias_all[:, 1, cols], op=ALU.add)
+            nc.sync.dma_start(out=out_1[b].rearrange("(p t) e -> p t e", t=T)[:, t, :], in_=v_all[b][:, t, :])
+
+        def regroup_values(b):
+            v_grp = stage.tile([P, E, PACK], BF16, align_bytes=64, name="v_grp", bufs=1)
+            nc.gpsimd.tensor_scalar(
+                out=v_grp[:, 0:BANK, :], in0=v_all[b][:, :, 0:BANK].rearrange("p t e -> p e t"),
+                scalar1=1.0, scalar2=0.0, op0=ALU.mult, op1=ALU.add,
+            )
+            nc.vector.tensor_copy(out=v_grp[:, BANK:E, :], in_=v_all[b][:, :, BANK:E].rearrange("p t e -> p e t"))
+            return v_grp
+
+        def quantise_values(v_grp):
+            v_codes = stage.tile([P, E], U32, align_bytes=64, name="v_codes")
+            v_scales = stage.tile([P, E], U8, align_bytes=64, name="v_scales")
+            for h in range(HALVES):
+                cols = slice(h * BANK, (h + 1) * BANK)
+                nc.vector.quantize_mx(
+                    out=v_codes[:, cols].bitcast(FP8X4), scales=v_scales[:, cols],
+                    in_=v_grp[:, cols, :].rearrange("p e t -> p (e t)"),
+                )
+            return v_codes, v_scales
+
+        def normalise_keys(b, j, norm_banks):
+            per_bank = BANK // P
+            norm = norm_banks[j // per_bank][:, (j % per_bank) * P : (j % per_bank + 1) * P]
+            k2_grp = work.tile([P, P, PACK], BF16, align_bytes=64, name="k2_grp")
+            nc.vector.tensor_tensor(
+                out=k2_grp[:], in0=g_all[b][:, :, j * P : (j + 1) * P].rearrange("p t e -> p e t"),
+                in1=norm.unsqueeze(2).to_broadcast([P, P, PACK]), op=ALU.mult,
+            )
+            return k2_grp
+
+        def key_value(b, j, k2_grp, v_codes, v_scales):
+            k2_codes = work.tile([P, P], U32, align_bytes=64, name="k2_codes")
+            k2_scales = work.tile([P, P], U8, align_bytes=64, name="k2_scales")
+            nc.vector.quantize_mx(
+                out=k2_codes[:].bitcast(FP8X4), scales=k2_scales[:], in_=k2_grp[:].rearrange("p e t -> p (e t)")
+            )
+            kv_rows = rows.tile([P, E], F32, name="kv_rows")
+            for h in range(HALVES):
+                cols = slice(h * BANK, (h + 1) * BANK)
+                bank = psum.tile([P, BANK], F32, name="bank")
+                nc.tensor.matmul_mx(
+                    out=bank[:], lhsT=k2_codes[:].bitcast(FP8X4), lhsT_scale=k2_scales[:],
+                    rhs=v_codes[:, cols].bitcast(FP8X4), rhs_scale=v_scales[:, cols], start=True, stop=True,
+                )
+                nc.scalar.copy(out=kv_rows[:, cols], in_=bank[:])
+            nc.sync.dma_start(out=out_0[b, j * P : (j + 1) * P, :], in_=kv_rows[:])
+
+        wk_codes, wk_scales = prepare_w(wk_raw, "wk")
+        prepare_x(0)
+        spread_biases()
+        wv_codes, wv_scales = prepare_w(wv_raw, "wv")
+        prepare_x(1)
+
+        k_banks = project(wk_codes, wk_scales, 0)
+        v_banks = project(wv_codes, wv_scales, 0)
+        for tile_index in range(B * T):
+            b, t = divmod(tile_index, T)
+            k_now, v_now = k_banks, v_banks
+            if tile_index + 1 < B * T:
+                k_banks = project(wk_codes, wk_scales, tile_index + 1)
+                v_banks = project(wv_codes, wv_scales, tile_index + 1)
+            keys(b, t, k_now)
+            values(b, t, v_now)
+            if tile_index == T - 1:
+                v_grp0 = regroup_values(0)
+            if tile_index == T + 1:
+                sums0 = sum_over_tokens(0)
+            if tile_index == T + 2:
+                inv_norm0 = invert_norms(sums0)
+        v_codes0, v_scales0 = quantise_values(v_grp0)
+        norm_banks0 = spread_norms(inv_norm0)
+        v_grp1 = regroup_values(1)
+
+        k2_next = normalise_keys(0, 0, norm_banks0)
+        for j in range(CHUNKS):
+            k2_now = k2_next
+            if j + 1 < CHUNKS:
+                k2_next = normalise_keys(0, j + 1, norm_banks0)
+            key_value(0, j, k2_now, v_codes0, v_scales0)
+            if j == 2:
+                sums1 = sum_over_tokens(1)
+            if j == 4:
+                inv_norm1 = invert_norms(sums1)
+            if j == 6:
+                v_codes1, v_scales1 = quantise_values(v_grp1)
+                norm_banks1 = spread_norms(inv_norm1)
+
+        k2_next = normalise_keys(1, 0, norm_banks1)
+        for j in range(CHUNKS):
+            k2_now = k2_next
+            if j + 1 < CHUNKS:
+                k2_next = normalise_keys(1, j + 1, norm_banks1)
+            key_value(1, j, k2_now, v_codes1, v_scales1)

@@ -19,6 +19,7 @@ PASSES = C // (P * PACK)
 BANK = 512
 HALVES = E // BANK
 CHUNKS = E // P
+VECTOR_COLS = 640
 EPS_SUM = 1e-7
 EPS_NORM = 1e-12
 
@@ -30,11 +31,9 @@ def tile_essattn_pa_kernel(tc, x, wk, bk, wv, bv, out_0, out_1):
     with ExitStack() as ctx:
         const = ctx.enter_context(tc.tile_pool(name="const", bufs=1))
         keep = ctx.enter_context(tc.tile_pool(name="keep", bufs=1))
-        raw = ctx.enter_context(tc.tile_pool(name="raw", bufs=3))
         stage = ctx.enter_context(tc.tile_pool(name="stage", bufs=2))
         work = ctx.enter_context(tc.tile_pool(name="work", bufs=3))
         small = ctx.enter_context(tc.tile_pool(name="small", bufs=4))
-        rows = ctx.enter_context(tc.tile_pool(name="rows", bufs=4))
         psum = ctx.enter_context(tc.psum_pool(name="psum", bufs=8))
         ctx.enter_context(tc.manual_schedule())
 
@@ -44,101 +43,109 @@ def tile_essattn_pa_kernel(tc, x, wk, bk, wv, bv, out_0, out_1):
         nc.vector.memset(ones_bf[:], 1.0)
         ones_col = const.tile([P, 1], F32)
         nc.vector.memset(ones_col[:], 1.0)
-        eps_sum = const.tile([P, 1], F32)
-        nc.vector.memset(eps_sum[:], EPS_SUM)
         warm = const.tile([P, 1], F32)
         nc.scalar.activation(out=warm[:], in_=ones_col[:], func=ACT.Abs_reciprocal_sqrt)
 
-        x_raw = [keep.tile([P, T, C], BF16, name="x_raw%d" % b) for b in range(B)]
+        with tc.tile_pool(name="loaded", bufs=1) as loaded, tc.tile_pool(name="raw", bufs=4) as raw, tc.tile_pool(
+            name="grouped", bufs=2
+        ) as grouped_pool:
+            x_raw = [loaded.tile([P, T, C], BF16, name="x_raw%d" % b) for b in range(B)]
 
-        def load_x(b):
-            tokens = x[b].rearrange("(p t) c -> p t c", t=T)
-            for half in range(2):
-                pair = slice(2 * half, 2 * half + 2)
-                nc.sync.dma_start(out=x_raw[b][:, pair, :], in_=tokens[:, pair, :])
+            def load_x(b):
+                tokens = x[b].rearrange("(p t) c -> p t c", t=T)
+                for half in range(2):
+                    pair = slice(2 * half, 2 * half + 2)
+                    nc.sync.dma_start(out=x_raw[b][:, pair, :], in_=tokens[:, pair, :])
 
-        def load_w(w):
-            tiles = []
-            for g in range(PASSES):
-                w_raw = raw.tile([P, PACK, E], BF16, name="w_raw")
-                for u in range(2):
-                    first = g * P * PACK + u * 2 * P
-                    nc.sync.dma_start(
-                        out=w_raw[:, 2 * u : 2 * u + 2, :],
-                        in_=w[first : first + 2 * P, :].rearrange("(q e) n -> q e n", e=2),
-                    )
-                tiles.append(w_raw)
-            return tiles
+            def load_w(w):
+                tiles = []
+                for g in range(PASSES):
+                    w_raw = raw.tile([P, PACK, E], BF16, name="w_raw")
+                    for u in range(2):
+                        first = g * P * PACK + u * 2 * P
+                        nc.sync.dma_start(
+                            out=w_raw[:, 2 * u : 2 * u + 2, :],
+                            in_=w[first : first + 2 * P, :].rearrange("(q e) n -> q e n", e=2),
+                        )
+                    tiles.append(w_raw)
+                return tiles
 
-        bias_rows = const.tile([P, 2, E], BF16)
-        nc.vector.memset(bias_rows[:], 0.0)
+            bias_rows = const.tile([P, 2, E], BF16)
+            nc.vector.memset(bias_rows[:], 0.0)
 
-        wk_raw = load_w(wk)
-        load_x(0)
-        nc.sync.dma_start(out=bias_rows[0:1, 0, :], in_=bk.unsqueeze(0))
-        nc.sync.dma_start(out=bias_rows[0:1, 1, :], in_=bv.unsqueeze(0))
-        wv_raw = load_w(wv)
-        load_x(1)
+            wk_raw = load_w(wk)
+            load_x(0)
+            nc.sync.dma_start(out=bias_rows[0:1, 0, :], in_=bk.unsqueeze(0))
+            nc.sync.dma_start(out=bias_rows[0:1, 1, :], in_=bv.unsqueeze(0))
+            wv_raw = load_w(wv)
+            load_x(1)
 
-        bias_all = const.tile([P, 2, E], F32)
+            bias_all = const.tile([P, 2, E], F32)
 
-        def spread_biases():
-            for i in range(2):
-                for h in range(HALVES):
-                    cols = slice(h * BANK, (h + 1) * BANK)
+            def spread_biases():
+                for i in range(2):
+                    for h in range(HALVES):
+                        cols = slice(h * BANK, (h + 1) * BANK)
+                        bank = psum.tile([P, BANK], F32, name="bank")
+                        nc.tensor.matmul(out=bank[:], lhsT=ones_bf[:], rhs=bias_rows[:, i, cols], start=True, stop=True)
+                        nc.scalar.copy(out=bias_all[:, i, cols], in_=bank[:])
+
+            x_codes = keep.tile([P, B * T, PASSES * P], U32, align_bytes=64)
+            x_scales = keep.tile([P, B * T, PASSES * P], U8, align_bytes=64)
+
+            def prepare_x(b):
+                words = x_raw[b][:].bitcast(F32)
+                banks = []
+                for t in range(T):
                     bank = psum.tile([P, BANK], F32, name="bank")
-                    nc.tensor.matmul(out=bank[:], lhsT=ones_bf[:], rhs=bias_rows[:, i, cols], start=True, stop=True)
-                    nc.scalar.copy(out=bias_all[:, i, cols], in_=bank[:])
+                    for q in range(PASSES * 2):
+                        nc.tensor.transpose(bank[:, q * P : (q + 1) * P], words[:, t, q * P : (q + 1) * P], ident[:])
+                    banks.append(bank)
+                grouped = []
+                for t in range(T + 1):
+                    if t < T:
+                        x_grp = grouped_pool.tile([P, PASSES * P * PACK], BF16, align_bytes=64, name="x_grp")
+                        nc.scalar.copy(
+                            out=x_grp[:].bitcast(F32).rearrange("p (g r u) -> p g r u", g=PASSES, u=2),
+                            in_=banks[t][:].rearrange("p (g u r) -> p g r u", g=PASSES, u=2),
+                        )
+                        grouped.append(x_grp)
+                    if t > 0:
+                        nc.vector.quantize_mx(
+                            out=x_codes[:, b * T + t - 1, :].bitcast(FP8X4),
+                            scales=x_scales[:, b * T + t - 1, :],
+                            in_=grouped[t - 1][:],
+                        )
 
-        x_codes = keep.tile([P, B * T, PASSES * P], U32, align_bytes=64)
-        x_scales = keep.tile([P, B * T, PASSES * P], U8, align_bytes=64)
+            def prepare_w(w_raw, name):
+                codes = keep.tile([P, PASSES, E], U32, align_bytes=64, name=name + "_codes")
+                scales = keep.tile([P, PASSES, E], U8, align_bytes=64, name=name + "_scales")
+                grouped = []
+                for g in range(PASSES):
+                    w_grp = grouped_pool.tile([P, E, PACK], BF16, align_bytes=64, name="w_grp")
+                    for copy, cols in ((nc.vector.tensor_copy, slice(0, VECTOR_COLS)), (nc.scalar.copy, slice(VECTOR_COLS, E))):
+                        copy(
+                            out=w_grp[:, cols, :].rearrange("p (c i) t -> p c t i", i=4),
+                            in_=w_raw[g][:, :, cols].rearrange("p t (c i) -> p c t i", i=4),
+                        )
+                    grouped.append(w_grp)
+                for g in range(PASSES):
+                    for h in range(HALVES):
+                        cols = slice(h * BANK, (h + 1) * BANK)
+                        nc.vector.quantize_mx(
+                            out=codes[:, g, cols].bitcast(FP8X4),
+                            scales=scales[:, g, cols],
+                            in_=grouped[g][:, cols, :].rearrange("p n t -> p (n t)"),
+                        )
+                return codes, scales
 
-        def prepare_x(b):
-            words = x_raw[b][:].bitcast(F32)
-            banks = []
-            for t in range(T):
-                bank = psum.tile([P, BANK], F32, name="bank")
-                for q in range(PASSES * 2):
-                    nc.tensor.transpose(bank[:, q * P : (q + 1) * P], words[:, t, q * P : (q + 1) * P], ident[:])
-                banks.append(bank)
-            grouped = []
-            for t in range(T + 1):
-                if t < T:
-                    x_grp = stage.tile([P, PASSES * P * PACK], BF16, align_bytes=64, name="x_grp")
-                    nc.scalar.copy(
-                        out=x_grp[:].bitcast(F32).rearrange("p (g r u) -> p g r u", g=PASSES, u=2),
-                        in_=banks[t][:].rearrange("p (g u r) -> p g r u", g=PASSES, u=2),
-                    )
-                    grouped.append(x_grp)
-                if t > 0:
-                    nc.vector.quantize_mx(
-                        out=x_codes[:, b * T + t - 1, :].bitcast(FP8X4),
-                        scales=x_scales[:, b * T + t - 1, :],
-                        in_=grouped[t - 1][:],
-                    )
+            wk_codes, wk_scales = prepare_w(wk_raw, "wk")
+            prepare_x(0)
+            spread_biases()
+            wv_codes, wv_scales = prepare_w(wv_raw, "wv")
+            prepare_x(1)
 
-        def prepare_w(w_raw, name):
-            codes = keep.tile([P, PASSES, E], U32, align_bytes=64, name=name + "_codes")
-            scales = keep.tile([P, PASSES, E], U8, align_bytes=64, name=name + "_scales")
-            grouped = []
-            for g in range(PASSES):
-                w_grp = stage.tile([P, E, PACK], BF16, align_bytes=64, name="w_grp")
-                for h, copy in enumerate((nc.vector.tensor_copy, nc.scalar.copy)):
-                    cols = slice(h * BANK, (h + 1) * BANK)
-                    copy(
-                        out=w_grp[:, cols, :].rearrange("p (c i) t -> p c t i", i=4),
-                        in_=w_raw[g][:, :, cols].rearrange("p t (c i) -> p c t i", i=4),
-                    )
-                grouped.append(w_grp)
-            for g in range(PASSES):
-                for h in range(HALVES):
-                    cols = slice(h * BANK, (h + 1) * BANK)
-                    nc.vector.quantize_mx(
-                        out=codes[:, g, cols].bitcast(FP8X4),
-                        scales=scales[:, g, cols],
-                        in_=grouped[g][:, cols, :].rearrange("p n t -> p (n t)"),
-                    )
-            return codes, scales
+        rows = ctx.enter_context(tc.tile_pool(name="rows", bufs=8))
 
         def project(w_codes, w_scales, tile_index):
             banks = []
@@ -160,71 +167,82 @@ def tile_essattn_pa_kernel(tc, x, wk, bk, wv, bv, out_0, out_1):
             return banks
 
         g_all = [keep.tile([P, T, E], F32, name="g_all%d" % b) for b in range(B)]
-        pair_sums = [[], []]
+        PAIRS = T // 2
+        sum_banks = [None, None]
 
-        def keys(b, t, banks):
-            feat = g_all[b][:, t, :]
+        def add_key_bias(b, t, banks):
             row_sum = small.tile([P, HALVES], F32, name="row_sum")
             for h in range(HALVES):
                 cols = slice(h * BANK, (h + 1) * BANK)
                 nc.vector.scalar_tensor_tensor(
-                    out=feat[:, cols], in0=banks[h][:], scalar=1.0, in1=bias_all[:, 0, cols],
+                    out=g_all[b][:, t, cols], in0=banks[h][:], scalar=1.0, in1=bias_all[:, 0, cols],
                     op0=ALU.mult, op1=ALU.add, accum_out=row_sum[:, h : h + 1],
                 )
+            return row_sum
+
+        def negative_mean(row_sum):
             neg_mean = small.tile([P, 1], F32, name="neg_mean")
             nc.vector.tensor_scalar(
                 out=neg_mean[:], in0=row_sum[:, 0:1], scalar1=row_sum[:, 1:2], scalar2=-1.0 / E,
                 op0=ALU.add, op1=ALU.mult,
             )
+            return neg_mean
+
+        def square_centred(b, t, neg_mean):
             f_sum = small.tile([P, 1], F32, name="f_sum")
-            nc.scalar.activation(out=feat, in_=feat, func=ACT.Square, bias=neg_mean[:], scale=1.0, accum_out=f_sum[:])
-            inv_sum = small.tile([P, 1], F32, name="inv_sum")
-            nc.scalar.activation(out=inv_sum[:], in_=f_sum[:], func=ACT.Abs_reciprocal_sqrt, bias=eps_sum[:], scale=1.0)
-            nc.scalar.square(out=inv_sum[:], in_=inv_sum[:])
+            nc.scalar.activation(
+                out=g_all[b][:, t, :], in_=g_all[b][:, t, :], func=ACT.Square, bias=neg_mean[:], scale=1.0,
+                accum_out=f_sum[:],
+            )
+            return f_sum
+
+        def scale_features(b, t, inv_sum, last_sq):
             g_sq = work.tile([P, E], F32, name="g_sq", bufs=5)
-            nc.scalar.activation(out=g_sq[:], in_=feat, func=ACT.Square, scale=inv_sum[:])
-            nc.gpsimd.tensor_scalar(out=feat, in0=feat, scalar1=inv_sum[:], scalar2=0.0, op0=ALU.mult, op1=ALU.add)
-            if t % 2 == 0:
-                pair_sums[b].append(g_sq)
-            else:
-                nc.gpsimd.tensor_tensor(out=pair_sums[b][-1][:], in0=pair_sums[b][-1][:], in1=g_sq[:], op=ALU.add)
+            nc.scalar.activation(out=g_sq[:], in_=g_all[b][:, t, :], func=ACT.Square, scale=inv_sum[:])
+            if t % 2 == 1:
+                nc.gpsimd.tensor_tensor(out=g_sq[:], in0=last_sq[:], in1=g_sq[:], op=ALU.add)
+            nc.gpsimd.tensor_scalar(
+                out=g_all[b][:, t, :], in0=g_all[b][:, t, :], scalar1=inv_sum[:], scalar2=0.0,
+                op0=ALU.mult, op1=ALU.add,
+            )
+            return g_sq
 
-        def sum_over_tokens(b):
-            bank = psum.tile([P, BANK], F32, name="bank")
+        def sum_over_partitions(b, i, pair_sq):
+            if i == 0:
+                sum_banks[b] = psum.tile([P, BANK], F32, name="bank")
             for j in range(CHUNKS):
-                for i, part in enumerate(pair_sums[b]):
-                    nc.tensor.matmul(
-                        out=bank[:, j : j + 1], lhsT=part[:, j * P : (j + 1) * P], rhs=ones_col[:],
-                        start=(i == 0), stop=(i == len(pair_sums[b]) - 1),
-                    )
-            return bank
+                col = PAIRS * j + i
+                nc.tensor.matmul(
+                    out=sum_banks[b][:, col : col + 1], lhsT=pair_sq[:, j * P : (j + 1) * P], rhs=ones_col[:],
+                    start=True, stop=True,
+                )
 
-        def invert_norms(bank):
+        def clamp_sums(b):
+            sums = small.tile([P, CHUNKS], F32, name="sums")
+            nc.vector.tensor_reduce(
+                out=sums[:], in_=sum_banks[b][:, 0 : PAIRS * CHUNKS].rearrange("p (j i) -> p j i", i=PAIRS),
+                axis=mybir.AxisListType.X, op=ALU.add,
+            )
             inv_norm = small.tile([P, CHUNKS], F32, name="inv_norm")
-            nc.vector.tensor_scalar_max(out=inv_norm[:], in0=bank[:, 0:CHUNKS], scalar1=EPS_NORM * EPS_NORM)
-            nc.scalar.activation(out=inv_norm[:], in_=inv_norm[:], func=ACT.Abs_reciprocal_sqrt)
+            nc.vector.tensor_scalar_max(out=inv_norm[:], in0=sums[:], scalar1=EPS_NORM * EPS_NORM)
             return inv_norm
 
         def spread_norms(inv_norm):
+            nc.scalar.activation(out=inv_norm[:], in_=inv_norm[:], func=ACT.Abs_reciprocal_sqrt)
             banks = []
             for h in range(HALVES):
                 bank = psum.tile([P, BANK], F32, name="bank")
                 for i in range(BANK // P):
                     j = h * (BANK // P) + i
-                    nc.tensor.matmul(
-                        out=bank[:, i * P : (i + 1) * P], lhsT=inv_norm[:, j : j + 1].to_broadcast([P, P]),
-                        rhs=ident[:], start=True, stop=True,
-                    )
+                    nc.tensor.transpose(bank[:, i * P : (i + 1) * P], inv_norm[:, j : j + 1].to_broadcast([P, P]), ident[:])
                 banks.append(bank)
             return banks
 
         v_all = [keep.tile([P, T, E], F32, name="v_all%d" % b) for b in range(B)]
 
-        def values(b, t, banks):
-            for h in range(HALVES):
-                cols = slice(h * BANK, (h + 1) * BANK)
-                nc.vector.tensor_tensor(out=v_all[b][:, t, cols], in0=banks[h][:], in1=bias_all[:, 1, cols], op=ALU.add)
-            nc.sync.dma_start(out=out_1[b].rearrange("(p t) e -> p t e", t=T)[:, t, :], in_=v_all[b][:, t, :])
+        def add_value_bias(b, t, h, banks):
+            cols = slice(h * BANK, (h + 1) * BANK)
+            nc.vector.tensor_tensor(out=v_all[b][:, t, cols], in0=banks[h][:], in1=bias_all[:, 1, cols], op=ALU.add)
 
         def regroup_values(b):
             v_grp = stage.tile([P, E, PACK], BF16, align_bytes=64, name="v_grp", bufs=1)
@@ -238,7 +256,7 @@ def tile_essattn_pa_kernel(tc, x, wk, bk, wv, bv, out_0, out_1):
         def quantise_values(v_grp):
             v_codes = stage.tile([P, E], U32, align_bytes=64, name="v_codes")
             v_scales = stage.tile([P, E], U8, align_bytes=64, name="v_scales")
-            for h in range(HALVES):
+            for h in (1, 0):
                 cols = slice(h * BANK, (h + 1) * BANK)
                 nc.vector.quantize_mx(
                     out=v_codes[:, cols].bitcast(FP8X4), scales=v_scales[:, cols],
@@ -273,31 +291,44 @@ def tile_essattn_pa_kernel(tc, x, wk, bk, wv, bv, out_0, out_1):
                 nc.scalar.copy(out=kv_rows[:, cols], in_=bank[:])
             nc.sync.dma_start(out=out_0[b, j * P : (j + 1) * P, :], in_=kv_rows[:])
 
-        wk_codes, wk_scales = prepare_w(wk_raw, "wk")
-        prepare_x(0)
-        spread_biases()
-        wv_codes, wv_scales = prepare_w(wv_raw, "wv")
-        prepare_x(1)
-
+        tiles = [divmod(i, T) for i in range(B * T)]
+        pair_sq = []
+        SUM_LAG = 3
         k_banks = project(wk_codes, wk_scales, 0)
-        v_banks = project(wv_codes, wv_scales, 0)
-        for tile_index in range(B * T):
-            b, t = divmod(tile_index, T)
-            k_now, v_now = k_banks, v_banks
-            if tile_index + 1 < B * T:
-                k_banks = project(wk_codes, wk_scales, tile_index + 1)
-                v_banks = project(wv_codes, wv_scales, tile_index + 1)
-            keys(b, t, k_now)
-            values(b, t, v_now)
-            if tile_index == T - 1:
+        v_next = project(wv_codes, wv_scales, 0)
+        row_sum = add_key_bias(0, 0, k_banks)
+        neg_mean = negative_mean(row_sum)
+        f_next = square_centred(0, 0, neg_mean)
+        g_sq = None
+        for r, (b, t) in enumerate(tiles):
+            v_banks, f_sum = v_next, f_next
+            more = r + 1 < len(tiles)
+            if more:
+                nb, nt = tiles[r + 1]
+                k_banks = project(wk_codes, wk_scales, r + 1)
+                v_next = project(wv_codes, wv_scales, r + 1)
+                row_sum = add_key_bias(nb, nt, k_banks)
+            if r >= SUM_LAG and tiles[r - SUM_LAG][1] % 2 == 1:
+                sum_over_partitions(*pair_sq[(r - SUM_LAG) // 2])
+            add_value_bias(b, t, 0, v_banks)
+            if more:
+                neg_mean = negative_mean(row_sum)
+            inv_sum = small.tile([P, 1], F32, name="inv_sum")
+            nc.vector.tensor_scalar_add(out=inv_sum[:], in0=f_sum[:], scalar1=EPS_SUM)
+            add_value_bias(b, t, 1, v_banks)
+            nc.sync.dma_start(out=out_1[b].rearrange("(p t) e -> p t e", t=T)[:, t, :], in_=v_all[b][:, t, :])
+            nc.vector.reciprocal(out=inv_sum[:], in_=inv_sum[:])
+            if more:
+                f_next = square_centred(nb, nt, neg_mean)
+            else:
+                norm_banks0 = spread_norms(clamp_sums(0))
+            g_sq = scale_features(b, t, inv_sum, g_sq)
+            if t % 2 == 1:
+                pair_sq.append((b, t // 2, g_sq))
+            if (b, t) == (0, T - 1):
                 v_grp0 = regroup_values(0)
-            if tile_index == T + 1:
-                sums0 = sum_over_tokens(0)
-            if tile_index == T + 2:
-                inv_norm0 = invert_norms(sums0)
-        v_codes0, v_scales0 = quantise_values(v_grp0)
-        norm_banks0 = spread_norms(inv_norm0)
-        v_grp1 = regroup_values(1)
+            if (b, t) == (1, T - 2):
+                v_codes0, v_scales0 = quantise_values(v_grp0)
 
         k2_next = normalise_keys(0, 0, norm_banks0)
         for j in range(CHUNKS):
@@ -305,13 +336,16 @@ def tile_essattn_pa_kernel(tc, x, wk, bk, wv, bv, out_0, out_1):
             if j + 1 < CHUNKS:
                 k2_next = normalise_keys(0, j + 1, norm_banks0)
             key_value(0, j, k2_now, v_codes0, v_scales0)
+            if j == 0:
+                sum_over_partitions(*pair_sq[2])
+            if j == 1:
+                sum_over_partitions(*pair_sq[3])
             if j == 2:
-                sums1 = sum_over_tokens(1)
-            if j == 4:
-                inv_norm1 = invert_norms(sums1)
+                norm_banks1 = spread_norms(clamp_sums(1))
+            if j == 3:
+                v_grp1 = regroup_values(1)
             if j == 6:
                 v_codes1, v_scales1 = quantise_values(v_grp1)
-                norm_banks1 = spread_norms(inv_norm1)
 
         k2_next = normalise_keys(1, 0, norm_banks1)
         for j in range(CHUNKS):

@@ -180,21 +180,19 @@ def tile_essattn_pa_kernel(tc, x, wk, bk, wv, bv, out_0, out_1):
                 )
             return row_sum
 
-        def negative_mean(row_sum):
-            neg_mean = small.tile([P, 1], F32, name="neg_mean")
-            nc.vector.tensor_scalar(
-                out=neg_mean[:], in0=row_sum[:, 0:1], scalar1=row_sum[:, 1:2], scalar2=-1.0 / E,
-                op0=ALU.add, op1=ALU.mult,
-            )
-            return neg_mean
+        def row_total(row_sum):
+            total = small.tile([P, 1], F32, name="total")
+            nc.vector.tensor_reduce(out=total[:], in_=row_sum[:], axis=mybir.AxisListType.X, op=ALU.add)
+            return total
 
-        def square_centred(b, t, neg_mean):
-            f_sum = small.tile([P, 1], F32, name="f_sum")
+        f_sums = const.tile([P, B * T, 2], F32)
+        nc.vector.memset(f_sums[:], E * E * EPS_SUM)
+
+        def square_centred(b, t, total):
             nc.scalar.activation(
-                out=g_all[b][:, t, :], in_=g_all[b][:, t, :], func=ACT.Square, bias=neg_mean[:], scale=1.0,
-                accum_out=f_sum[:],
+                out=g_all[b][:, t, :], in_=g_all[b][:, t, :], func=ACT.Square, bias=total[:], scale=-float(E),
+                accum_out=f_sums[:, b * T + t, 0:1],
             )
-            return f_sum
 
         def scale_features(b, t, inv_sum, last_sq):
             g_sq = work.tile([P, E], F32, name="g_sq", bufs=5)
@@ -217,7 +215,7 @@ def tile_essattn_pa_kernel(tc, x, wk, bk, wv, bv, out_0, out_1):
                     start=True, stop=True,
                 )
 
-        def clamp_sums(b):
+        def invert_norms(b):
             sums = small.tile([P, CHUNKS], F32, name="sums")
             nc.vector.tensor_reduce(
                 out=sums[:], in_=sum_banks[b][:, 0 : PAIRS * CHUNKS].rearrange("p (j i) -> p j i", i=PAIRS),
@@ -225,10 +223,10 @@ def tile_essattn_pa_kernel(tc, x, wk, bk, wv, bv, out_0, out_1):
             )
             inv_norm = small.tile([P, CHUNKS], F32, name="inv_norm")
             nc.vector.tensor_scalar_max(out=inv_norm[:], in0=sums[:], scalar1=EPS_NORM * EPS_NORM)
+            nc.scalar.activation(out=inv_norm[:], in_=inv_norm[:], func=ACT.Abs_reciprocal_sqrt)
             return inv_norm
 
         def spread_norms(inv_norm):
-            nc.scalar.activation(out=inv_norm[:], in_=inv_norm[:], func=ACT.Abs_reciprocal_sqrt)
             banks = []
             for h in range(HALVES):
                 bank = psum.tile([P, BANK], F32, name="bank")
@@ -246,17 +244,17 @@ def tile_essattn_pa_kernel(tc, x, wk, bk, wv, bv, out_0, out_1):
 
         def regroup_values(b):
             v_grp = stage.tile([P, E, PACK], BF16, align_bytes=64, name="v_grp", bufs=1)
+            nc.vector.tensor_copy(out=v_grp[:, 0:BANK, :], in_=v_all[b][:, :, 0:BANK].rearrange("p t e -> p e t"))
             nc.gpsimd.tensor_scalar(
-                out=v_grp[:, 0:BANK, :], in0=v_all[b][:, :, 0:BANK].rearrange("p t e -> p e t"),
+                out=v_grp[:, BANK:E, :], in0=v_all[b][:, :, BANK:E].rearrange("p t e -> p e t"),
                 scalar1=1.0, scalar2=0.0, op0=ALU.mult, op1=ALU.add,
             )
-            nc.vector.tensor_copy(out=v_grp[:, BANK:E, :], in_=v_all[b][:, :, BANK:E].rearrange("p t e -> p e t"))
             return v_grp
 
         def quantise_values(v_grp):
             v_codes = stage.tile([P, E], U32, align_bytes=64, name="v_codes")
             v_scales = stage.tile([P, E], U8, align_bytes=64, name="v_scales")
-            for h in (1, 0):
+            for h in range(HALVES):
                 cols = slice(h * BANK, (h + 1) * BANK)
                 nc.vector.quantize_mx(
                     out=v_codes[:, cols].bitcast(FP8X4), scales=v_scales[:, cols],
@@ -297,11 +295,10 @@ def tile_essattn_pa_kernel(tc, x, wk, bk, wv, bv, out_0, out_1):
         k_banks = project(wk_codes, wk_scales, 0)
         v_next = project(wv_codes, wv_scales, 0)
         row_sum = add_key_bias(0, 0, k_banks)
-        neg_mean = negative_mean(row_sum)
-        f_next = square_centred(0, 0, neg_mean)
+        square_centred(0, 0, row_total(row_sum))
         g_sq = None
         for r, (b, t) in enumerate(tiles):
-            v_banks, f_sum = v_next, f_next
+            v_banks = v_next
             more = r + 1 < len(tiles)
             if more:
                 nb, nt = tiles[r + 1]
@@ -312,16 +309,16 @@ def tile_essattn_pa_kernel(tc, x, wk, bk, wv, bv, out_0, out_1):
                 sum_over_partitions(*pair_sq[(r - SUM_LAG) // 2])
             add_value_bias(b, t, 0, v_banks)
             if more:
-                neg_mean = negative_mean(row_sum)
+                total = row_total(row_sum)
             inv_sum = small.tile([P, 1], F32, name="inv_sum")
-            nc.vector.tensor_scalar_add(out=inv_sum[:], in0=f_sum[:], scalar1=EPS_SUM)
+            nc.vector.tensor_reduce(out=inv_sum[:], in_=f_sums[:, r, :], axis=mybir.AxisListType.X, op=ALU.add)
             add_value_bias(b, t, 1, v_banks)
             nc.sync.dma_start(out=out_1[b].rearrange("(p t) e -> p t e", t=T)[:, t, :], in_=v_all[b][:, t, :])
             nc.vector.reciprocal(out=inv_sum[:], in_=inv_sum[:])
             if more:
-                f_next = square_centred(nb, nt, neg_mean)
+                square_centred(nb, nt, total)
             else:
-                norm_banks0 = spread_norms(clamp_sums(0))
+                norm_banks0 = spread_norms(invert_norms(0))
             g_sq = scale_features(b, t, inv_sum, g_sq)
             if t % 2 == 1:
                 pair_sq.append((b, t // 2, g_sq))
@@ -338,12 +335,12 @@ def tile_essattn_pa_kernel(tc, x, wk, bk, wv, bv, out_0, out_1):
             key_value(0, j, k2_now, v_codes0, v_scales0)
             if j == 0:
                 sum_over_partitions(*pair_sq[2])
-            if j == 1:
-                sum_over_partitions(*pair_sq[3])
-            if j == 2:
-                norm_banks1 = spread_norms(clamp_sums(1))
-            if j == 3:
                 v_grp1 = regroup_values(1)
+            if j == 3:
+                sum_over_partitions(*pair_sq[3])
+                inv_norm1 = invert_norms(1)
+            if j == 5:
+                norm_banks1 = spread_norms(inv_norm1)
             if j == 6:
                 v_codes1, v_scales1 = quantise_values(v_grp1)
 

@@ -41,10 +41,10 @@ def tile_essattn_pa_kernel(tc, x, wk, bk, wv, bv, out_0, out_1):
         make_identity(nc, ident[:])
         ones_bf = const.tile([P, P], BF16)
         nc.vector.memset(ones_bf[:], 1.0)
-        ones_col = const.tile([P, 1], F32)
-        nc.vector.memset(ones_col[:], 1.0)
+        ones_f32 = const.tile([P, P], F32)
+        nc.vector.memset(ones_f32[:], 1.0)
         warm = const.tile([P, 1], F32)
-        nc.scalar.activation(out=warm[:], in_=ones_col[:], func=ACT.Abs_reciprocal_sqrt)
+        nc.scalar.activation(out=warm[:], in_=ones_f32[:, 0:1], func=ACT.Abs_reciprocal_sqrt)
 
         with tc.tile_pool(name="loaded", bufs=1) as loaded, tc.tile_pool(name="raw", bufs=4) as raw, tc.tile_pool(
             name="grouped", bufs=2
@@ -205,36 +205,22 @@ def tile_essattn_pa_kernel(tc, x, wk, bk, wv, bv, out_0, out_1):
             )
             return g_sq
 
-        def sum_over_partitions(b, i, pair_sq):
+        def sum_over_tokens(b, i, pair_sq):
             if i == 0:
-                sum_banks[b] = psum.tile([P, BANK], F32, name="bank")
-            for j in range(CHUNKS):
-                col = PAIRS * j + i
+                sum_banks[b] = [psum.tile([P, BANK], F32, name="bank") for h in range(HALVES)]
+            for h in range(HALVES):
                 nc.tensor.matmul(
-                    out=sum_banks[b][:, col : col + 1], lhsT=pair_sq[:, j * P : (j + 1) * P], rhs=ones_col[:],
-                    start=True, stop=True,
+                    out=sum_banks[b][h][:], lhsT=ones_f32[:], rhs=pair_sq[:, h * BANK : (h + 1) * BANK],
+                    start=(i == 0), stop=(i == PAIRS - 1),
                 )
 
         def invert_norms(b):
-            sums = small.tile([P, CHUNKS], F32, name="sums")
-            nc.vector.tensor_reduce(
-                out=sums[:], in_=sum_banks[b][:, 0 : PAIRS * CHUNKS].rearrange("p (j i) -> p j i", i=PAIRS),
-                axis=mybir.AxisListType.X, op=ALU.add,
-            )
-            inv_norm = small.tile([P, CHUNKS], F32, name="inv_norm")
-            nc.vector.tensor_scalar_max(out=inv_norm[:], in0=sums[:], scalar1=EPS_NORM * EPS_NORM)
-            nc.scalar.activation(out=inv_norm[:], in_=inv_norm[:], func=ACT.Abs_reciprocal_sqrt)
-            return inv_norm
-
-        def spread_norms(inv_norm):
-            banks = []
+            inv_norm = stage.tile([P, E], F32, name="inv_norm")
             for h in range(HALVES):
-                bank = psum.tile([P, BANK], F32, name="bank")
-                for i in range(BANK // P):
-                    j = h * (BANK // P) + i
-                    nc.tensor.transpose(bank[:, i * P : (i + 1) * P], inv_norm[:, j : j + 1].to_broadcast([P, P]), ident[:])
-                banks.append(bank)
-            return banks
+                nc.scalar.activation(
+                    out=inv_norm[:, h * BANK : (h + 1) * BANK], in_=sum_banks[b][h][:], func=ACT.Abs_reciprocal_sqrt
+                )
+            return inv_norm
 
         v_all = [keep.tile([P, T, E], F32, name="v_all%d" % b) for b in range(B)]
 
@@ -262,13 +248,12 @@ def tile_essattn_pa_kernel(tc, x, wk, bk, wv, bv, out_0, out_1):
                 )
             return v_codes, v_scales
 
-        def normalise_keys(b, j, norm_banks):
-            per_bank = BANK // P
-            norm = norm_banks[j // per_bank][:, (j % per_bank) * P : (j % per_bank + 1) * P]
+        def normalise_keys(b, j, inv_norm):
+            cols = slice(j * P, (j + 1) * P)
             k2_grp = work.tile([P, P, PACK], BF16, align_bytes=64, name="k2_grp")
-            nc.vector.tensor_tensor(
-                out=k2_grp[:], in0=g_all[b][:, :, j * P : (j + 1) * P].rearrange("p t e -> p e t"),
-                in1=norm.unsqueeze(2).to_broadcast([P, P, PACK]), op=ALU.mult,
+            nc.vector.scalar_tensor_tensor(
+                out=k2_grp[:], in0=inv_norm[:, cols].unsqueeze(2).to_broadcast([P, P, PACK]), scalar=1.0 / EPS_NORM,
+                in1=g_all[b][:, :, cols].rearrange("p t e -> p e t"), op0=ALU.min, op1=ALU.mult,
             )
             return k2_grp
 
@@ -306,7 +291,7 @@ def tile_essattn_pa_kernel(tc, x, wk, bk, wv, bv, out_0, out_1):
                 v_next = project(wv_codes, wv_scales, r + 1)
                 row_sum = add_key_bias(nb, nt, k_banks)
             if r >= SUM_LAG and tiles[r - SUM_LAG][1] % 2 == 1:
-                sum_over_partitions(*pair_sq[(r - SUM_LAG) // 2])
+                sum_over_tokens(*pair_sq[(r - SUM_LAG) // 2])
             add_value_bias(b, t, 0, v_banks)
             if more:
                 total = row_total(row_sum)
@@ -318,7 +303,7 @@ def tile_essattn_pa_kernel(tc, x, wk, bk, wv, bv, out_0, out_1):
             if more:
                 square_centred(nb, nt, total)
             else:
-                norm_banks0 = spread_norms(invert_norms(0))
+                inv_norm0 = invert_norms(0)
             g_sq = scale_features(b, t, inv_sum, g_sq)
             if t % 2 == 1:
                 pair_sq.append((b, t // 2, g_sq))
@@ -327,26 +312,25 @@ def tile_essattn_pa_kernel(tc, x, wk, bk, wv, bv, out_0, out_1):
             if (b, t) == (1, T - 2):
                 v_codes0, v_scales0 = quantise_values(v_grp0)
 
-        k2_next = normalise_keys(0, 0, norm_banks0)
+        k2_next = normalise_keys(0, 0, inv_norm0)
         for j in range(CHUNKS):
             k2_now = k2_next
             if j + 1 < CHUNKS:
-                k2_next = normalise_keys(0, j + 1, norm_banks0)
+                k2_next = normalise_keys(0, j + 1, inv_norm0)
             key_value(0, j, k2_now, v_codes0, v_scales0)
             if j == 0:
-                sum_over_partitions(*pair_sq[2])
+                sum_over_tokens(*pair_sq[2])
                 v_grp1 = regroup_values(1)
             if j == 3:
-                sum_over_partitions(*pair_sq[3])
+                sum_over_tokens(*pair_sq[3])
+            if j == 4:
                 inv_norm1 = invert_norms(1)
-            if j == 5:
-                norm_banks1 = spread_norms(inv_norm1)
             if j == 6:
                 v_codes1, v_scales1 = quantise_values(v_grp1)
 
-        k2_next = normalise_keys(1, 0, norm_banks1)
+        k2_next = normalise_keys(1, 0, inv_norm1)
         for j in range(CHUNKS):
             k2_now = k2_next
             if j + 1 < CHUNKS:
-                k2_next = normalise_keys(1, j + 1, norm_banks1)
+                k2_next = normalise_keys(1, j + 1, inv_norm1)
             key_value(1, j, k2_now, v_codes1, v_scales1)

@@ -19,7 +19,10 @@ PASSES = C // (P * PACK)
 BANK = 512
 HALVES = E // BANK
 CHUNKS = E // P
-VECTOR_COLS = 640
+VECTOR_COLS = (512, 256)
+FEATS = 6
+SQS = 5
+ROWS = 6
 EPS_SUM = 1e-7
 EPS_NORM = 1e-12
 
@@ -34,7 +37,7 @@ def tile_essattn_pa_kernel(tc, x, wk, bk, wv, bv, out_0, out_1):
         stage = ctx.enter_context(tc.tile_pool(name="stage", bufs=2))
         work = ctx.enter_context(tc.tile_pool(name="work", bufs=3))
         small = ctx.enter_context(tc.tile_pool(name="small", bufs=4))
-        psum = ctx.enter_context(tc.psum_pool(name="psum", bufs=8))
+        psum = ctx.enter_context(tc.psum_pool(name="psum", bufs=6))
         ctx.enter_context(tc.manual_schedule())
 
         ident = const.tile([P, P], F32)
@@ -45,109 +48,20 @@ def tile_essattn_pa_kernel(tc, x, wk, bk, wv, bv, out_0, out_1):
         nc.vector.memset(ones_f32[:], 1.0)
         warm = const.tile([P, 1], F32)
         nc.scalar.activation(out=warm[:], in_=ones_f32[:, 0:1], func=ACT.Abs_reciprocal_sqrt)
+        bias_rows = const.tile([P, 2, E], BF16)
+        nc.gpsimd.memset(bias_rows[:], 0.0)
+        f_sums = const.tile([P, B * T, 2], F32)
+        nc.vector.memset(f_sums[:], E * E * EPS_SUM)
+        bias_all = const.tile([P, 2, E], BF16)
 
-        with tc.tile_pool(name="loaded", bufs=1) as loaded, tc.tile_pool(name="raw", bufs=4) as raw, tc.tile_pool(
-            name="grouped", bufs=2
-        ) as grouped_pool:
-            x_raw = [loaded.tile([P, T, C], BF16, name="x_raw%d" % b) for b in range(B)]
+        x_codes = keep.tile([P, B * T, PASSES * P], U32, align_bytes=64)
+        x_scales = keep.tile([P, B * T, PASSES * P], U8, align_bytes=64)
+        w_codes = [keep.tile([P, PASSES, E], U32, align_bytes=64, name="w_codes%d" % i) for i in range(2)]
+        w_scales = [keep.tile([P, PASSES, E], U8, align_bytes=64, name="w_scales%d" % i) for i in range(2)]
+        g_all = [keep.tile([P, T, E], F32, name="g_all%d" % b) for b in range(B)]
+        v_all = [keep.tile([P, T, E], F32, name="v_all%d" % b) for b in range(B)]
 
-            def load_x(b):
-                tokens = x[b].rearrange("(p t) c -> p t c", t=T)
-                for half in range(2):
-                    pair = slice(2 * half, 2 * half + 2)
-                    nc.sync.dma_start(out=x_raw[b][:, pair, :], in_=tokens[:, pair, :])
-
-            def load_w(w):
-                tiles = []
-                for g in range(PASSES):
-                    w_raw = raw.tile([P, PACK, E], BF16, name="w_raw")
-                    for u in range(2):
-                        first = g * P * PACK + u * 2 * P
-                        nc.sync.dma_start(
-                            out=w_raw[:, 2 * u : 2 * u + 2, :],
-                            in_=w[first : first + 2 * P, :].rearrange("(q e) n -> q e n", e=2),
-                        )
-                    tiles.append(w_raw)
-                return tiles
-
-            bias_rows = const.tile([P, 2, E], BF16)
-            nc.vector.memset(bias_rows[:], 0.0)
-
-            wk_raw = load_w(wk)
-            load_x(0)
-            nc.sync.dma_start(out=bias_rows[0:1, 0, :], in_=bk.unsqueeze(0))
-            nc.sync.dma_start(out=bias_rows[0:1, 1, :], in_=bv.unsqueeze(0))
-            wv_raw = load_w(wv)
-            load_x(1)
-
-            bias_all = const.tile([P, 2, E], F32)
-
-            def spread_biases():
-                for i in range(2):
-                    for h in range(HALVES):
-                        cols = slice(h * BANK, (h + 1) * BANK)
-                        bank = psum.tile([P, BANK], F32, name="bank")
-                        nc.tensor.matmul(out=bank[:], lhsT=ones_bf[:], rhs=bias_rows[:, i, cols], start=True, stop=True)
-                        nc.scalar.copy(out=bias_all[:, i, cols], in_=bank[:])
-
-            x_codes = keep.tile([P, B * T, PASSES * P], U32, align_bytes=64)
-            x_scales = keep.tile([P, B * T, PASSES * P], U8, align_bytes=64)
-
-            def prepare_x(b):
-                words = x_raw[b][:].bitcast(F32)
-                banks = []
-                for t in range(T):
-                    bank = psum.tile([P, BANK], F32, name="bank")
-                    for q in range(PASSES * 2):
-                        nc.tensor.transpose(bank[:, q * P : (q + 1) * P], words[:, t, q * P : (q + 1) * P], ident[:])
-                    banks.append(bank)
-                grouped = []
-                for t in range(T + 1):
-                    if t < T:
-                        x_grp = grouped_pool.tile([P, PASSES * P * PACK], BF16, align_bytes=64, name="x_grp")
-                        nc.scalar.copy(
-                            out=x_grp[:].bitcast(F32).rearrange("p (g r u) -> p g r u", g=PASSES, u=2),
-                            in_=banks[t][:].rearrange("p (g u r) -> p g r u", g=PASSES, u=2),
-                        )
-                        grouped.append(x_grp)
-                    if t > 0:
-                        nc.vector.quantize_mx(
-                            out=x_codes[:, b * T + t - 1, :].bitcast(FP8X4),
-                            scales=x_scales[:, b * T + t - 1, :],
-                            in_=grouped[t - 1][:],
-                        )
-
-            def prepare_w(w_raw, name):
-                codes = keep.tile([P, PASSES, E], U32, align_bytes=64, name=name + "_codes")
-                scales = keep.tile([P, PASSES, E], U8, align_bytes=64, name=name + "_scales")
-                grouped = []
-                for g in range(PASSES):
-                    w_grp = grouped_pool.tile([P, E, PACK], BF16, align_bytes=64, name="w_grp")
-                    for copy, cols in ((nc.vector.tensor_copy, slice(0, VECTOR_COLS)), (nc.scalar.copy, slice(VECTOR_COLS, E))):
-                        copy(
-                            out=w_grp[:, cols, :].rearrange("p (c i) t -> p c t i", i=4),
-                            in_=w_raw[g][:, :, cols].rearrange("p t (c i) -> p c t i", i=4),
-                        )
-                    grouped.append(w_grp)
-                for g in range(PASSES):
-                    for h in range(HALVES):
-                        cols = slice(h * BANK, (h + 1) * BANK)
-                        nc.vector.quantize_mx(
-                            out=codes[:, g, cols].bitcast(FP8X4),
-                            scales=scales[:, g, cols],
-                            in_=grouped[g][:, cols, :].rearrange("p n t -> p (n t)"),
-                        )
-                return codes, scales
-
-            wk_codes, wk_scales = prepare_w(wk_raw, "wk")
-            prepare_x(0)
-            spread_biases()
-            wv_codes, wv_scales = prepare_w(wv_raw, "wv")
-            prepare_x(1)
-
-        rows = ctx.enter_context(tc.tile_pool(name="rows", bufs=8))
-
-        def project(w_codes, w_scales, tile_index):
+        def project(weight, tile_index):
             banks = []
             for h in range(HALVES):
                 cols = slice(h * BANK, (h + 1) * BANK)
@@ -158,179 +72,538 @@ def tile_essattn_pa_kernel(tc, x, wk, bk, wv, bv, out_0, out_1):
                         out=bank[:],
                         lhsT=x_codes[:, tile_index, toks].bitcast(FP8X4),
                         lhsT_scale=x_scales[:, tile_index, toks],
-                        rhs=w_codes[:, g, cols].bitcast(FP8X4),
-                        rhs_scale=w_scales[:, g, cols],
+                        rhs=w_codes[weight][:, g, cols].bitcast(FP8X4),
+                        rhs_scale=w_scales[weight][:, g, cols],
                         start=(g == 0),
                         stop=(g == PASSES - 1),
                     )
                 banks.append(bank)
             return banks
 
-        g_all = [keep.tile([P, T, E], F32, name="g_all%d" % b) for b in range(B)]
-        PAIRS = T // 2
-        sum_banks = [None, None]
+        feats = {}
+        row_sums = {}
+        totals = {}
+        inv_sums = {}
+        squares = {}
+        sum_banks = {}
+        inv_norms = {}
+        k_banks = {}
+        v_banks = {}
 
-        def add_key_bias(b, t, banks):
+        def KP(b, t):
+            k_banks[b, t] = project(0, b * T + t)
+
+        def KE(b, t):
             row_sum = small.tile([P, HALVES], F32, name="row_sum")
+            feat = work.tile([P, E], F32, name="feat", bufs=FEATS)
             for h in range(HALVES):
                 cols = slice(h * BANK, (h + 1) * BANK)
                 nc.vector.scalar_tensor_tensor(
-                    out=g_all[b][:, t, cols], in0=banks[h][:], scalar=1.0, in1=bias_all[:, 0, cols],
+                    out=feat[:, cols], in0=k_banks[b, t][h][:], scalar=1.0, in1=bias_all[:, 0, cols],
                     op0=ALU.mult, op1=ALU.add, accum_out=row_sum[:, h : h + 1],
                 )
-            return row_sum
+            feats[b, t] = feat
+            row_sums[b, t] = row_sum
 
-        def row_total(row_sum):
+        def KT(b, t):
             total = small.tile([P, 1], F32, name="total")
-            nc.vector.tensor_reduce(out=total[:], in_=row_sum[:], axis=mybir.AxisListType.X, op=ALU.add)
-            return total
+            nc.vector.tensor_reduce(out=total[:], in_=row_sums[b, t][:], axis=mybir.AxisListType.X, op=ALU.add)
+            totals[b, t] = total
 
-        f_sums = const.tile([P, B * T, 2], F32)
-        nc.vector.memset(f_sums[:], E * E * EPS_SUM)
-
-        def square_centred(b, t, total):
+        def KG(b, t):
             nc.scalar.activation(
-                out=g_all[b][:, t, :], in_=g_all[b][:, t, :], func=ACT.Square, bias=total[:], scale=-float(E),
+                out=feats[b, t][:], in_=feats[b, t][:], func=ACT.Square, bias=totals[b, t][:], scale=-float(E),
                 accum_out=f_sums[:, b * T + t, 0:1],
             )
 
-        def scale_features(b, t, inv_sum, last_sq):
-            g_sq = work.tile([P, E], F32, name="g_sq", bufs=5)
-            nc.scalar.activation(out=g_sq[:], in_=g_all[b][:, t, :], func=ACT.Square, scale=inv_sum[:])
-            if t % 2 == 1:
-                nc.gpsimd.tensor_tensor(out=g_sq[:], in0=last_sq[:], in1=g_sq[:], op=ALU.add)
-            nc.gpsimd.tensor_scalar(
-                out=g_all[b][:, t, :], in0=g_all[b][:, t, :], scalar1=inv_sum[:], scalar2=0.0,
+        def KI(b, t):
+            inv = small.tile([P, 1], F32, name="inv_sum", bufs=8)
+            nc.vector.tensor_reduce(out=inv[:], in_=f_sums[:, b * T + t, :], axis=mybir.AxisListType.X, op=ALU.add)
+            inv_sums[b, t] = inv
+
+        def KR(b, t):
+            nc.vector.reciprocal(out=inv_sums[b, t][:], in_=inv_sums[b, t][:])
+
+        def KS(b, t, engine=None):
+            (engine or nc.vector).tensor_scalar(
+                out=g_all[b][:, t, :], in0=feats[b, t][:], scalar1=inv_sums[b, t][:], scalar2=0.0,
                 op0=ALU.mult, op1=ALU.add,
             )
-            return g_sq
 
-        def sum_over_tokens(b, i, pair_sq):
-            if i == 0:
-                sum_banks[b] = [psum.tile([P, BANK], F32, name="bank") for h in range(HALVES)]
+        def KSG(b, t):
+            KS(b, t, nc.gpsimd)
+
+        def KH(b, t):
+            g_sq = work.tile([P, E], F32, name="g_sq", bufs=SQS)
+            nc.scalar.activation(out=g_sq[:], in_=feats[b, t][:], func=ACT.Square, scale=inv_sums[b, t][:])
+            squares[b, t] = g_sq
+
+        def KA(b, t):
+            nc.gpsimd.tensor_tensor(out=squares[b, t][:], in0=squares[b, t - 1][:], in1=squares[b, t][:], op=ALU.add)
+
+        def KAV(b, t):
+            nc.vector.tensor_tensor(out=squares[b, t][:], in0=squares[b, t - 1][:], in1=squares[b, t][:], op=ALU.add)
+
+        def KN(b, t, first, last):
+            if first:
+                sum_banks[b] = [psum.tile([P, BANK], F32, name="sums", bufs=2) for h in range(HALVES)]
             for h in range(HALVES):
                 nc.tensor.matmul(
-                    out=sum_banks[b][h][:], lhsT=ones_f32[:], rhs=pair_sq[:, h * BANK : (h + 1) * BANK],
-                    start=(i == 0), stop=(i == PAIRS - 1),
+                    out=sum_banks[b][h][:], lhsT=ones_f32[:], rhs=squares[b, t][:, h * BANK : (h + 1) * BANK],
+                    start=bool(first), stop=bool(last),
                 )
 
-        def invert_norms(b):
-            inv_norm = stage.tile([P, E], F32, name="inv_norm")
-            for h in range(HALVES):
-                nc.scalar.activation(
-                    out=inv_norm[:, h * BANK : (h + 1) * BANK], in_=sum_banks[b][h][:], func=ACT.Abs_reciprocal_sqrt
-                )
-            return inv_norm
-
-        v_all = [keep.tile([P, T, E], F32, name="v_all%d" % b) for b in range(B)]
-
-        def add_value_bias(b, t, h, banks):
-            cols = slice(h * BANK, (h + 1) * BANK)
-            nc.vector.tensor_tensor(out=v_all[b][:, t, cols], in0=banks[h][:], in1=bias_all[:, 1, cols], op=ALU.add)
-
-        def regroup_values(b):
-            v_grp = stage.tile([P, E, PACK], BF16, align_bytes=64, name="v_grp", bufs=1)
-            nc.vector.tensor_copy(out=v_grp[:, 0:BANK, :], in_=v_all[b][:, :, 0:BANK].rearrange("p t e -> p e t"))
-            nc.gpsimd.tensor_scalar(
-                out=v_grp[:, BANK:E, :], in0=v_all[b][:, :, BANK:E].rearrange("p t e -> p e t"),
-                scalar1=1.0, scalar2=0.0, op0=ALU.mult, op1=ALU.add,
+        def NR(b, h):
+            if h == 0:
+                inv_norms[b] = stage.tile([P, E], F32, name="inv_norm")
+            nc.scalar.activation(
+                out=inv_norms[b][:, h * BANK : (h + 1) * BANK], in_=sum_banks[b][h][:], func=ACT.Abs_reciprocal_sqrt
             )
-            return v_grp
 
-        def quantise_values(v_grp):
-            v_codes = stage.tile([P, E], U32, align_bytes=64, name="v_codes")
-            v_scales = stage.tile([P, E], U8, align_bytes=64, name="v_scales")
-            for h in range(HALVES):
-                cols = slice(h * BANK, (h + 1) * BANK)
-                nc.vector.quantize_mx(
-                    out=v_codes[:, cols].bitcast(FP8X4), scales=v_scales[:, cols],
-                    in_=v_grp[:, cols, :].rearrange("p e t -> p (e t)"),
-                )
-            return v_codes, v_scales
+        v_grp = {}
+        v_quant = {}
 
-        def normalise_keys(b, j, inv_norm):
+        def VP(b, t):
+            v_banks[b, t] = project(1, b * T + t)
+
+        def VF(b, t, h):
+            cols = slice(h * BANK, (h + 1) * BANK)
+            nc.vector.tensor_tensor(out=v_all[b][:, t, cols], in0=v_banks[b, t][h][:], in1=bias_all[:, 1, cols], op=ALU.add)
+            if h == 1:
+                nc.sync.dma_start(out=out_1[b].rearrange("(p t) e -> p t e", t=T)[:, t, :], in_=v_all[b][:, t, :])
+
+        def VR(b, h, copy=None):
+            cols = slice(h * BANK, (h + 1) * BANK)
+            if h == 0:
+                v_grp[b] = rows.tile([P, E, PACK], BF16, align_bytes=64, name="v_grp", bufs=1)
+            (copy or nc.vector.tensor_copy)(out=v_grp[b][:, cols, :], in_=v_all[b][:, :, cols].rearrange("p t e -> p e t"))
+
+        def VRS(b, h):
+            VR(b, h, nc.scalar.copy)
+
+        def VQ(b, h):
+            if h == 0:
+                v_codes = stage.tile([P, E], U32, align_bytes=64, name="v_codes")
+                v_scales = stage.tile([P, E], U8, align_bytes=64, name="v_scales")
+                v_quant[b] = (v_codes, v_scales)
+            cols = slice(h * BANK, (h + 1) * BANK)
+            nc.vector.quantize_mx(
+                out=v_quant[b][0][:, cols].bitcast(FP8X4), scales=v_quant[b][1][:, cols],
+                in_=v_grp[b][:, cols, :].rearrange("p e t -> p (e t)"),
+            )
+
+        k2_grps = {}
+        k2_quant = {}
+        kv_banks = {}
+        kv_rows = {}
+
+        def M(b, j):
             cols = slice(j * P, (j + 1) * P)
             k2_grp = work.tile([P, P, PACK], BF16, align_bytes=64, name="k2_grp")
             nc.vector.scalar_tensor_tensor(
-                out=k2_grp[:], in0=inv_norm[:, cols].unsqueeze(2).to_broadcast([P, P, PACK]), scalar=1.0 / EPS_NORM,
+                out=k2_grp[:], in0=inv_norms[b][:, cols].unsqueeze(2).to_broadcast([P, P, PACK]), scalar=1.0 / EPS_NORM,
                 in1=g_all[b][:, :, cols].rearrange("p t e -> p e t"), op0=ALU.min, op1=ALU.mult,
             )
-            return k2_grp
+            k2_grps[b, j] = k2_grp
 
-        def key_value(b, j, k2_grp, v_codes, v_scales):
+        def Q(b, j):
             k2_codes = work.tile([P, P], U32, align_bytes=64, name="k2_codes")
             k2_scales = work.tile([P, P], U8, align_bytes=64, name="k2_scales")
             nc.vector.quantize_mx(
-                out=k2_codes[:].bitcast(FP8X4), scales=k2_scales[:], in_=k2_grp[:].rearrange("p e t -> p (e t)")
+                out=k2_codes[:].bitcast(FP8X4), scales=k2_scales[:], in_=k2_grps[b, j][:].rearrange("p e t -> p (e t)")
             )
-            kv_rows = rows.tile([P, E], F32, name="kv_rows")
+            k2_quant[b, j] = (k2_codes, k2_scales)
+
+        def KV(b, j, h):
+            v_codes, v_scales = v_quant[b]
+            k2_codes, k2_scales = k2_quant[b, j]
+            cols = slice(h * BANK, (h + 1) * BANK)
+            bank = psum.tile([P, BANK], F32, name="bank")
+            nc.tensor.matmul_mx(
+                out=bank[:], lhsT=k2_codes[:].bitcast(FP8X4), lhsT_scale=k2_scales[:],
+                rhs=v_codes[:, cols].bitcast(FP8X4), rhs_scale=v_scales[:, cols], start=True, stop=True,
+            )
+            kv_banks[b, j, h] = bank
+
+        def O(b, j, h, copy=None):
+            if (b, j) not in kv_rows:
+                kv_rows[b, j] = rows.tile([P, E], F32, name="kv_rows", bufs=ROWS)
+            (copy or nc.scalar.copy)(out=kv_rows[b, j][:, h * BANK : (h + 1) * BANK], in_=kv_banks[b, j, h][:])
+
+        def OV(b, j, h):
+            O(b, j, h, nc.vector.tensor_copy)
+
+        def ST(b, j):
+            nc.sync.dma_start(out=out_0[b, j * P : (j + 1) * P, :], in_=kv_rows[b, j][:])
+
+        w_raws = {}
+
+        def LX(b, half):
+            tokens = x[b].rearrange("(p t) c -> p t c", t=T)
+            pair = slice(2 * half, 2 * half + 2)
+            nc.sync.dma_start(out=x_raw[b][:, pair, :], in_=tokens[:, pair, :])
+
+        def LW(i, g):
+            w_raw = raw.tile([P, PACK, E], BF16, name="w_raw")
+            w = (wk, wv)[i]
+            for u in range(2):
+                first = g * P * PACK + u * 2 * P
+                nc.sync.dma_start(
+                    out=w_raw[:, 2 * u : 2 * u + 2, :],
+                    in_=w[first : first + 2 * P, :].rearrange("(q e) n -> q e n", e=2),
+                )
+            w_raws[i, g] = w_raw
+
+        def LWH(i, g, h):
+            w = (wk, wv)[i]
+            cols = slice(h * BANK, (h + 1) * BANK)
+            if h == 0:
+                w_raws[i, g] = raw.tile([P, PACK, E], BF16, name="w_raw")
+            for u in range(2):
+                first = g * P * PACK + u * 2 * P
+                nc.sync.dma_start(
+                    out=w_raws[i, g][:, 2 * u : 2 * u + 2, cols],
+                    in_=w[first : first + 2 * P, cols].rearrange("(q e) n -> q e n", e=2),
+                )
+
+        def LB(i):
+            nc.sync.dma_start(out=bias_rows[0:1, i, :], in_=(bk, bv)[i].unsqueeze(0))
+
+        bias_banks = {}
+
+        def BM(i):
+            bank = psum.tile([P, E], BF16, name="bank")
             for h in range(HALVES):
                 cols = slice(h * BANK, (h + 1) * BANK)
-                bank = psum.tile([P, BANK], F32, name="bank")
-                nc.tensor.matmul_mx(
-                    out=bank[:], lhsT=k2_codes[:].bitcast(FP8X4), lhsT_scale=k2_scales[:],
-                    rhs=v_codes[:, cols].bitcast(FP8X4), rhs_scale=v_scales[:, cols], start=True, stop=True,
-                )
-                nc.scalar.copy(out=kv_rows[:, cols], in_=bank[:])
-            nc.sync.dma_start(out=out_0[b, j * P : (j + 1) * P, :], in_=kv_rows[:])
+                nc.tensor.matmul(out=bank[:, cols], lhsT=ones_bf[:], rhs=bias_rows[:, i, cols], start=True, stop=True)
+            bias_banks[i] = bank
 
-        tiles = [divmod(i, T) for i in range(B * T)]
-        pair_sq = []
-        SUM_LAG = 3
-        k_banks = project(wk_codes, wk_scales, 0)
-        v_next = project(wv_codes, wv_scales, 0)
-        row_sum = add_key_bias(0, 0, k_banks)
-        square_centred(0, 0, row_total(row_sum))
-        g_sq = None
-        for r, (b, t) in enumerate(tiles):
-            v_banks = v_next
-            more = r + 1 < len(tiles)
-            if more:
-                nb, nt = tiles[r + 1]
-                k_banks = project(wk_codes, wk_scales, r + 1)
-                v_next = project(wv_codes, wv_scales, r + 1)
-                row_sum = add_key_bias(nb, nt, k_banks)
-            if r >= SUM_LAG and tiles[r - SUM_LAG][1] % 2 == 1:
-                sum_over_tokens(*pair_sq[(r - SUM_LAG) // 2])
-            add_value_bias(b, t, 0, v_banks)
-            if more:
-                total = row_total(row_sum)
-            inv_sum = small.tile([P, 1], F32, name="inv_sum")
-            nc.vector.tensor_reduce(out=inv_sum[:], in_=f_sums[:, r, :], axis=mybir.AxisListType.X, op=ALU.add)
-            add_value_bias(b, t, 1, v_banks)
-            nc.sync.dma_start(out=out_1[b].rearrange("(p t) e -> p t e", t=T)[:, t, :], in_=v_all[b][:, t, :])
-            nc.vector.reciprocal(out=inv_sum[:], in_=inv_sum[:])
-            if more:
-                square_centred(nb, nt, total)
-            else:
-                inv_norm0 = invert_norms(0)
-            g_sq = scale_features(b, t, inv_sum, g_sq)
-            if t % 2 == 1:
-                pair_sq.append((b, t // 2, g_sq))
-            if (b, t) == (0, T - 1):
-                v_grp0 = regroup_values(0)
-            if (b, t) == (1, T - 2):
-                v_codes0, v_scales0 = quantise_values(v_grp0)
+        def BC(i):
+            nc.scalar.copy(out=bias_all[:, i, :], in_=bias_banks[i][:])
 
-        k2_next = normalise_keys(0, 0, inv_norm0)
-        for j in range(CHUNKS):
-            k2_now = k2_next
-            if j + 1 < CHUNKS:
-                k2_next = normalise_keys(0, j + 1, inv_norm0)
-            key_value(0, j, k2_now, v_codes0, v_scales0)
-            if j == 0:
-                sum_over_tokens(*pair_sq[2])
-                v_grp1 = regroup_values(1)
-            if j == 3:
-                sum_over_tokens(*pair_sq[3])
-            if j == 4:
-                inv_norm1 = invert_norms(1)
-            if j == 6:
-                v_codes1, v_scales1 = quantise_values(v_grp1)
+        x_banks = {}
+        x_grps = {}
+        w_grps = {}
 
-        k2_next = normalise_keys(1, 0, inv_norm1)
-        for j in range(CHUNKS):
-            k2_now = k2_next
-            if j + 1 < CHUNKS:
-                k2_next = normalise_keys(1, j + 1, inv_norm1)
-            key_value(1, j, k2_now, v_codes1, v_scales1)
+        def XT(b, t):
+            words = x_raw[b][:].bitcast(F32)
+            bank = psum.tile([P, BANK], F32, name="bank")
+            for q in range(PASSES * 2):
+                nc.tensor.transpose(bank[:, q * P : (q + 1) * P], words[:, t, q * P : (q + 1) * P], ident[:])
+            x_banks[b, t] = bank
+
+        def XC(b, t):
+            x_grp = grouped_pool.tile([P, PASSES * P * PACK], BF16, align_bytes=64, name="x_grp")
+            nc.scalar.copy(
+                out=x_grp[:].bitcast(F32).rearrange("p (g r u) -> p g r u", g=PASSES, u=2),
+                in_=x_banks[b, t][:].rearrange("p (g u r) -> p g r u", g=PASSES, u=2),
+            )
+            x_grps[b, t] = x_grp
+
+        def XQ(b, t):
+            nc.vector.quantize_mx(
+                out=x_codes[:, b * T + t, :].bitcast(FP8X4), scales=x_scales[:, b * T + t, :], in_=x_grps[b, t][:]
+            )
+
+        def regroup(copy, i, g, cols):
+            if (i, g) not in w_grps:
+                w_grps[i, g] = grouped_pool.tile([P, E, PACK], BF16, align_bytes=64, name="w_grp")
+            copy(
+                out=w_grps[i, g][:, cols, :].rearrange("p (c i) t -> p c t i", i=4),
+                in_=w_raws[i, g][:, :, cols].rearrange("p t (c i) -> p c t i", i=4),
+            )
+
+        def WGV(i, g):
+            regroup(nc.vector.tensor_copy, i, g, slice(0, VECTOR_COLS[i]))
+
+        def WGS(i, g):
+            regroup(nc.scalar.copy, i, g, slice(VECTOR_COLS[i], E))
+
+        def WQ(i, g, h):
+            cols = slice(h * BANK, (h + 1) * BANK)
+            nc.vector.quantize_mx(
+                out=w_codes[i][:, g, cols].bitcast(FP8X4), scales=w_scales[i][:, g, cols],
+                in_=w_grps[i, g][:, cols, :].rearrange("p n t -> p (n t)"),
+            )
+
+        with tc.tile_pool(name="loaded", bufs=1) as loaded, tc.tile_pool(name="raw", bufs=3) as raw, tc.tile_pool(
+            name="grouped", bufs=2
+        ) as grouped_pool:
+            x_raw = [loaded.tile([P, T, C], BF16, name="x_raw%d" % b) for b in range(B)]
+            LWH(0, 0, 0)
+            WGV(0, 0)
+            LX(0, 0)
+            XT(0, 0)
+            XC(0, 0)
+            XQ(0, 0)
+            LWH(0, 0, 1)
+            WGS(0, 0)
+            LB(0)
+            BM(0)
+            LB(1)
+            BM(1)
+            XT(0, 1)
+            XC(0, 1)
+            LWH(0, 1, 0)
+            WGV(0, 1)
+            WQ(0, 0, 0)
+            WQ(0, 1, 0)
+            XQ(0, 1)
+            WQ(0, 0, 1)
+            LWH(0, 1, 1)
+            WGS(0, 1)
+            WQ(0, 1, 1)
+            LX(0, 1)
+            XT(0, 2)
+            XC(0, 2)
+            XQ(0, 2)
+            XT(0, 3)
+            BC(0)
+            KP(0, 0)
+            BC(1)
+            KP(0, 1)
+            XC(0, 3)
+            KP(0, 2)
+            LW(1, 0)
+            WGV(1, 0)
+            KE(0, 0)
+            XQ(0, 3)
+            KE(0, 1)
+            KT(0, 0)
+            KE(0, 2)
+            KT(0, 1)
+            WGS(1, 0)
+            WQ(1, 0, 0)
+            LW(1, 1)
+            LX(1, 0)
+            XT(1, 0)
+            XC(1, 0)
+            XQ(1, 0)
+            KT(0, 2)
+            XT(1, 1)
+            WGS(1, 1)
+            WGV(1, 1)
+            WQ(1, 0, 1)
+            KP(0, 3)
+            KG(0, 0)
+            KE(0, 3)
+            XC(1, 1)
+            XQ(1, 1)
+            KI(0, 0)
+            KT(0, 3)
+            KG(0, 1)
+            LX(1, 1)
+            XT(1, 2)
+            XT(1, 3)
+            KP(1, 0)
+            KE(1, 0)
+            KR(0, 0)
+            XC(1, 2)
+            WQ(1, 1, 0)
+            KP(1, 1)
+            WQ(1, 1, 1)
+            KG(0, 2)
+            KT(1, 0)
+            VP(0, 0)
+            KI(0, 1)
+            XC(1, 3)
+            KE(1, 1)
+            VP(0, 1)
+            KR(0, 1)
+            KG(0, 3)
+            KS(0, 0)
+            KS(0, 1)
+            KH(0, 0)
+            XQ(1, 2)
+            KP(1, 2)
+            KH(0, 1)
+            KA(0, 1)
+            XQ(1, 3)
+        rows = ctx.enter_context(tc.tile_pool(name="rows", bufs=ROWS))
+        KT(1, 1)
+        KG(1, 0)
+        KI(0, 2)
+        VF(0, 0, 0)
+        KR(0, 2)
+        KH(0, 2)
+        VF(0, 0, 1)
+        VP(0, 2)
+        KG(1, 1)
+        KI(0, 3)
+        VF(0, 1, 0)
+        KR(0, 3)
+        KH(0, 3)
+        VF(0, 1, 1)
+        KP(1, 3)
+        KS(0, 2)
+        KE(1, 2)
+        VP(0, 3)
+        KN(0, 1, 1, 0)
+        KI(1, 0)
+        KT(1, 2)
+        KG(1, 2)
+        VF(0, 2, 0)
+        KR(1, 0)
+        KH(1, 0)
+        VF(0, 2, 1)
+        KE(1, 3)
+        KI(1, 1)
+        KT(1, 3)
+        KG(1, 3)
+        VF(0, 3, 0)
+        KR(1, 1)
+        KH(1, 1)
+        VF(0, 3, 1)
+        KS(0, 3)
+        KA(0, 3)
+        KN(0, 3, 0, 1)
+        VP(1, 0)
+        NR(0, 0)
+        NR(0, 1)
+        KN(1, 0, 1, 0)
+        VP(1, 1)
+        KN(1, 1, 0, 0)
+        VR(0, 0)
+        VF(1, 0, 0)
+        VR(0, 1)
+        VF(1, 0, 1)
+        KI(1, 2)
+        KI(1, 3)
+        VQ(0, 0)
+        KR(1, 2)
+        KH(1, 2)
+        KR(1, 3)
+        KH(1, 3)
+        VQ(0, 1)
+        M(0, 0)
+        KS(1, 0)
+        M(0, 1)
+        Q(0, 0)
+        KV(0, 0, 0)
+        KV(0, 0, 1)
+        O(0, 0, 0)
+        O(0, 0, 1)
+        ST(0, 0)
+        VF(1, 1, 0)
+        VF(1, 1, 1)
+        Q(0, 1)
+        KV(0, 1, 0)
+        KV(0, 1, 1)
+        VP(1, 2)
+        O(0, 1, 0)
+        O(0, 1, 1)
+        ST(0, 1)
+        M(0, 2)
+        KS(1, 1)
+        Q(0, 2)
+        KV(0, 2, 0)
+        KV(0, 2, 1)
+        O(0, 2, 0)
+        O(0, 2, 1)
+        ST(0, 2)
+        M(0, 3)
+        M(0, 4)
+        Q(0, 3)
+        KV(0, 3, 0)
+        KV(0, 3, 1)
+        VP(1, 3)
+        O(0, 3, 0)
+        O(0, 3, 1)
+        ST(0, 3)
+        VF(1, 2, 0)
+        VF(1, 2, 1)
+        Q(0, 4)
+        KV(0, 4, 0)
+        KV(0, 4, 1)
+        O(0, 4, 0)
+        O(0, 4, 1)
+        ST(0, 4)
+        M(0, 5)
+        KS(1, 2)
+        Q(0, 5)
+        KV(0, 5, 0)
+        KV(0, 5, 1)
+        KN(1, 2, 0, 0)
+        O(0, 5, 0)
+        KN(1, 3, 0, 1)
+        O(0, 5, 1)
+        ST(0, 5)
+        NR(1, 0)
+        NR(1, 1)
+        M(0, 6)
+        VF(1, 3, 0)
+        VF(1, 3, 1)
+        Q(0, 6)
+        KV(0, 6, 0)
+        KV(0, 6, 1)
+        O(0, 6, 0)
+        O(0, 6, 1)
+        ST(0, 6)
+        M(0, 7)
+        KS(1, 3)
+        VR(1, 0)
+        Q(0, 7)
+        KV(0, 7, 0)
+        KV(0, 7, 1)
+        O(0, 7, 0)
+        O(0, 7, 1)
+        ST(0, 7)
+        VR(1, 1)
+        VQ(1, 0)
+        VQ(1, 1)
+        M(1, 0)
+        M(1, 1)
+        Q(1, 0)
+        KV(1, 0, 0)
+        KV(1, 0, 1)
+        O(1, 0, 0)
+        O(1, 0, 1)
+        ST(1, 0)
+        M(1, 2)
+        Q(1, 1)
+        KV(1, 1, 0)
+        KV(1, 1, 1)
+        O(1, 1, 0)
+        M(1, 3)
+        Q(1, 2)
+        KV(1, 2, 0)
+        KV(1, 2, 1)
+        O(1, 2, 0)
+        O(1, 2, 1)
+        M(1, 4)
+        Q(1, 3)
+        KV(1, 3, 0)
+        KV(1, 3, 1)
+        O(1, 3, 0)
+        OV(1, 1, 1)
+        ST(1, 1)
+        ST(1, 2)
+        M(1, 5)
+        Q(1, 4)
+        KV(1, 4, 0)
+        O(1, 4, 0)
+        KV(1, 4, 1)
+        O(1, 4, 1)
+        M(1, 6)
+        Q(1, 5)
+        KV(1, 5, 0)
+        O(1, 5, 0)
+        KV(1, 5, 1)
+        OV(1, 3, 1)
+        ST(1, 3)
+        ST(1, 4)
+        M(1, 7)
+        Q(1, 6)
+        KV(1, 6, 0)
+        O(1, 6, 0)
+        KV(1, 6, 1)
+        O(1, 6, 1)
+        Q(1, 7)
+        KV(1, 7, 0)
+        O(1, 7, 0)
+        KV(1, 7, 1)
+        O(1, 7, 1)
+        OV(1, 5, 1)
+        ST(1, 5)
+        ST(1, 6)
+        ST(1, 7)

@@ -50,8 +50,7 @@ def tile_essattn_pa_kernel(tc, x, wk, bk, wv, bv, out_0, out_1):
         nc.scalar.activation(out=warm[:], in_=ones_f32[:, 0:1], func=ACT.Abs_reciprocal_sqrt)
         bias_rows = const.tile([P, 2, E], BF16)
         nc.gpsimd.memset(bias_rows[:], 0.0)
-        f_sums = const.tile([P, B * T, 2], F32)
-        nc.vector.memset(f_sums[:], E * E * EPS_SUM)
+        f_sums = const.tile([P, B * T], F32)
         bias_all = const.tile([P, 2, E], BF16)
 
         x_codes = keep.tile([P, B * T, PASSES * P], U32, align_bytes=64)
@@ -84,6 +83,7 @@ def tile_essattn_pa_kernel(tc, x, wk, bk, wv, bv, out_0, out_1):
         row_sums = {}
         totals = {}
         inv_sums = {}
+        dens = {}
         squares = {}
         sum_banks = {}
         inv_norms = {}
@@ -105,28 +105,35 @@ def tile_essattn_pa_kernel(tc, x, wk, bk, wv, bv, out_0, out_1):
             feats[b, t] = feat
             row_sums[b, t] = row_sum
 
-        def KT(b, t):
+        def KTG(b, t):
             total = small.tile([P, 1], F32, name="total")
-            nc.vector.tensor_reduce(out=total[:], in_=row_sums[b, t][:], axis=mybir.AxisListType.X, op=ALU.add)
+            nc.gpsimd.tensor_tensor(out=total[:], in0=row_sums[b, t][:, 0:1], in1=row_sums[b, t][:, 1:2], op=ALU.add)
             totals[b, t] = total
 
         def KG(b, t):
             nc.scalar.activation(
                 out=feats[b, t][:], in_=feats[b, t][:], func=ACT.Square, bias=totals[b, t][:], scale=-float(E),
-                accum_out=f_sums[:, b * T + t, 0:1],
+                accum_out=f_sums[:, b * T + t : b * T + t + 1],
             )
 
-        def KI(b, t):
-            inv = small.tile([P, 1], F32, name="inv_sum", bufs=8)
-            nc.vector.tensor_reduce(out=inv[:], in_=f_sums[:, b * T + t, :], axis=mybir.AxisListType.X, op=ALU.add)
-            inv_sums[b, t] = inv
+        def KDG(b, p):
+            den = small.tile([P, 2], F32, name="den")
+            first = b * T + 2 * p
+            nc.gpsimd.tensor_scalar(
+                out=den[:], in0=f_sums[:, first : first + 2], scalar1=1.0, scalar2=E * E * EPS_SUM,
+                op0=ALU.mult, op1=ALU.add,
+            )
+            dens[b, p] = den
 
-        def KR(b, t):
-            nc.vector.reciprocal(out=inv_sums[b, t][:], in_=inv_sums[b, t][:])
+        def KR2(b, p):
+            inv = small.tile([P, 2], F32, name="inv_sum", bufs=4)
+            nc.vector.reciprocal(out=inv[:], in_=dens[b, p][:])
+            for i in range(2):
+                inv_sums[b, 2 * p + i] = inv[:, i : i + 1]
 
         def KS(b, t, engine=None):
             (engine or nc.vector).tensor_scalar(
-                out=g_all[b][:, t, :], in0=feats[b, t][:], scalar1=inv_sums[b, t][:], scalar2=0.0,
+                out=g_all[b][:, t, :], in0=feats[b, t][:], scalar1=inv_sums[b, t], scalar2=0.0,
                 op0=ALU.mult, op1=ALU.add,
             )
 
@@ -135,7 +142,7 @@ def tile_essattn_pa_kernel(tc, x, wk, bk, wv, bv, out_0, out_1):
 
         def KH(b, t):
             g_sq = work.tile([P, E], F32, name="g_sq", bufs=SQS)
-            nc.scalar.activation(out=g_sq[:], in_=feats[b, t][:], func=ACT.Square, scale=inv_sums[b, t][:])
+            nc.scalar.activation(out=g_sq[:], in_=feats[b, t][:], func=ACT.Square, scale=inv_sums[b, t])
             squares[b, t] = g_sq
 
         def KA(b, t):
@@ -174,7 +181,7 @@ def tile_essattn_pa_kernel(tc, x, wk, bk, wv, bv, out_0, out_1):
 
         def VR(b, h, copy=None):
             cols = slice(h * BANK, (h + 1) * BANK)
-            if h == 0:
+            if b not in v_grp:
                 v_grp[b] = rows.tile([P, E, PACK], BF16, align_bytes=64, name="v_grp", bufs=1)
             (copy or nc.vector.tensor_copy)(out=v_grp[b][:, cols, :], in_=v_all[b][:, :, cols].rearrange("p t e -> p e t"))
 
@@ -197,22 +204,24 @@ def tile_essattn_pa_kernel(tc, x, wk, bk, wv, bv, out_0, out_1):
         kv_banks = {}
         kv_rows = {}
 
-        def M(b, j):
-            cols = slice(j * P, (j + 1) * P)
-            k2_grp = work.tile([P, P, PACK], BF16, align_bytes=64, name="k2_grp")
+        def M2(b, q):
+            cols = slice(2 * q * P, 2 * (q + 1) * P)
+            k2_grp = work.tile([P, 2 * P, PACK], BF16, align_bytes=64, name="k2_grp", bufs=2)
             nc.vector.scalar_tensor_tensor(
-                out=k2_grp[:], in0=inv_norms[b][:, cols].unsqueeze(2).to_broadcast([P, P, PACK]), scalar=1.0 / EPS_NORM,
+                out=k2_grp[:], in0=inv_norms[b][:, cols].unsqueeze(2).to_broadcast([P, 2 * P, PACK]), scalar=1.0 / EPS_NORM,
                 in1=g_all[b][:, :, cols].rearrange("p t e -> p e t"), op0=ALU.min, op1=ALU.mult,
             )
-            k2_grps[b, j] = k2_grp
+            k2_grps[b, q] = k2_grp
 
-        def Q(b, j):
-            k2_codes = work.tile([P, P], U32, align_bytes=64, name="k2_codes")
-            k2_scales = work.tile([P, P], U8, align_bytes=64, name="k2_scales")
+        def Q2(b, q):
+            k2_codes = work.tile([P, 2 * P], U32, align_bytes=64, name="k2_codes")
+            k2_scales = work.tile([P, 2 * P], U8, align_bytes=64, name="k2_scales")
             nc.vector.quantize_mx(
-                out=k2_codes[:].bitcast(FP8X4), scales=k2_scales[:], in_=k2_grps[b, j][:].rearrange("p e t -> p (e t)")
+                out=k2_codes[:].bitcast(FP8X4), scales=k2_scales[:], in_=k2_grps[b, q][:].rearrange("p e t -> p (e t)")
             )
-            k2_quant[b, j] = (k2_codes, k2_scales)
+            for i in range(2):
+                rows_of_j = slice(i * P, (i + 1) * P)
+                k2_quant[b, 2 * q + i] = (k2_codes[:, rows_of_j], k2_scales[:, rows_of_j])
 
         def KV(b, j, h):
             v_codes, v_scales = v_quant[b]
@@ -220,7 +229,7 @@ def tile_essattn_pa_kernel(tc, x, wk, bk, wv, bv, out_0, out_1):
             cols = slice(h * BANK, (h + 1) * BANK)
             bank = psum.tile([P, BANK], F32, name="bank")
             nc.tensor.matmul_mx(
-                out=bank[:], lhsT=k2_codes[:].bitcast(FP8X4), lhsT_scale=k2_scales[:],
+                out=bank[:], lhsT=k2_codes.bitcast(FP8X4), lhsT_scale=k2_scales,
                 rhs=v_codes[:, cols].bitcast(FP8X4), rhs_scale=v_scales[:, cols], start=True, stop=True,
             )
             kv_banks[b, j, h] = bank
@@ -232,6 +241,10 @@ def tile_essattn_pa_kernel(tc, x, wk, bk, wv, bv, out_0, out_1):
 
         def OV(b, j, h):
             O(b, j, h, nc.vector.tensor_copy)
+
+        def STH(b, j, h):
+            cols = slice(h * BANK, (h + 1) * BANK)
+            nc.sync.dma_start(out=out_0[b, j * P : (j + 1) * P, cols], in_=kv_rows[b, j][:, cols])
 
         def ST(b, j):
             nc.sync.dma_start(out=out_0[b, j * P : (j + 1) * P, :], in_=kv_rows[b, j][:])
@@ -293,16 +306,25 @@ def tile_essattn_pa_kernel(tc, x, wk, bk, wv, bv, out_0, out_1):
             x_banks[b, t] = bank
 
         def XC(b, t):
-            x_grp = grouped_pool.tile([P, PASSES * P * PACK], BF16, align_bytes=64, name="x_grp")
+            if t % 2 == 0:
+                x_grps[b, t // 2] = grouped_pool.tile([P, 2, PASSES * P * PACK], BF16, align_bytes=64, name="x_grp")
             nc.scalar.copy(
-                out=x_grp[:].bitcast(F32).rearrange("p (g r u) -> p g r u", g=PASSES, u=2),
+                out=x_grps[b, t // 2][:, t % 2, :].bitcast(F32).rearrange("p (g r u) -> p g r u", g=PASSES, u=2),
                 in_=x_banks[b, t][:].rearrange("p (g u r) -> p g r u", g=PASSES, u=2),
             )
-            x_grps[b, t] = x_grp
 
         def XQ(b, t):
+            i = b * T + t
             nc.vector.quantize_mx(
-                out=x_codes[:, b * T + t, :].bitcast(FP8X4), scales=x_scales[:, b * T + t, :], in_=x_grps[b, t][:]
+                out=x_codes[:, i, :].bitcast(FP8X4), scales=x_scales[:, i, :], in_=x_grps[b, t // 2][:, t % 2, :]
+            )
+
+        def XQ2(b, p):
+            i = b * T + 2 * p
+            nc.vector.quantize_mx(
+                out=x_codes[:, i : i + 2, :].rearrange("p i c -> p (i c)").bitcast(FP8X4),
+                scales=x_scales[:, i : i + 2, :].rearrange("p i c -> p (i c)"),
+                in_=x_grps[b, p][:].rearrange("p i c -> p (i c)"),
             )
 
         def regroup(copy, i, g, cols):
@@ -311,6 +333,12 @@ def tile_essattn_pa_kernel(tc, x, wk, bk, wv, bv, out_0, out_1):
             copy(
                 out=w_grps[i, g][:, cols, :].rearrange("p (c i) t -> p c t i", i=4),
                 in_=w_raws[i, g][:, :, cols].rearrange("p t (c i) -> p c t i", i=4),
+            )
+
+        def WQF(i, g):
+            nc.vector.quantize_mx(
+                out=w_codes[i][:, g, :].bitcast(FP8X4), scales=w_scales[i][:, g, :],
+                in_=w_grps[i, g][:].rearrange("p n t -> p (n t)"),
             )
 
         def WGV(i, g):
@@ -332,23 +360,23 @@ def tile_essattn_pa_kernel(tc, x, wk, bk, wv, bv, out_0, out_1):
             x_raw = [loaded.tile([P, T, C], BF16, name="x_raw%d" % b) for b in range(B)]
             LWH(0, 0, 0)
             WGV(0, 0)
+            WQ(0, 0, 0)
             LX(0, 0)
             XT(0, 0)
             XC(0, 0)
+            XT(0, 1)
             XQ(0, 0)
             LWH(0, 0, 1)
             WGS(0, 0)
+            XC(0, 1)
             LB(0)
             BM(0)
             LB(1)
             BM(1)
-            XT(0, 1)
-            XC(0, 1)
             LWH(0, 1, 0)
             WGV(0, 1)
-            WQ(0, 0, 0)
-            WQ(0, 1, 0)
             XQ(0, 1)
+            WQ(0, 1, 0)
             WQ(0, 0, 1)
             LWH(0, 1, 1)
             WGS(0, 1)
@@ -356,254 +384,228 @@ def tile_essattn_pa_kernel(tc, x, wk, bk, wv, bv, out_0, out_1):
             LX(0, 1)
             XT(0, 2)
             XC(0, 2)
-            XQ(0, 2)
             XT(0, 3)
             BC(0)
             KP(0, 0)
             BC(1)
+            XQ(0, 2)
             KP(0, 1)
             XC(0, 3)
             KP(0, 2)
             LW(1, 0)
             WGV(1, 0)
             KE(0, 0)
+            KTG(0, 0)
+            WGS(1, 0)
             XQ(0, 3)
             KE(0, 1)
-            KT(0, 0)
+            KTG(0, 1)
             KE(0, 2)
-            KT(0, 1)
-            WGS(1, 0)
-            WQ(1, 0, 0)
+            KTG(0, 2)
             LW(1, 1)
+            WGV(1, 1)
             LX(1, 0)
             XT(1, 0)
             XC(1, 0)
-            XQ(1, 0)
-            KT(0, 2)
             XT(1, 1)
-            WGS(1, 1)
-            WGV(1, 1)
-            WQ(1, 0, 1)
-            KP(0, 3)
             KG(0, 0)
-            KE(0, 3)
+            KP(0, 3)
             XC(1, 1)
-            XQ(1, 1)
-            KI(0, 0)
-            KT(0, 3)
+            XQ(1, 0)
+            WGS(1, 1)
+            WQF(1, 0)
             KG(0, 1)
+            KE(0, 3)
+            KTG(0, 3)
+            XQ(1, 1)
+            KDG(0, 0)
             LX(1, 1)
             XT(1, 2)
             XT(1, 3)
             KP(1, 0)
-            KE(1, 0)
-            KR(0, 0)
             XC(1, 2)
-            WQ(1, 1, 0)
             KP(1, 1)
-            WQ(1, 1, 1)
-            KG(0, 2)
-            KT(1, 0)
-            VP(0, 0)
-            KI(0, 1)
+            KE(1, 0)
             XC(1, 3)
-            KE(1, 1)
+            WQF(1, 1)
+            VP(0, 0)
+            KG(0, 2)
+            KR2(0, 0)
             VP(0, 1)
-            KR(0, 1)
+            KE(1, 1)
             KG(0, 3)
-            KS(0, 0)
-            KS(0, 1)
-            KH(0, 0)
-            XQ(1, 2)
-            KP(1, 2)
-            KH(0, 1)
-            KA(0, 1)
-            XQ(1, 3)
+            XQ2(1, 1)
         rows = ctx.enter_context(tc.tile_pool(name="rows", bufs=ROWS))
-        KT(1, 1)
-        KG(1, 0)
-        KI(0, 2)
+        KP(1, 2)
+        KH(0, 0)
+        KS(0, 0)
+        KS(0, 1)
         VF(0, 0, 0)
-        KR(0, 2)
-        KH(0, 2)
         VF(0, 0, 1)
         VP(0, 2)
+        KTG(1, 0)
+        KG(1, 0)
+        KH(0, 1)
+        KTG(1, 1)
         KG(1, 1)
-        KI(0, 3)
+        KDG(0, 1)
+        KR2(0, 1)
+        KH(0, 2)
         VF(0, 1, 0)
-        KR(0, 3)
-        KH(0, 3)
         VF(0, 1, 1)
         KP(1, 3)
-        KS(0, 2)
+        KH(0, 3)
         KE(1, 2)
         VP(0, 3)
-        KN(0, 1, 1, 0)
-        KI(1, 0)
-        KT(1, 2)
-        KG(1, 2)
+        KS(0, 2)
         VF(0, 2, 0)
-        KR(1, 0)
-        KH(1, 0)
         VF(0, 2, 1)
         KE(1, 3)
-        KI(1, 1)
-        KT(1, 3)
-        KG(1, 3)
         VF(0, 3, 0)
-        KR(1, 1)
-        KH(1, 1)
         VF(0, 3, 1)
         KS(0, 3)
+        KA(0, 1)
+        KN(0, 1, 1, 0)
+        VP(1, 0)
+        KTG(1, 2)
+        KG(1, 2)
         KA(0, 3)
         KN(0, 3, 0, 1)
-        VP(1, 0)
+        VP(1, 1)
+        VP(1, 2)
+        KTG(1, 3)
+        KG(1, 3)
+        KDG(1, 0)
+        KR2(1, 0)
+        KH(1, 0)
         NR(0, 0)
         NR(0, 1)
+        KH(1, 1)
+        VRS(0, 1)
+        VF(1, 0, 0)
+        VF(1, 0, 1)
+        VP(1, 3)
         KN(1, 0, 1, 0)
-        VP(1, 1)
         KN(1, 1, 0, 0)
         VR(0, 0)
-        VF(1, 0, 0)
-        VR(0, 1)
-        VF(1, 0, 1)
-        KI(1, 2)
-        KI(1, 3)
-        VQ(0, 0)
-        KR(1, 2)
-        KH(1, 2)
-        KR(1, 3)
-        KH(1, 3)
-        VQ(0, 1)
-        M(0, 0)
-        KS(1, 0)
-        M(0, 1)
-        Q(0, 0)
-        KV(0, 0, 0)
-        KV(0, 0, 1)
-        O(0, 0, 0)
-        O(0, 0, 1)
-        ST(0, 0)
         VF(1, 1, 0)
         VF(1, 1, 1)
-        Q(0, 1)
+        KS(1, 0)
+        VQ(0, 0)
+        VF(1, 2, 0)
+        VF(1, 2, 1)
+        KDG(1, 1)
+        KR2(1, 1)
+        KH(1, 2)
+        KN(1, 2, 0, 0)
+        KH(1, 3)
+        KS(1, 1)
+        VF(1, 3, 0)
+        VF(1, 3, 1)
+        M2(0, 0)
+        M2(0, 1)
+        Q2(0, 0)
+        KV(0, 0, 0)
+        O(0, 0, 0)
+        VQ(0, 1)
+        KV(0, 0, 1)
         KV(0, 1, 0)
         KV(0, 1, 1)
-        VP(1, 2)
+        O(0, 0, 1)
+        ST(0, 0)
         O(0, 1, 0)
         O(0, 1, 1)
         ST(0, 1)
-        M(0, 2)
-        KS(1, 1)
-        Q(0, 2)
+        Q2(0, 1)
         KV(0, 2, 0)
         KV(0, 2, 1)
-        O(0, 2, 0)
-        O(0, 2, 1)
-        ST(0, 2)
-        M(0, 3)
-        M(0, 4)
-        Q(0, 3)
         KV(0, 3, 0)
         KV(0, 3, 1)
-        VP(1, 3)
+        O(0, 2, 0)
+        KN(1, 3, 0, 1)
+        O(0, 2, 1)
+        ST(0, 2)
         O(0, 3, 0)
         O(0, 3, 1)
         ST(0, 3)
-        VF(1, 2, 0)
-        VF(1, 2, 1)
-        Q(0, 4)
+        KS(1, 2)
+        M2(0, 2)
+        KS(1, 3)
+        Q2(0, 2)
         KV(0, 4, 0)
         KV(0, 4, 1)
+        KV(0, 5, 0)
         O(0, 4, 0)
+        KV(0, 5, 1)
         O(0, 4, 1)
         ST(0, 4)
-        M(0, 5)
-        KS(1, 2)
-        Q(0, 5)
-        KV(0, 5, 0)
-        KV(0, 5, 1)
-        KN(1, 2, 0, 0)
         O(0, 5, 0)
-        KN(1, 3, 0, 1)
         O(0, 5, 1)
         ST(0, 5)
         NR(1, 0)
         NR(1, 1)
-        M(0, 6)
-        VF(1, 3, 0)
-        VF(1, 3, 1)
-        Q(0, 6)
+        M2(0, 3)
+        VR(1, 0)
+        Q2(0, 3)
         KV(0, 6, 0)
         KV(0, 6, 1)
+        KV(0, 7, 0)
+        KV(0, 7, 1)
         O(0, 6, 0)
         O(0, 6, 1)
         ST(0, 6)
-        M(0, 7)
-        KS(1, 3)
-        VR(1, 0)
-        Q(0, 7)
-        KV(0, 7, 0)
-        KV(0, 7, 1)
         O(0, 7, 0)
+        VR(1, 1)
         O(0, 7, 1)
         ST(0, 7)
-        VR(1, 1)
         VQ(1, 0)
         VQ(1, 1)
-        M(1, 0)
-        M(1, 1)
-        Q(1, 0)
+        M2(1, 0)
+        M2(1, 1)
+        Q2(1, 0)
         KV(1, 0, 0)
         KV(1, 0, 1)
+        KV(1, 1, 0)
+        KV(1, 1, 1)
         O(1, 0, 0)
         O(1, 0, 1)
         ST(1, 0)
-        M(1, 2)
-        Q(1, 1)
-        KV(1, 1, 0)
-        KV(1, 1, 1)
         O(1, 1, 0)
-        M(1, 3)
-        Q(1, 2)
+        M2(1, 2)
+        Q2(1, 1)
         KV(1, 2, 0)
         KV(1, 2, 1)
-        O(1, 2, 0)
-        O(1, 2, 1)
-        M(1, 4)
-        Q(1, 3)
         KV(1, 3, 0)
         KV(1, 3, 1)
-        O(1, 3, 0)
+        O(1, 2, 0)
+        O(1, 2, 1)
         OV(1, 1, 1)
         ST(1, 1)
         ST(1, 2)
-        M(1, 5)
-        Q(1, 4)
+        O(1, 3, 0)
+        M2(1, 3)
+        Q2(1, 2)
         KV(1, 4, 0)
-        O(1, 4, 0)
         KV(1, 4, 1)
-        O(1, 4, 1)
-        M(1, 6)
-        Q(1, 5)
         KV(1, 5, 0)
-        O(1, 5, 0)
+        O(1, 4, 0)
         KV(1, 5, 1)
+        O(1, 5, 0)
         OV(1, 3, 1)
         ST(1, 3)
-        ST(1, 4)
-        M(1, 7)
-        Q(1, 6)
+        Q2(1, 3)
         KV(1, 6, 0)
-        O(1, 6, 0)
+        O(1, 5, 1)
         KV(1, 6, 1)
-        O(1, 6, 1)
-        Q(1, 7)
-        KV(1, 7, 0)
-        O(1, 7, 0)
-        KV(1, 7, 1)
-        O(1, 7, 1)
-        OV(1, 5, 1)
+        OV(1, 4, 1)
+        ST(1, 4)
         ST(1, 5)
+        O(1, 6, 0)
+        KV(1, 7, 0)
+        OV(1, 6, 1)
         ST(1, 6)
-        ST(1, 7)
+        O(1, 7, 0)
+        STH(1, 7, 0)
+        KV(1, 7, 1)
+        OV(1, 7, 1)
+        STH(1, 7, 1)

@@ -19,10 +19,10 @@ PASSES = C // (P * PACK)
 BANK = 512
 HALVES = E // BANK
 CHUNKS = E // P
-VECTOR_COLS = (512, 256)
+VECTOR_COLS = (768, 256)
 FEATS = 6
 SQS = 5
-ROWS = 6
+ROWS = 8
 EPS_SUM = 1e-7
 EPS_NORM = 1e-12
 
@@ -50,7 +50,6 @@ def tile_essattn_pa_kernel(tc, x, wk, bk, wv, bv, out_0, out_1):
         nc.scalar.activation(out=warm[:], in_=ones_f32[:, 0:1], func=ACT.Abs_reciprocal_sqrt)
         bias_rows = const.tile([P, 2, E], BF16)
         nc.gpsimd.memset(bias_rows[:], 0.0)
-        f_sums = const.tile([P, B * T], F32)
         bias_all = const.tile([P, 2, E], BF16)
 
         x_codes = keep.tile([P, B * T, PASSES * P], U32, align_bytes=64)
@@ -80,7 +79,10 @@ def tile_essattn_pa_kernel(tc, x, wk, bk, wv, bv, out_0, out_1):
             return banks
 
         feats = {}
-        row_sums = {}
+        row_pairs = {}
+        f_pairs = {(b, p): const.tile([P, 2, 2], F32, name="f_pair%d%d" % (b, p)) for b in range(B) for p in range(2)}
+        for pair in f_pairs.values():
+            nc.vector.memset(pair[:], E * E * EPS_SUM)
         totals = {}
         inv_sums = {}
         dens = {}
@@ -94,36 +96,34 @@ def tile_essattn_pa_kernel(tc, x, wk, bk, wv, bv, out_0, out_1):
             k_banks[b, t] = project(0, b * T + t)
 
         def KE(b, t):
-            row_sum = small.tile([P, HALVES], F32, name="row_sum")
+            if t % 2 == 0:
+                row_pairs[b, t // 2] = small.tile([P, 2, HALVES], F32, name="row_pair")
+            row_sum = row_pairs[b, t // 2]
             feat = work.tile([P, E], F32, name="feat", bufs=FEATS)
             for h in range(HALVES):
                 cols = slice(h * BANK, (h + 1) * BANK)
                 nc.vector.scalar_tensor_tensor(
                     out=feat[:, cols], in0=k_banks[b, t][h][:], scalar=1.0, in1=bias_all[:, 0, cols],
-                    op0=ALU.mult, op1=ALU.add, accum_out=row_sum[:, h : h + 1],
+                    op0=ALU.mult, op1=ALU.add, accum_out=row_sum[:, t % 2, h : h + 1],
                 )
             feats[b, t] = feat
-            row_sums[b, t] = row_sum
 
-        def KTG(b, t):
-            total = small.tile([P, 1], F32, name="total")
-            nc.gpsimd.tensor_tensor(out=total[:], in0=row_sums[b, t][:, 0:1], in1=row_sums[b, t][:, 1:2], op=ALU.add)
-            totals[b, t] = total
+        def KT2(b, p):
+            total = small.tile([P, 2], F32, name="total2")
+            nc.vector.tensor_reduce(out=total[:], in_=row_pairs[b, p][:], axis=mybir.AxisListType.X, op=ALU.add)
+            for i in range(2):
+                totals[b, 2 * p + i] = total[:, i : i + 1]
+
+        def KI2(b, p):
+            den = small.tile([P, 2], F32, name="den")
+            nc.vector.tensor_reduce(out=den[:], in_=f_pairs[b, p][:], axis=mybir.AxisListType.X, op=ALU.add)
+            dens[b, p] = den
 
         def KG(b, t):
             nc.scalar.activation(
-                out=feats[b, t][:], in_=feats[b, t][:], func=ACT.Square, bias=totals[b, t][:], scale=-float(E),
-                accum_out=f_sums[:, b * T + t : b * T + t + 1],
+                out=feats[b, t][:], in_=feats[b, t][:], func=ACT.Square, bias=totals[b, t], scale=-float(E),
+                accum_out=f_pairs[b, t // 2][:, t % 2, 0:1],
             )
-
-        def KDG(b, p):
-            den = small.tile([P, 2], F32, name="den")
-            first = b * T + 2 * p
-            nc.gpsimd.tensor_scalar(
-                out=den[:], in0=f_sums[:, first : first + 2], scalar1=1.0, scalar2=E * E * EPS_SUM,
-                op0=ALU.mult, op1=ALU.add,
-            )
-            dens[b, p] = den
 
         def KR2(b, p):
             inv = small.tile([P, 2], F32, name="inv_sum", bufs=4)
@@ -342,7 +342,10 @@ def tile_essattn_pa_kernel(tc, x, wk, bk, wv, bv, out_0, out_1):
             )
 
         def WGV(i, g):
-            regroup(nc.vector.tensor_copy, i, g, slice(0, VECTOR_COLS[i]))
+            regroup(nc.vector.tensor_copy, i, g, slice(0, min(BANK, VECTOR_COLS[i])))
+
+        def WGW(i, g):
+            regroup(nc.vector.tensor_copy, i, g, slice(BANK, VECTOR_COLS[i]))
 
         def WGS(i, g):
             regroup(nc.scalar.copy, i, g, slice(VECTOR_COLS[i], E))
@@ -365,43 +368,43 @@ def tile_essattn_pa_kernel(tc, x, wk, bk, wv, bv, out_0, out_1):
             XT(0, 0)
             XC(0, 0)
             XT(0, 1)
-            XQ(0, 0)
-            LWH(0, 0, 1)
-            WGS(0, 0)
             XC(0, 1)
+            LWH(0, 0, 1)
+            WGW(0, 0)
+            WGS(0, 0)
+            XQ(0, 0)
             LB(0)
             BM(0)
+            BC(0)
             LB(1)
             BM(1)
+            BC(1)
             LWH(0, 1, 0)
             WGV(0, 1)
             XQ(0, 1)
             WQ(0, 1, 0)
-            WQ(0, 0, 1)
             LWH(0, 1, 1)
             WGS(0, 1)
+            WGW(0, 1)
+            WQ(0, 0, 1)
             WQ(0, 1, 1)
             LX(0, 1)
             XT(0, 2)
-            XC(0, 2)
             XT(0, 3)
-            BC(0)
             KP(0, 0)
-            BC(1)
-            XQ(0, 2)
+            XC(0, 2)
             KP(0, 1)
             XC(0, 3)
+            XQ(0, 2)
             KP(0, 2)
-            LW(1, 0)
-            WGV(1, 0)
-            KE(0, 0)
-            KTG(0, 0)
-            WGS(1, 0)
             XQ(0, 3)
+            KE(0, 0)
+            LW(1, 0)
+            WGS(1, 0)
+            WGV(1, 0)
             KE(0, 1)
-            KTG(0, 1)
             KE(0, 2)
-            KTG(0, 2)
+            KT2(0, 0)
             LW(1, 1)
             WGV(1, 1)
             LX(1, 0)
@@ -411,118 +414,114 @@ def tile_essattn_pa_kernel(tc, x, wk, bk, wv, bv, out_0, out_1):
             KG(0, 0)
             KP(0, 3)
             XC(1, 1)
-            XQ(1, 0)
             WGS(1, 1)
-            WQF(1, 0)
+            XQ(1, 0)
             KG(0, 1)
             KE(0, 3)
-            KTG(0, 3)
+            WQF(1, 0)
+            KT2(0, 1)
             XQ(1, 1)
-            KDG(0, 0)
             LX(1, 1)
             XT(1, 2)
             XT(1, 3)
             KP(1, 0)
             XC(1, 2)
             KP(1, 1)
-            KE(1, 0)
             XC(1, 3)
+            KG(0, 2)
+            KE(1, 0)
+            KG(0, 3)
             WQF(1, 1)
             VP(0, 0)
-            KG(0, 2)
-            KR2(0, 0)
             VP(0, 1)
+            KI2(0, 0)
             KE(1, 1)
-            KG(0, 3)
+            KR2(0, 0)
+            KSG(0, 0)
+            KSG(0, 1)
+            KH(0, 0)
             XQ2(1, 1)
         rows = ctx.enter_context(tc.tile_pool(name="rows", bufs=ROWS))
         KP(1, 2)
-        KH(0, 0)
-        KS(0, 0)
-        KS(0, 1)
+        KT2(1, 0)
+        KG(1, 0)
+        KH(0, 1)
+        KG(1, 1)
         VF(0, 0, 0)
         VF(0, 0, 1)
         VP(0, 2)
-        KTG(1, 0)
-        KG(1, 0)
-        KH(0, 1)
-        KTG(1, 1)
-        KG(1, 1)
-        KDG(0, 1)
-        KR2(0, 1)
-        KH(0, 2)
+        KI2(0, 1)
         VF(0, 1, 0)
         VF(0, 1, 1)
         KP(1, 3)
+        KR2(0, 1)
+        KSG(0, 2)
+        KH(0, 2)
         KH(0, 3)
         KE(1, 2)
         VP(0, 3)
-        KS(0, 2)
+        KA(0, 1)
         VF(0, 2, 0)
         VF(0, 2, 1)
-        KE(1, 3)
-        VF(0, 3, 0)
-        VF(0, 3, 1)
-        KS(0, 3)
-        KA(0, 1)
-        KN(0, 1, 1, 0)
         VP(1, 0)
-        KTG(1, 2)
-        KG(1, 2)
-        KA(0, 3)
-        KN(0, 3, 0, 1)
+        KN(0, 1, 1, 0)
+        KE(1, 3)
         VP(1, 1)
-        VP(1, 2)
-        KTG(1, 3)
+        VF(0, 3, 0)
+        KT2(1, 1)
+        KG(1, 2)
         KG(1, 3)
-        KDG(1, 0)
-        KR2(1, 0)
-        KH(1, 0)
-        NR(0, 0)
-        NR(0, 1)
-        KH(1, 1)
+        VF(0, 3, 1)
         VRS(0, 1)
+        KI2(1, 0)
         VF(1, 0, 0)
         VF(1, 0, 1)
-        VP(1, 3)
-        KN(1, 0, 1, 0)
-        KN(1, 1, 0, 0)
+        KR2(1, 0)
+        KH(1, 0)
         VR(0, 0)
         VF(1, 1, 0)
         VF(1, 1, 1)
-        KS(1, 0)
+        KSG(0, 3)
+        KI2(1, 1)
         VQ(0, 0)
+        KR2(1, 1)
+        VQ(0, 1)
+        KA(0, 3)
+        KN(0, 3, 0, 1)
+        VP(1, 2)
+        VP(1, 3)
+        NR(0, 0)
+        NR(0, 1)
+        KN(1, 0, 1, 0)
+        KH(1, 1)
+        KH(1, 2)
+        KH(1, 3)
+        M2(0, 0)
         VF(1, 2, 0)
         VF(1, 2, 1)
-        KDG(1, 1)
-        KR2(1, 1)
-        KH(1, 2)
-        KN(1, 2, 0, 0)
-        KH(1, 3)
-        KS(1, 1)
-        VF(1, 3, 0)
-        VF(1, 3, 1)
-        M2(0, 0)
-        M2(0, 1)
         Q2(0, 0)
         KV(0, 0, 0)
-        O(0, 0, 0)
-        VQ(0, 1)
         KV(0, 0, 1)
         KV(0, 1, 0)
         KV(0, 1, 1)
+        KN(1, 1, 0, 0)
+        O(0, 0, 0)
         O(0, 0, 1)
         ST(0, 0)
         O(0, 1, 0)
         O(0, 1, 1)
         ST(0, 1)
+        M2(0, 1)
+        VF(1, 3, 0)
+        VF(1, 3, 1)
+        KS(1, 1)
         Q2(0, 1)
         KV(0, 2, 0)
         KV(0, 2, 1)
         KV(0, 3, 0)
         KV(0, 3, 1)
+        KN(1, 2, 0, 0)
         O(0, 2, 0)
-        KN(1, 3, 0, 1)
         O(0, 2, 1)
         ST(0, 2)
         O(0, 3, 0)
@@ -535,8 +534,9 @@ def tile_essattn_pa_kernel(tc, x, wk, bk, wv, bv, out_0, out_1):
         KV(0, 4, 0)
         KV(0, 4, 1)
         KV(0, 5, 0)
-        O(0, 4, 0)
         KV(0, 5, 1)
+        O(0, 4, 0)
+        KN(1, 3, 0, 1)
         O(0, 4, 1)
         ST(0, 4)
         O(0, 5, 0)
@@ -544,8 +544,9 @@ def tile_essattn_pa_kernel(tc, x, wk, bk, wv, bv, out_0, out_1):
         ST(0, 5)
         NR(1, 0)
         NR(1, 1)
-        M2(0, 3)
         VR(1, 0)
+        M2(0, 3)
+        VR(1, 1)
         Q2(0, 3)
         KV(0, 6, 0)
         KV(0, 6, 1)
@@ -555,11 +556,11 @@ def tile_essattn_pa_kernel(tc, x, wk, bk, wv, bv, out_0, out_1):
         O(0, 6, 1)
         ST(0, 6)
         O(0, 7, 0)
-        VR(1, 1)
         O(0, 7, 1)
         ST(0, 7)
         VQ(1, 0)
         VQ(1, 1)
+        KSG(1, 0)
         M2(1, 0)
         M2(1, 1)
         Q2(1, 0)
@@ -579,10 +580,10 @@ def tile_essattn_pa_kernel(tc, x, wk, bk, wv, bv, out_0, out_1):
         KV(1, 3, 1)
         O(1, 2, 0)
         O(1, 2, 1)
+        O(1, 3, 0)
         OV(1, 1, 1)
         ST(1, 1)
         ST(1, 2)
-        O(1, 3, 0)
         M2(1, 3)
         Q2(1, 2)
         KV(1, 4, 0)
@@ -593,9 +594,9 @@ def tile_essattn_pa_kernel(tc, x, wk, bk, wv, bv, out_0, out_1):
         O(1, 5, 0)
         OV(1, 3, 1)
         ST(1, 3)
+        O(1, 5, 1)
         Q2(1, 3)
         KV(1, 6, 0)
-        O(1, 5, 1)
         KV(1, 6, 1)
         OV(1, 4, 1)
         ST(1, 4)

@@ -167,6 +167,10 @@ def tile_essattn_pa_kernel(tc, x, wk, bk, wv, bv, out_0, out_1):
                 out=inv_norms[b][:, h * BANK : (h + 1) * BANK], in_=sum_banks[b][h][:], func=ACT.Abs_reciprocal_sqrt
             )
 
+        def NB(b, h):
+            half = inv_norms[b][:, h * BANK : (h + 1) * BANK]
+            nc.vector.tensor_scalar_min(out=half, in0=half, scalar1=1.0 / EPS_NORM)
+
         v_grp = {}
         v_quant = {}
 
@@ -183,7 +187,10 @@ def tile_essattn_pa_kernel(tc, x, wk, bk, wv, bv, out_0, out_1):
             cols = slice(h * BANK, (h + 1) * BANK)
             if b not in v_grp:
                 v_grp[b] = rows.tile([P, E, PACK], BF16, align_bytes=64, name="v_grp", bufs=1)
-            (copy or nc.vector.tensor_copy)(out=v_grp[b][:, cols, :], in_=v_all[b][:, :, cols].rearrange("p t e -> p e t"))
+            (copy or nc.vector.tensor_copy)(
+                out=v_grp[b][:, cols, :].rearrange("p (c i) t -> p c t i", i=4),
+                in_=v_all[b][:, :, cols].rearrange("p t (c i) -> p c t i", i=4),
+            )
 
         def VRS(b, h):
             VR(b, h, nc.scalar.copy)
@@ -207,9 +214,11 @@ def tile_essattn_pa_kernel(tc, x, wk, bk, wv, bv, out_0, out_1):
         def M2(b, q):
             cols = slice(2 * q * P, 2 * (q + 1) * P)
             k2_grp = work.tile([P, 2 * P, PACK], BF16, align_bytes=64, name="k2_grp", bufs=2)
-            nc.vector.scalar_tensor_tensor(
-                out=k2_grp[:], in0=inv_norms[b][:, cols].unsqueeze(2).to_broadcast([P, 2 * P, PACK]), scalar=1.0 / EPS_NORM,
-                in1=g_all[b][:, :, cols].rearrange("p t e -> p e t"), op0=ALU.min, op1=ALU.mult,
+            nc.vector.tensor_tensor(
+                out=k2_grp[:].rearrange("p (c i) t -> p c t i", i=4),
+                in0=g_all[b][:, :, cols].rearrange("p t (c i) -> p c t i", i=4),
+                in1=inv_norms[b][:, cols].rearrange("p (c i) -> p c i", i=4).unsqueeze(2).to_broadcast([P, P // 2, PACK, 4]),
+                op=ALU.mult,
             )
             k2_grps[b, q] = k2_grp
 
@@ -384,8 +393,8 @@ def tile_essattn_pa_kernel(tc, x, wk, bk, wv, bv, out_0, out_1):
             XQ(0, 1)
             WQ(0, 1, 0)
             LWH(0, 1, 1)
-            WGS(0, 1)
             WGW(0, 1)
+            WGS(0, 1)
             WQ(0, 0, 1)
             WQ(0, 1, 1)
             LX(0, 1)
@@ -394,10 +403,10 @@ def tile_essattn_pa_kernel(tc, x, wk, bk, wv, bv, out_0, out_1):
             KP(0, 0)
             XC(0, 2)
             KP(0, 1)
-            XC(0, 3)
             XQ(0, 2)
-            KP(0, 2)
+            XC(0, 3)
             XQ(0, 3)
+            KP(0, 2)
             KE(0, 0)
             LW(1, 0)
             WGS(1, 0)
@@ -428,12 +437,12 @@ def tile_essattn_pa_kernel(tc, x, wk, bk, wv, bv, out_0, out_1):
             XC(1, 2)
             KP(1, 1)
             XC(1, 3)
-            KG(0, 2)
             KE(1, 0)
-            KG(0, 3)
+            KG(0, 2)
             WQF(1, 1)
             VP(0, 0)
             VP(0, 1)
+            KG(0, 3)
             KI2(0, 0)
             KE(1, 1)
             KR2(0, 0)
@@ -446,8 +455,8 @@ def tile_essattn_pa_kernel(tc, x, wk, bk, wv, bv, out_0, out_1):
         KT2(1, 0)
         KG(1, 0)
         KH(0, 1)
-        KG(1, 1)
         VF(0, 0, 0)
+        KG(1, 1)
         VF(0, 0, 1)
         VP(0, 2)
         KI2(0, 1)
@@ -460,10 +469,10 @@ def tile_essattn_pa_kernel(tc, x, wk, bk, wv, bv, out_0, out_1):
         KH(0, 3)
         KE(1, 2)
         VP(0, 3)
-        KA(0, 1)
         VF(0, 2, 0)
         VF(0, 2, 1)
         VP(1, 0)
+        KA(0, 1)
         KN(0, 1, 1, 0)
         KE(1, 3)
         VP(1, 1)
@@ -481,9 +490,9 @@ def tile_essattn_pa_kernel(tc, x, wk, bk, wv, bv, out_0, out_1):
         VR(0, 0)
         VF(1, 1, 0)
         VF(1, 1, 1)
-        KSG(0, 3)
         KI2(1, 1)
         VQ(0, 0)
+        KSG(0, 3)
         KR2(1, 1)
         VQ(0, 1)
         KA(0, 3)
@@ -496,6 +505,8 @@ def tile_essattn_pa_kernel(tc, x, wk, bk, wv, bv, out_0, out_1):
         KH(1, 1)
         KH(1, 2)
         KH(1, 3)
+        NB(0, 0)
+        NB(0, 1)
         M2(0, 0)
         VF(1, 2, 0)
         VF(1, 2, 1)
@@ -560,6 +571,8 @@ def tile_essattn_pa_kernel(tc, x, wk, bk, wv, bv, out_0, out_1):
         ST(0, 7)
         VQ(1, 0)
         VQ(1, 1)
+        NB(1, 0)
+        NB(1, 1)
         KSG(1, 0)
         M2(1, 0)
         M2(1, 1)

@@ -19,7 +19,7 @@ PASSES = C // (P * PACK)
 BANK = 512
 HALVES = E // BANK
 CHUNKS = E // P
-VECTOR_COLS = (768, 256)
+VECTOR_COLS = ((768, 768), (0, 256))
 FEATS = 6
 SQS = 5
 ROWS = 8
@@ -85,6 +85,8 @@ def tile_essattn_pa_kernel(tc, x, wk, bk, wv, bv, out_0, out_1):
             nc.vector.memset(pair[:], E * E * EPS_SUM)
         totals = {}
         inv_sums = {}
+        inv_pairs = {}
+        late_invs = {}
         dens = {}
         squares = {}
         sum_banks = {}
@@ -128,6 +130,7 @@ def tile_essattn_pa_kernel(tc, x, wk, bk, wv, bv, out_0, out_1):
         def KR2(b, p):
             inv = small.tile([P, 2], F32, name="inv_sum", bufs=4)
             nc.vector.reciprocal(out=inv[:], in_=dens[b, p][:])
+            inv_pairs[b, p] = inv
             for i in range(2):
                 inv_sums[b, 2 * p + i] = inv[:, i : i + 1]
 
@@ -137,8 +140,17 @@ def tile_essattn_pa_kernel(tc, x, wk, bk, wv, bv, out_0, out_1):
                 op0=ALU.mult, op1=ALU.add,
             )
 
+        def GATE(b, p):
+            late = small.tile([P, 2], F32, name="late_inv")
+            nc.vector.tensor_copy(out=late[:], in_=inv_pairs[b, p][:])
+            for i in range(2):
+                late_invs[b, 2 * p + i] = late[:, i : i + 1]
+
         def KSG(b, t):
-            KS(b, t, nc.gpsimd)
+            nc.gpsimd.tensor_scalar(
+                out=g_all[b][:, t, :], in0=feats[b, t][:], scalar1=late_invs.get((b, t), inv_sums[b, t]), scalar2=0.0,
+                op0=ALU.mult, op1=ALU.add,
+            )
 
         def KH(b, t):
             g_sq = work.tile([P, E], F32, name="g_sq", bufs=SQS)
@@ -351,13 +363,13 @@ def tile_essattn_pa_kernel(tc, x, wk, bk, wv, bv, out_0, out_1):
             )
 
         def WGV(i, g):
-            regroup(nc.vector.tensor_copy, i, g, slice(0, min(BANK, VECTOR_COLS[i])))
+            regroup(nc.vector.tensor_copy, i, g, slice(0, min(BANK, VECTOR_COLS[i][g])))
 
         def WGW(i, g):
-            regroup(nc.vector.tensor_copy, i, g, slice(BANK, VECTOR_COLS[i]))
+            regroup(nc.vector.tensor_copy, i, g, slice(BANK, VECTOR_COLS[i][g]))
 
         def WGS(i, g):
-            regroup(nc.scalar.copy, i, g, slice(VECTOR_COLS[i], E))
+            regroup(nc.scalar.copy, i, g, slice(VECTOR_COLS[i][g], E))
 
         def WQ(i, g, h):
             cols = slice(h * BANK, (h + 1) * BANK)
@@ -408,12 +420,11 @@ def tile_essattn_pa_kernel(tc, x, wk, bk, wv, bv, out_0, out_1):
             XQ(0, 3)
             KP(0, 2)
             KE(0, 0)
-            LW(1, 0)
-            WGS(1, 0)
-            WGV(1, 0)
             KE(0, 1)
             KE(0, 2)
             KT2(0, 0)
+            LW(1, 0)
+            WGS(1, 0)
             LW(1, 1)
             WGV(1, 1)
             LX(1, 0)
@@ -423,10 +434,10 @@ def tile_essattn_pa_kernel(tc, x, wk, bk, wv, bv, out_0, out_1):
             KG(0, 0)
             KP(0, 3)
             XC(1, 1)
-            WGS(1, 1)
             XQ(1, 0)
-            KG(0, 1)
+            WGS(1, 1)
             KE(0, 3)
+            KG(0, 1)
             WQF(1, 0)
             KT2(0, 1)
             XQ(1, 1)
@@ -442,8 +453,8 @@ def tile_essattn_pa_kernel(tc, x, wk, bk, wv, bv, out_0, out_1):
             WQF(1, 1)
             VP(0, 0)
             VP(0, 1)
-            KG(0, 3)
             KI2(0, 0)
+            KG(0, 3)
             KE(1, 1)
             KR2(0, 0)
             KSG(0, 0)
@@ -456,9 +467,9 @@ def tile_essattn_pa_kernel(tc, x, wk, bk, wv, bv, out_0, out_1):
         KG(1, 0)
         KH(0, 1)
         VF(0, 0, 0)
-        KG(1, 1)
         VF(0, 0, 1)
         VP(0, 2)
+        KG(1, 1)
         KI2(0, 1)
         VF(0, 1, 0)
         VF(0, 1, 1)
@@ -467,15 +478,15 @@ def tile_essattn_pa_kernel(tc, x, wk, bk, wv, bv, out_0, out_1):
         KSG(0, 2)
         KH(0, 2)
         KH(0, 3)
+        KA(0, 1)
         KE(1, 2)
         VP(0, 3)
         VF(0, 2, 0)
         VF(0, 2, 1)
         VP(1, 0)
-        KA(0, 1)
-        KN(0, 1, 1, 0)
         KE(1, 3)
         VP(1, 1)
+        KN(0, 1, 1, 0)
         VF(0, 3, 0)
         KT2(1, 1)
         KG(1, 2)
@@ -485,14 +496,14 @@ def tile_essattn_pa_kernel(tc, x, wk, bk, wv, bv, out_0, out_1):
         KI2(1, 0)
         VF(1, 0, 0)
         VF(1, 0, 1)
+        KSG(0, 3)
         KR2(1, 0)
         KH(1, 0)
-        VR(0, 0)
         VF(1, 1, 0)
         VF(1, 1, 1)
         KI2(1, 1)
+        VR(0, 0)
         VQ(0, 0)
-        KSG(0, 3)
         KR2(1, 1)
         VQ(0, 1)
         KA(0, 3)
@@ -508,24 +519,24 @@ def tile_essattn_pa_kernel(tc, x, wk, bk, wv, bv, out_0, out_1):
         NB(0, 0)
         NB(0, 1)
         M2(0, 0)
-        VF(1, 2, 0)
-        VF(1, 2, 1)
+        M2(0, 1)
         Q2(0, 0)
         KV(0, 0, 0)
         KV(0, 0, 1)
-        KV(0, 1, 0)
-        KV(0, 1, 1)
-        KN(1, 1, 0, 0)
         O(0, 0, 0)
+        KV(0, 1, 0)
         O(0, 0, 1)
         ST(0, 0)
+        KV(0, 1, 1)
+        KN(1, 1, 0, 0)
         O(0, 1, 0)
         O(0, 1, 1)
         ST(0, 1)
-        M2(0, 1)
+        GATE(1, 0)
+        VF(1, 2, 0)
+        VF(1, 2, 1)
         VF(1, 3, 0)
         VF(1, 3, 1)
-        KS(1, 1)
         Q2(0, 1)
         KV(0, 2, 0)
         KV(0, 2, 1)
@@ -541,6 +552,7 @@ def tile_essattn_pa_kernel(tc, x, wk, bk, wv, bv, out_0, out_1):
         KS(1, 2)
         M2(0, 2)
         KS(1, 3)
+        KSG(1, 0)
         Q2(0, 2)
         KV(0, 4, 0)
         KV(0, 4, 1)
@@ -573,7 +585,7 @@ def tile_essattn_pa_kernel(tc, x, wk, bk, wv, bv, out_0, out_1):
         VQ(1, 1)
         NB(1, 0)
         NB(1, 1)
-        KSG(1, 0)
+        KSG(1, 1)
         M2(1, 0)
         M2(1, 1)
         Q2(1, 0)

@@ -19,7 +19,7 @@ PASSES = C // (P * PACK)
 BANK = 512
 HALVES = E // BANK
 CHUNKS = E // P
-VECTOR_COLS = ((768, 768), (0, 256))
+VECTOR_COLS = ((768, 768), (0, 512))
 FEATS = 6
 SQS = 5
 ROWS = 8
@@ -198,7 +198,7 @@ def tile_essattn_pa_kernel(tc, x, wk, bk, wv, bv, out_0, out_1):
         def VR(b, h, copy=None):
             cols = slice(h * BANK, (h + 1) * BANK)
             if b not in v_grp:
-                v_grp[b] = rows.tile([P, E, PACK], BF16, align_bytes=64, name="v_grp", bufs=1)
+                v_grp[b] = rows.tile([P, E, PACK], BF16, align_bytes=64, name="v_grp", bufs=2)
             (copy or nc.vector.tensor_copy)(
                 out=v_grp[b][:, cols, :].rearrange("p (c i) t -> p c t i", i=4),
                 in_=v_all[b][:, :, cols].rearrange("p t (c i) -> p c t i", i=4),
@@ -415,8 +415,8 @@ def tile_essattn_pa_kernel(tc, x, wk, bk, wv, bv, out_0, out_1):
             KP(0, 0)
             XC(0, 2)
             KP(0, 1)
-            XQ(0, 2)
             XC(0, 3)
+            XQ(0, 2)
             XQ(0, 3)
             KP(0, 2)
             KE(0, 0)
@@ -434,8 +434,8 @@ def tile_essattn_pa_kernel(tc, x, wk, bk, wv, bv, out_0, out_1):
             KG(0, 0)
             KP(0, 3)
             XC(1, 1)
-            XQ(1, 0)
             WGS(1, 1)
+            XQ(1, 0)
             KE(0, 3)
             KG(0, 1)
             WQF(1, 0)
@@ -452,8 +452,8 @@ def tile_essattn_pa_kernel(tc, x, wk, bk, wv, bv, out_0, out_1):
             KG(0, 2)
             WQF(1, 1)
             VP(0, 0)
-            VP(0, 1)
             KI2(0, 0)
+            VP(0, 1)
             KG(0, 3)
             KE(1, 1)
             KR2(0, 0)
@@ -467,9 +467,9 @@ def tile_essattn_pa_kernel(tc, x, wk, bk, wv, bv, out_0, out_1):
         KG(1, 0)
         KH(0, 1)
         VF(0, 0, 0)
+        KG(1, 1)
         VF(0, 0, 1)
         VP(0, 2)
-        KG(1, 1)
         KI2(0, 1)
         VF(0, 1, 0)
         VF(0, 1, 1)
@@ -478,7 +478,6 @@ def tile_essattn_pa_kernel(tc, x, wk, bk, wv, bv, out_0, out_1):
         KSG(0, 2)
         KH(0, 2)
         KH(0, 3)
-        KA(0, 1)
         KE(1, 2)
         VP(0, 3)
         VF(0, 2, 0)
@@ -486,90 +485,92 @@ def tile_essattn_pa_kernel(tc, x, wk, bk, wv, bv, out_0, out_1):
         VP(1, 0)
         KE(1, 3)
         VP(1, 1)
-        KN(0, 1, 1, 0)
+        KA(0, 1)
+        KI2(1, 0)
         VF(0, 3, 0)
         KT2(1, 1)
+        KR2(1, 0)
+        KH(1, 0)
+        KH(1, 1)
         KG(1, 2)
         KG(1, 3)
         VF(0, 3, 1)
+        VP(1, 2)
         VRS(0, 1)
-        KI2(1, 0)
         VF(1, 0, 0)
         VF(1, 0, 1)
-        KSG(0, 3)
-        KR2(1, 0)
-        KH(1, 0)
+        VP(1, 3)
+        KN(0, 1, 1, 0)
         VF(1, 1, 0)
         VF(1, 1, 1)
+        VF(1, 2, 0)
+        VF(1, 2, 1)
+        VF(1, 3, 0)
+        KSG(0, 3)
+        VF(1, 3, 1)
         KI2(1, 1)
         VR(0, 0)
-        VQ(0, 0)
         KR2(1, 1)
+        VQ(0, 0)
         VQ(0, 1)
         KA(0, 3)
         KN(0, 3, 0, 1)
-        VP(1, 2)
-        VP(1, 3)
         NR(0, 0)
         NR(0, 1)
-        KN(1, 0, 1, 0)
-        KH(1, 1)
         KH(1, 2)
         KH(1, 3)
+        VRS(1, 1)
         NB(0, 0)
         NB(0, 1)
         M2(0, 0)
         M2(0, 1)
         Q2(0, 0)
-        KV(0, 0, 0)
-        KV(0, 0, 1)
-        O(0, 0, 0)
-        KV(0, 1, 0)
-        O(0, 0, 1)
-        ST(0, 0)
-        KV(0, 1, 1)
-        KN(1, 1, 0, 0)
-        O(0, 1, 0)
-        O(0, 1, 1)
-        ST(0, 1)
-        GATE(1, 0)
-        VF(1, 2, 0)
-        VF(1, 2, 1)
-        VF(1, 3, 0)
-        VF(1, 3, 1)
+        KS(1, 0)
         Q2(0, 1)
-        KV(0, 2, 0)
-        KV(0, 2, 1)
-        KV(0, 3, 0)
-        KV(0, 3, 1)
-        KN(1, 2, 0, 0)
-        O(0, 2, 0)
-        O(0, 2, 1)
-        ST(0, 2)
-        O(0, 3, 0)
-        O(0, 3, 1)
-        ST(0, 3)
+        KS(1, 1)
         KS(1, 2)
+        VR(1, 0)
         M2(0, 2)
         KS(1, 3)
-        KSG(1, 0)
         Q2(0, 2)
+        M2(0, 3)
+        VQ(1, 0)
+        KA(1, 1)
+        KN(1, 1, 1, 0)
+        KN(1, 2, 0, 0)
+        KV(0, 0, 0)
+        KV(0, 0, 1)
+        KV(0, 1, 0)
+        KV(0, 1, 1)
+        KV(0, 2, 0)
+        O(0, 0, 0)
+        KV(0, 2, 1)
+        O(0, 0, 1)
+        ST(0, 0)
+        KV(0, 3, 0)
+        O(0, 1, 0)
+        KV(0, 3, 1)
+        O(0, 1, 1)
+        ST(0, 1)
+        KN(1, 3, 0, 1)
+        O(0, 2, 0)
         KV(0, 4, 0)
+        O(0, 2, 1)
+        ST(0, 2)
         KV(0, 4, 1)
+        O(0, 3, 0)
         KV(0, 5, 0)
+        O(0, 3, 1)
+        ST(0, 3)
         KV(0, 5, 1)
         O(0, 4, 0)
-        KN(1, 3, 0, 1)
         O(0, 4, 1)
         ST(0, 4)
+        NR(1, 0)
+        NR(1, 1)
         O(0, 5, 0)
         O(0, 5, 1)
         ST(0, 5)
-        NR(1, 0)
-        NR(1, 1)
-        VR(1, 0)
-        M2(0, 3)
-        VR(1, 1)
         Q2(0, 3)
         KV(0, 6, 0)
         KV(0, 6, 1)
@@ -581,11 +582,9 @@ def tile_essattn_pa_kernel(tc, x, wk, bk, wv, bv, out_0, out_1):
         O(0, 7, 0)
         O(0, 7, 1)
         ST(0, 7)
-        VQ(1, 0)
         VQ(1, 1)
         NB(1, 0)
         NB(1, 1)
-        KSG(1, 1)
         M2(1, 0)
         M2(1, 1)
         Q2(1, 0)
@@ -614,8 +613,8 @@ def tile_essattn_pa_kernel(tc, x, wk, bk, wv, bv, out_0, out_1):
         KV(1, 4, 0)
         KV(1, 4, 1)
         KV(1, 5, 0)
-        O(1, 4, 0)
         KV(1, 5, 1)
+        O(1, 4, 0)
         O(1, 5, 0)
         OV(1, 3, 1)
         ST(1, 3)
@@ -626,12 +625,12 @@ def tile_essattn_pa_kernel(tc, x, wk, bk, wv, bv, out_0, out_1):
         OV(1, 4, 1)
         ST(1, 4)
         ST(1, 5)
-        O(1, 6, 0)
         KV(1, 7, 0)
+        O(1, 6, 0)
         OV(1, 6, 1)
         ST(1, 6)
+        KV(1, 7, 1)
         O(1, 7, 0)
         STH(1, 7, 0)
-        KV(1, 7, 1)
         OV(1, 7, 1)
         STH(1, 7, 1)

@@ -10,6 +10,7 @@ U8 = mybir.dt.uint8
 FP8X4 = mybir.dt.float8_e4m3fn_x4
 ALU = mybir.AluOpType
 ACT = mybir.ActivationFunctionType
+AXIS_X = mybir.AxisListType.X
 
 P = 128
 PACK = 4
@@ -18,15 +19,19 @@ T = N // P
 PASSES = C // (P * PACK)
 BANK = 512
 HALVES = E // BANK
-CHUNKS = E // P
-VECTOR_COLS = ((768, 768), (0, 512))
-FEATS = 6
-SQS = 5
-ROWS = 8
+PAIR = 2 * P
+LINE = 4
 EPS_SUM = 1e-7
 EPS_NORM = 1e-12
+KEYS, VALUES = 0, 1
+WK_VECTOR = 768
+WV_VECTOR = 512
 
 FLOPS = 2 * (2 * B * N * C * E) + 2 * B * N * E * E
+
+
+def half(h):
+    return slice(h * BANK, (h + 1) * BANK)
 
 
 def tile_essattn_pa_kernel(tc, x, wk, bk, wv, bv, out_0, out_1):
@@ -51,586 +56,421 @@ def tile_essattn_pa_kernel(tc, x, wk, bk, wv, bv, out_0, out_1):
         bias_rows = const.tile([P, 2, E], BF16)
         nc.gpsimd.memset(bias_rows[:], 0.0)
         bias_all = const.tile([P, 2, E], BF16)
+        f_sums = {(b, p): const.tile([P, 2, 2], F32, name="f_sums%d%d" % (b, p)) for b in range(B) for p in range(2)}
+        for pair_sums in f_sums.values():
+            nc.vector.memset(pair_sums[:], E * E * EPS_SUM)
 
         x_codes = keep.tile([P, B * T, PASSES * P], U32, align_bytes=64)
         x_scales = keep.tile([P, B * T, PASSES * P], U8, align_bytes=64)
-        w_codes = [keep.tile([P, PASSES, E], U32, align_bytes=64, name="w_codes%d" % i) for i in range(2)]
-        w_scales = [keep.tile([P, PASSES, E], U8, align_bytes=64, name="w_scales%d" % i) for i in range(2)]
+        w_codes = [keep.tile([P, PASSES, E], U32, align_bytes=64, name="w_codes%d" % i) for i in (KEYS, VALUES)]
+        w_scales = [keep.tile([P, PASSES, E], U8, align_bytes=64, name="w_scales%d" % i) for i in (KEYS, VALUES)]
         g_all = [keep.tile([P, T, E], F32, name="g_all%d" % b) for b in range(B)]
         v_all = [keep.tile([P, T, E], F32, name="v_all%d" % b) for b in range(B)]
 
-        def project(weight, tile_index):
+        def project(weight, b, t):
             banks = []
             for h in range(HALVES):
-                cols = slice(h * BANK, (h + 1) * BANK)
                 bank = psum.tile([P, BANK], F32, name="bank")
                 for g in range(PASSES):
                     toks = slice(g * P, (g + 1) * P)
                     nc.tensor.matmul_mx(
                         out=bank[:],
-                        lhsT=x_codes[:, tile_index, toks].bitcast(FP8X4),
-                        lhsT_scale=x_scales[:, tile_index, toks],
-                        rhs=w_codes[weight][:, g, cols].bitcast(FP8X4),
-                        rhs_scale=w_scales[weight][:, g, cols],
+                        lhsT=x_codes[:, b * T + t, toks].bitcast(FP8X4),
+                        lhsT_scale=x_scales[:, b * T + t, toks],
+                        rhs=w_codes[weight][:, g, half(h)].bitcast(FP8X4),
+                        rhs_scale=w_scales[weight][:, g, half(h)],
                         start=(g == 0),
                         stop=(g == PASSES - 1),
                     )
                 banks.append(bank)
             return banks
 
-        feats = {}
-        row_pairs = {}
-        f_pairs = {(b, p): const.tile([P, 2, 2], F32, name="f_pair%d%d" % (b, p)) for b in range(B) for p in range(2)}
-        for pair in f_pairs.values():
-            nc.vector.memset(pair[:], E * E * EPS_SUM)
-        totals = {}
-        inv_sums = {}
-        inv_pairs = {}
-        late_invs = {}
-        dens = {}
-        squares = {}
-        sum_banks = {}
-        inv_norms = {}
-        k_banks = {}
-        v_banks = {}
+        k_banks, feats, row_sums, totals, inv_sums, squares = {}, {}, {}, {}, {}, {}
+        sum_banks, inv_norms = {}, {}
 
-        def KP(b, t):
-            k_banks[b, t] = project(0, b * T + t)
+        def project_keys(b, t):
+            k_banks[b, t] = project(KEYS, b, t)
 
-        def KE(b, t):
+        def add_key_bias(b, t):
             if t % 2 == 0:
-                row_pairs[b, t // 2] = small.tile([P, 2, HALVES], F32, name="row_pair")
-            row_sum = row_pairs[b, t // 2]
-            feat = work.tile([P, E], F32, name="feat", bufs=FEATS)
+                row_sums[b, t // 2] = small.tile([P, 2, HALVES], F32, name="row_sums")
+            feats[b, t] = work.tile([P, E], F32, name="feats", bufs=6)
             for h in range(HALVES):
-                cols = slice(h * BANK, (h + 1) * BANK)
                 nc.vector.scalar_tensor_tensor(
-                    out=feat[:, cols], in0=k_banks[b, t][h][:], scalar=1.0, in1=bias_all[:, 0, cols],
-                    op0=ALU.mult, op1=ALU.add, accum_out=row_sum[:, t % 2, h : h + 1],
+                    out=feats[b, t][:, half(h)], in0=k_banks[b, t][h][:], scalar=1.0, in1=bias_all[:, KEYS, half(h)],
+                    op0=ALU.mult, op1=ALU.add, accum_out=row_sums[b, t // 2][:, t % 2, h : h + 1],
                 )
-            feats[b, t] = feat
 
-        def KT2(b, p):
-            total = small.tile([P, 2], F32, name="total2")
-            nc.vector.tensor_reduce(out=total[:], in_=row_pairs[b, p][:], axis=mybir.AxisListType.X, op=ALU.add)
-            for i in range(2):
-                totals[b, 2 * p + i] = total[:, i : i + 1]
+        def total_rows(b, p):
+            totals[b, p] = small.tile([P, 2], F32, name="totals")
+            nc.vector.tensor_reduce(out=totals[b, p][:], in_=row_sums[b, p][:], axis=AXIS_X, op=ALU.add)
 
-        def KI2(b, p):
-            den = small.tile([P, 2], F32, name="den")
-            nc.vector.tensor_reduce(out=den[:], in_=f_pairs[b, p][:], axis=mybir.AxisListType.X, op=ALU.add)
-            dens[b, p] = den
-
-        def KG(b, t):
+        def square_centred(b, t):
             nc.scalar.activation(
-                out=feats[b, t][:], in_=feats[b, t][:], func=ACT.Square, bias=totals[b, t], scale=-float(E),
-                accum_out=f_pairs[b, t // 2][:, t % 2, 0:1],
+                out=feats[b, t][:], in_=feats[b, t][:], func=ACT.Square, bias=totals[b, t // 2][:, t % 2 : t % 2 + 1],
+                scale=-float(E), accum_out=f_sums[b, t // 2][:, t % 2, 0:1],
             )
 
-        def KR2(b, p):
-            inv = small.tile([P, 2], F32, name="inv_sum", bufs=4)
-            nc.vector.reciprocal(out=inv[:], in_=dens[b, p][:])
-            inv_pairs[b, p] = inv
-            for i in range(2):
-                inv_sums[b, 2 * p + i] = inv[:, i : i + 1]
+        def add_eps(b, p):
+            inv_sums[b, p] = small.tile([P, 2], F32, name="inv_sums")
+            nc.vector.tensor_reduce(out=inv_sums[b, p][:], in_=f_sums[b, p][:], axis=AXIS_X, op=ALU.add)
 
-        def KS(b, t, engine=None):
-            (engine or nc.vector).tensor_scalar(
-                out=g_all[b][:, t, :], in0=feats[b, t][:], scalar1=inv_sums[b, t], scalar2=0.0,
+        def invert_sums(b, p):
+            nc.vector.reciprocal(out=inv_sums[b, p][:], in_=inv_sums[b, p][:])
+
+        def inv_sum(b, t):
+            return inv_sums[b, t // 2][:, t % 2 : t % 2 + 1]
+
+        def scale_features(engine, b, t):
+            engine.tensor_scalar(
+                out=g_all[b][:, t, :], in0=feats[b, t][:], scalar1=inv_sum(b, t), scalar2=0.0,
                 op0=ALU.mult, op1=ALU.add,
             )
 
-        def GATE(b, p):
-            late = small.tile([P, 2], F32, name="late_inv")
-            nc.vector.tensor_copy(out=late[:], in_=inv_pairs[b, p][:])
-            for i in range(2):
-                late_invs[b, 2 * p + i] = late[:, i : i + 1]
+        def square_features(b, t):
+            squares[b, t] = work.tile([P, E], F32, name="squares", bufs=5)
+            nc.scalar.activation(out=squares[b, t][:], in_=feats[b, t][:], func=ACT.Square, scale=inv_sum(b, t))
 
-        def KSG(b, t):
-            nc.gpsimd.tensor_scalar(
-                out=g_all[b][:, t, :], in0=feats[b, t][:], scalar1=late_invs.get((b, t), inv_sums[b, t]), scalar2=0.0,
-                op0=ALU.mult, op1=ALU.add,
-            )
-
-        def KH(b, t):
-            g_sq = work.tile([P, E], F32, name="g_sq", bufs=SQS)
-            nc.scalar.activation(out=g_sq[:], in_=feats[b, t][:], func=ACT.Square, scale=inv_sums[b, t])
-            squares[b, t] = g_sq
-
-        def KA(b, t):
+        def add_squares(b, t):
             nc.gpsimd.tensor_tensor(out=squares[b, t][:], in0=squares[b, t - 1][:], in1=squares[b, t][:], op=ALU.add)
 
-        def KAV(b, t):
-            nc.vector.tensor_tensor(out=squares[b, t][:], in0=squares[b, t - 1][:], in1=squares[b, t][:], op=ALU.add)
-
-        def KN(b, t, first, last):
+        def sum_over_tokens(b, t, first, last):
             if first:
-                sum_banks[b] = [psum.tile([P, BANK], F32, name="sums", bufs=2) for h in range(HALVES)]
+                sum_banks[b] = [psum.tile([P, BANK], F32, name="sums", bufs=HALVES) for h in range(HALVES)]
             for h in range(HALVES):
                 nc.tensor.matmul(
-                    out=sum_banks[b][h][:], lhsT=ones_f32[:], rhs=squares[b, t][:, h * BANK : (h + 1) * BANK],
-                    start=bool(first), stop=bool(last),
+                    out=sum_banks[b][h][:], lhsT=ones_f32[:], rhs=squares[b, t][:, half(h)], start=first, stop=last
                 )
 
-        def NR(b, h):
-            if h == 0:
-                inv_norms[b] = stage.tile([P, E], F32, name="inv_norm")
-            nc.scalar.activation(
-                out=inv_norms[b][:, h * BANK : (h + 1) * BANK], in_=sum_banks[b][h][:], func=ACT.Abs_reciprocal_sqrt
+        def invert_norms(b):
+            inv_norms[b] = stage.tile([P, E], F32, name="inv_norm")
+            for h in range(HALVES):
+                nc.scalar.activation(out=inv_norms[b][:, half(h)], in_=sum_banks[b][h][:], func=ACT.Abs_reciprocal_sqrt)
+
+        def bound_norms(b):
+            for h in range(HALVES):
+                nc.vector.tensor_scalar_min(
+                    out=inv_norms[b][:, half(h)], in0=inv_norms[b][:, half(h)], scalar1=1.0 / EPS_NORM
+                )
+
+        v_banks, v_grps, v_quantised = {}, {}, {}
+
+        def project_values(b, t):
+            v_banks[b, t] = project(VALUES, b, t)
+
+        def add_value_bias(b, t, h):
+            nc.vector.tensor_tensor(
+                out=v_all[b][:, t, half(h)], in0=v_banks[b, t][h][:], in1=bias_all[:, VALUES, half(h)], op=ALU.add
             )
-
-        def NB(b, h):
-            half = inv_norms[b][:, h * BANK : (h + 1) * BANK]
-            nc.vector.tensor_scalar_min(out=half, in0=half, scalar1=1.0 / EPS_NORM)
-
-        v_grp = {}
-        v_quant = {}
-
-        def VP(b, t):
-            v_banks[b, t] = project(1, b * T + t)
-
-        def VF(b, t, h):
-            cols = slice(h * BANK, (h + 1) * BANK)
-            nc.vector.tensor_tensor(out=v_all[b][:, t, cols], in0=v_banks[b, t][h][:], in1=bias_all[:, 1, cols], op=ALU.add)
-            if h == 1:
+            if h == HALVES - 1:
                 nc.sync.dma_start(out=out_1[b].rearrange("(p t) e -> p t e", t=T)[:, t, :], in_=v_all[b][:, t, :])
 
-        def VR(b, h, copy=None):
-            cols = slice(h * BANK, (h + 1) * BANK)
-            if b not in v_grp:
-                v_grp[b] = rows.tile([P, E, PACK], BF16, align_bytes=64, name="v_grp", bufs=2)
-            (copy or nc.vector.tensor_copy)(
-                out=v_grp[b][:, cols, :].rearrange("p (c i) t -> p c t i", i=4),
-                in_=v_all[b][:, :, cols].rearrange("p t (c i) -> p c t i", i=4),
+        def regroup_values(copy, b, h):
+            if b not in v_grps:
+                v_grps[b] = rows.tile([P, E, PACK], BF16, align_bytes=64, name="v_grp", bufs=2)
+            copy(
+                out=v_grps[b][:, half(h), :].rearrange("p (c i) t -> p c t i", i=LINE),
+                in_=v_all[b][:, :, half(h)].rearrange("p t (c i) -> p c t i", i=LINE),
             )
 
-        def VRS(b, h):
-            VR(b, h, nc.scalar.copy)
-
-        def VQ(b, h):
-            if h == 0:
+        def quantise_values(b, h):
+            if b not in v_quantised:
                 v_codes = stage.tile([P, E], U32, align_bytes=64, name="v_codes")
                 v_scales = stage.tile([P, E], U8, align_bytes=64, name="v_scales")
-                v_quant[b] = (v_codes, v_scales)
-            cols = slice(h * BANK, (h + 1) * BANK)
+                v_quantised[b] = (v_codes, v_scales)
+            v_codes, v_scales = v_quantised[b]
             nc.vector.quantize_mx(
-                out=v_quant[b][0][:, cols].bitcast(FP8X4), scales=v_quant[b][1][:, cols],
-                in_=v_grp[b][:, cols, :].rearrange("p e t -> p (e t)"),
+                out=v_codes[:, half(h)].bitcast(FP8X4), scales=v_scales[:, half(h)],
+                in_=v_grps[b][:, half(h), :].rearrange("p e t -> p (e t)"),
             )
 
-        k2_grps = {}
-        k2_quant = {}
-        kv_banks = {}
-        kv_rows = {}
+        k2_grps, k2_quantised, kv_banks, kv_rows = {}, {}, {}, {}
 
-        def M2(b, q):
-            cols = slice(2 * q * P, 2 * (q + 1) * P)
-            k2_grp = work.tile([P, 2 * P, PACK], BF16, align_bytes=64, name="k2_grp", bufs=2)
+        def normalise_keys(b, q):
+            cols = slice(q * PAIR, (q + 1) * PAIR)
+            k2_grps[b, q] = work.tile([P, PAIR, PACK], BF16, align_bytes=64, name="k2_grp", bufs=2)
+            lines = [P, PAIR // LINE, PACK, LINE]
             nc.vector.tensor_tensor(
-                out=k2_grp[:].rearrange("p (c i) t -> p c t i", i=4),
-                in0=g_all[b][:, :, cols].rearrange("p t (c i) -> p c t i", i=4),
-                in1=inv_norms[b][:, cols].rearrange("p (c i) -> p c i", i=4).unsqueeze(2).to_broadcast([P, P // 2, PACK, 4]),
+                out=k2_grps[b, q][:].rearrange("p (c i) t -> p c t i", i=LINE),
+                in0=g_all[b][:, :, cols].rearrange("p t (c i) -> p c t i", i=LINE),
+                in1=inv_norms[b][:, cols].rearrange("p (c i) -> p c i", i=LINE).unsqueeze(2).to_broadcast(lines),
                 op=ALU.mult,
             )
-            k2_grps[b, q] = k2_grp
 
-        def Q2(b, q):
-            k2_codes = work.tile([P, 2 * P], U32, align_bytes=64, name="k2_codes")
-            k2_scales = work.tile([P, 2 * P], U8, align_bytes=64, name="k2_scales")
+        def quantise_keys(b, q):
+            k2_codes = work.tile([P, PAIR], U32, align_bytes=64, name="k2_codes")
+            k2_scales = work.tile([P, PAIR], U8, align_bytes=64, name="k2_scales")
             nc.vector.quantize_mx(
                 out=k2_codes[:].bitcast(FP8X4), scales=k2_scales[:], in_=k2_grps[b, q][:].rearrange("p e t -> p (e t)")
             )
-            for i in range(2):
-                rows_of_j = slice(i * P, (i + 1) * P)
-                k2_quant[b, 2 * q + i] = (k2_codes[:, rows_of_j], k2_scales[:, rows_of_j])
+            k2_quantised[b, q] = (k2_codes, k2_scales)
 
-        def KV(b, j, h):
-            v_codes, v_scales = v_quant[b]
-            k2_codes, k2_scales = k2_quant[b, j]
-            cols = slice(h * BANK, (h + 1) * BANK)
-            bank = psum.tile([P, BANK], F32, name="bank")
-            nc.tensor.matmul_mx(
-                out=bank[:], lhsT=k2_codes.bitcast(FP8X4), lhsT_scale=k2_scales,
-                rhs=v_codes[:, cols].bitcast(FP8X4), rhs_scale=v_scales[:, cols], start=True, stop=True,
-            )
-            kv_banks[b, j, h] = bank
-
-        def O(b, j, h, copy=None):
-            if (b, j) not in kv_rows:
-                kv_rows[b, j] = rows.tile([P, E], F32, name="kv_rows", bufs=ROWS)
-            (copy or nc.scalar.copy)(out=kv_rows[b, j][:, h * BANK : (h + 1) * BANK], in_=kv_banks[b, j, h][:])
-
-        def OV(b, j, h):
-            O(b, j, h, nc.vector.tensor_copy)
-
-        def STH(b, j, h):
-            cols = slice(h * BANK, (h + 1) * BANK)
-            nc.sync.dma_start(out=out_0[b, j * P : (j + 1) * P, cols], in_=kv_rows[b, j][:, cols])
-
-        def ST(b, j):
-            nc.sync.dma_start(out=out_0[b, j * P : (j + 1) * P, :], in_=kv_rows[b, j][:])
-
-        w_raws = {}
-
-        def LX(b, half):
-            tokens = x[b].rearrange("(p t) c -> p t c", t=T)
-            pair = slice(2 * half, 2 * half + 2)
-            nc.sync.dma_start(out=x_raw[b][:, pair, :], in_=tokens[:, pair, :])
-
-        def LW(i, g):
-            w_raw = raw.tile([P, PACK, E], BF16, name="w_raw")
-            w = (wk, wv)[i]
-            for u in range(2):
-                first = g * P * PACK + u * 2 * P
-                nc.sync.dma_start(
-                    out=w_raw[:, 2 * u : 2 * u + 2, :],
-                    in_=w[first : first + 2 * P, :].rearrange("(q e) n -> q e n", e=2),
-                )
-            w_raws[i, g] = w_raw
-
-        def LWH(i, g, h):
-            w = (wk, wv)[i]
-            cols = slice(h * BANK, (h + 1) * BANK)
-            if h == 0:
-                w_raws[i, g] = raw.tile([P, PACK, E], BF16, name="w_raw")
-            for u in range(2):
-                first = g * P * PACK + u * 2 * P
-                nc.sync.dma_start(
-                    out=w_raws[i, g][:, 2 * u : 2 * u + 2, cols],
-                    in_=w[first : first + 2 * P, cols].rearrange("(q e) n -> q e n", e=2),
-                )
-
-        def LB(i):
-            nc.sync.dma_start(out=bias_rows[0:1, i, :], in_=(bk, bv)[i].unsqueeze(0))
-
-        bias_banks = {}
-
-        def BM(i):
-            bank = psum.tile([P, E], BF16, name="bank")
+        def multiply(b, j):
+            k2_codes, k2_scales = k2_quantised[b, j // 2]
+            v_codes, v_scales = v_quantised[b]
+            keys = slice(j % 2 * P, (j % 2 + 1) * P)
             for h in range(HALVES):
-                cols = slice(h * BANK, (h + 1) * BANK)
-                nc.tensor.matmul(out=bank[:, cols], lhsT=ones_bf[:], rhs=bias_rows[:, i, cols], start=True, stop=True)
-            bias_banks[i] = bank
+                bank = psum.tile([P, BANK], F32, name="bank")
+                nc.tensor.matmul_mx(
+                    out=bank[:], lhsT=k2_codes[:, keys].bitcast(FP8X4), lhsT_scale=k2_scales[:, keys],
+                    rhs=v_codes[:, half(h)].bitcast(FP8X4), rhs_scale=v_scales[:, half(h)], start=True, stop=True,
+                )
+                kv_banks[b, j, h] = bank
 
-        def BC(i):
-            nc.scalar.copy(out=bias_all[:, i, :], in_=bias_banks[i][:])
+        def empty_bank(copy, b, j, h):
+            if (b, j) not in kv_rows:
+                kv_rows[b, j] = rows.tile([P, E], F32, name="kv_rows")
+            copy(out=kv_rows[b, j][:, half(h)], in_=kv_banks[b, j, h][:])
 
-        x_banks = {}
-        x_grps = {}
-        w_grps = {}
-
-        def XT(b, t):
-            words = x_raw[b][:].bitcast(F32)
-            bank = psum.tile([P, BANK], F32, name="bank")
-            for q in range(PASSES * 2):
-                nc.tensor.transpose(bank[:, q * P : (q + 1) * P], words[:, t, q * P : (q + 1) * P], ident[:])
-            x_banks[b, t] = bank
-
-        def XC(b, t):
-            if t % 2 == 0:
-                x_grps[b, t // 2] = grouped_pool.tile([P, 2, PASSES * P * PACK], BF16, align_bytes=64, name="x_grp")
-            nc.scalar.copy(
-                out=x_grps[b, t // 2][:, t % 2, :].bitcast(F32).rearrange("p (g r u) -> p g r u", g=PASSES, u=2),
-                in_=x_banks[b, t][:].rearrange("p (g u r) -> p g r u", g=PASSES, u=2),
-            )
-
-        def XQ(b, t):
-            i = b * T + t
-            nc.vector.quantize_mx(
-                out=x_codes[:, i, :].bitcast(FP8X4), scales=x_scales[:, i, :], in_=x_grps[b, t // 2][:, t % 2, :]
-            )
-
-        def XQ2(b, p):
-            i = b * T + 2 * p
-            nc.vector.quantize_mx(
-                out=x_codes[:, i : i + 2, :].rearrange("p i c -> p (i c)").bitcast(FP8X4),
-                scales=x_scales[:, i : i + 2, :].rearrange("p i c -> p (i c)"),
-                in_=x_grps[b, p][:].rearrange("p i c -> p (i c)"),
-            )
-
-        def regroup(copy, i, g, cols):
-            if (i, g) not in w_grps:
-                w_grps[i, g] = grouped_pool.tile([P, E, PACK], BF16, align_bytes=64, name="w_grp")
-            copy(
-                out=w_grps[i, g][:, cols, :].rearrange("p (c i) t -> p c t i", i=4),
-                in_=w_raws[i, g][:, :, cols].rearrange("p t (c i) -> p c t i", i=4),
-            )
-
-        def WQF(i, g):
-            nc.vector.quantize_mx(
-                out=w_codes[i][:, g, :].bitcast(FP8X4), scales=w_scales[i][:, g, :],
-                in_=w_grps[i, g][:].rearrange("p n t -> p (n t)"),
-            )
-
-        def WGV(i, g):
-            regroup(nc.vector.tensor_copy, i, g, slice(0, min(BANK, VECTOR_COLS[i][g])))
-
-        def WGW(i, g):
-            regroup(nc.vector.tensor_copy, i, g, slice(BANK, VECTOR_COLS[i][g]))
-
-        def WGS(i, g):
-            regroup(nc.scalar.copy, i, g, slice(VECTOR_COLS[i][g], E))
-
-        def WQ(i, g, h):
-            cols = slice(h * BANK, (h + 1) * BANK)
-            nc.vector.quantize_mx(
-                out=w_codes[i][:, g, cols].bitcast(FP8X4), scales=w_scales[i][:, g, cols],
-                in_=w_grps[i, g][:, cols, :].rearrange("p n t -> p (n t)"),
-            )
+        def store(b, j, cols=slice(0, E)):
+            nc.sync.dma_start(out=out_0[b, j * P : (j + 1) * P, cols], in_=kv_rows[b, j][:, cols])
 
         with tc.tile_pool(name="loaded", bufs=1) as loaded, tc.tile_pool(name="raw", bufs=3) as raw, tc.tile_pool(
             name="grouped", bufs=2
-        ) as grouped_pool:
+        ) as grouped:
             x_raw = [loaded.tile([P, T, C], BF16, name="x_raw%d" % b) for b in range(B)]
-            LWH(0, 0, 0)
-            WGV(0, 0)
-            WQ(0, 0, 0)
-            LX(0, 0)
-            XT(0, 0)
-            XC(0, 0)
-            XT(0, 1)
-            XC(0, 1)
-            LWH(0, 0, 1)
-            WGW(0, 0)
-            WGS(0, 0)
-            XQ(0, 0)
-            LB(0)
-            BM(0)
-            BC(0)
-            LB(1)
-            BM(1)
-            BC(1)
-            LWH(0, 1, 0)
-            WGV(0, 1)
-            XQ(0, 1)
-            WQ(0, 1, 0)
-            LWH(0, 1, 1)
-            WGW(0, 1)
-            WGS(0, 1)
-            WQ(0, 0, 1)
-            WQ(0, 1, 1)
-            LX(0, 1)
-            XT(0, 2)
-            XT(0, 3)
-            KP(0, 0)
-            XC(0, 2)
-            KP(0, 1)
-            XC(0, 3)
-            XQ(0, 2)
-            XQ(0, 3)
-            KP(0, 2)
-            KE(0, 0)
-            KE(0, 1)
-            KE(0, 2)
-            KT2(0, 0)
-            LW(1, 0)
-            WGS(1, 0)
-            LW(1, 1)
-            WGV(1, 1)
-            LX(1, 0)
-            XT(1, 0)
-            XC(1, 0)
-            XT(1, 1)
-            KG(0, 0)
-            KP(0, 3)
-            XC(1, 1)
-            WGS(1, 1)
-            XQ(1, 0)
-            KE(0, 3)
-            KG(0, 1)
-            WQF(1, 0)
-            KT2(0, 1)
-            XQ(1, 1)
-            LX(1, 1)
-            XT(1, 2)
-            XT(1, 3)
-            KP(1, 0)
-            XC(1, 2)
-            KP(1, 1)
-            XC(1, 3)
-            KE(1, 0)
-            KG(0, 2)
-            WQF(1, 1)
-            VP(0, 0)
-            KI2(0, 0)
-            VP(0, 1)
-            KG(0, 3)
-            KE(1, 1)
-            KR2(0, 0)
-            KSG(0, 0)
-            KSG(0, 1)
-            KH(0, 0)
-            XQ2(1, 1)
-        rows = ctx.enter_context(tc.tile_pool(name="rows", bufs=ROWS))
-        KP(1, 2)
-        KT2(1, 0)
-        KG(1, 0)
-        KH(0, 1)
-        VF(0, 0, 0)
-        KG(1, 1)
-        VF(0, 0, 1)
-        VP(0, 2)
-        KI2(0, 1)
-        VF(0, 1, 0)
-        VF(0, 1, 1)
-        KP(1, 3)
-        KR2(0, 1)
-        KSG(0, 2)
-        KH(0, 2)
-        KH(0, 3)
-        KE(1, 2)
-        VP(0, 3)
-        VF(0, 2, 0)
-        VF(0, 2, 1)
-        VP(1, 0)
-        KE(1, 3)
-        VP(1, 1)
-        KA(0, 1)
-        KI2(1, 0)
-        VF(0, 3, 0)
-        KT2(1, 1)
-        KR2(1, 0)
-        KH(1, 0)
-        KH(1, 1)
-        KG(1, 2)
-        KG(1, 3)
-        VF(0, 3, 1)
-        VP(1, 2)
-        VRS(0, 1)
-        VF(1, 0, 0)
-        VF(1, 0, 1)
-        VP(1, 3)
-        KN(0, 1, 1, 0)
-        VF(1, 1, 0)
-        VF(1, 1, 1)
-        VF(1, 2, 0)
-        VF(1, 2, 1)
-        VF(1, 3, 0)
-        KSG(0, 3)
-        VF(1, 3, 1)
-        KI2(1, 1)
-        VR(0, 0)
-        KR2(1, 1)
-        VQ(0, 0)
-        VQ(0, 1)
-        KA(0, 3)
-        KN(0, 3, 0, 1)
-        NR(0, 0)
-        NR(0, 1)
-        KH(1, 2)
-        KH(1, 3)
-        VRS(1, 1)
-        NB(0, 0)
-        NB(0, 1)
-        M2(0, 0)
-        M2(0, 1)
-        Q2(0, 0)
-        KS(1, 0)
-        Q2(0, 1)
-        KS(1, 1)
-        KS(1, 2)
-        VR(1, 0)
-        M2(0, 2)
-        KS(1, 3)
-        Q2(0, 2)
-        M2(0, 3)
-        VQ(1, 0)
-        KA(1, 1)
-        KN(1, 1, 1, 0)
-        KN(1, 2, 0, 0)
-        KV(0, 0, 0)
-        KV(0, 0, 1)
-        KV(0, 1, 0)
-        KV(0, 1, 1)
-        KV(0, 2, 0)
-        O(0, 0, 0)
-        KV(0, 2, 1)
-        O(0, 0, 1)
-        ST(0, 0)
-        KV(0, 3, 0)
-        O(0, 1, 0)
-        KV(0, 3, 1)
-        O(0, 1, 1)
-        ST(0, 1)
-        KN(1, 3, 0, 1)
-        O(0, 2, 0)
-        KV(0, 4, 0)
-        O(0, 2, 1)
-        ST(0, 2)
-        KV(0, 4, 1)
-        O(0, 3, 0)
-        KV(0, 5, 0)
-        O(0, 3, 1)
-        ST(0, 3)
-        KV(0, 5, 1)
-        O(0, 4, 0)
-        O(0, 4, 1)
-        ST(0, 4)
-        NR(1, 0)
-        NR(1, 1)
-        O(0, 5, 0)
-        O(0, 5, 1)
-        ST(0, 5)
-        Q2(0, 3)
-        KV(0, 6, 0)
-        KV(0, 6, 1)
-        KV(0, 7, 0)
-        KV(0, 7, 1)
-        O(0, 6, 0)
-        O(0, 6, 1)
-        ST(0, 6)
-        O(0, 7, 0)
-        O(0, 7, 1)
-        ST(0, 7)
-        VQ(1, 1)
-        NB(1, 0)
-        NB(1, 1)
-        M2(1, 0)
-        M2(1, 1)
-        Q2(1, 0)
-        KV(1, 0, 0)
-        KV(1, 0, 1)
-        KV(1, 1, 0)
-        KV(1, 1, 1)
-        O(1, 0, 0)
-        O(1, 0, 1)
-        ST(1, 0)
-        O(1, 1, 0)
-        M2(1, 2)
-        Q2(1, 1)
-        KV(1, 2, 0)
-        KV(1, 2, 1)
-        KV(1, 3, 0)
-        KV(1, 3, 1)
-        O(1, 2, 0)
-        O(1, 2, 1)
-        O(1, 3, 0)
-        OV(1, 1, 1)
-        ST(1, 1)
-        ST(1, 2)
-        M2(1, 3)
-        Q2(1, 2)
-        KV(1, 4, 0)
-        KV(1, 4, 1)
-        KV(1, 5, 0)
-        KV(1, 5, 1)
-        O(1, 4, 0)
-        O(1, 5, 0)
-        OV(1, 3, 1)
-        ST(1, 3)
-        O(1, 5, 1)
-        Q2(1, 3)
-        KV(1, 6, 0)
-        KV(1, 6, 1)
-        OV(1, 4, 1)
-        ST(1, 4)
-        ST(1, 5)
-        KV(1, 7, 0)
-        O(1, 6, 0)
-        OV(1, 6, 1)
-        ST(1, 6)
-        KV(1, 7, 1)
-        O(1, 7, 0)
-        STH(1, 7, 0)
-        OV(1, 7, 1)
-        STH(1, 7, 1)
+
+            def load_x(b, p):
+                pair = slice(2 * p, 2 * p + 2)
+                nc.sync.dma_start(
+                    out=x_raw[b][:, pair, :], in_=x[b].rearrange("(p t) c -> p t c", t=T)[:, pair, :]
+                )
+
+            w_raw = {}
+
+            def load_w(i, g):
+                w_raw[i, g] = raw.tile([P, PACK, E], BF16, name="w_raw")
+                for u in range(2):
+                    first = g * P * PACK + u * 2 * P
+                    nc.sync.dma_start(
+                        out=w_raw[i, g][:, 2 * u : 2 * u + 2, :],
+                        in_=(wk, wv)[i][first : first + 2 * P, :].rearrange("(q e) n -> q e n", e=2),
+                    )
+
+            load_w(KEYS, 0)
+            load_x(0, 0)
+            for i in (KEYS, VALUES):
+                nc.sync.dma_start(out=bias_rows[0:1, i, :], in_=(bk, bv)[i].unsqueeze(0))
+            load_w(KEYS, 1)
+            load_x(0, 1)
+            load_w(VALUES, 0)
+
+            x_banks, x_grps, w_grps, bias_banks = {}, {}, {}, {}
+
+            def multiply_bias(i):
+                bias_banks[i] = psum.tile([P, E], BF16, name="bank")
+                for h in range(HALVES):
+                    nc.tensor.matmul(
+                        out=bias_banks[i][:, half(h)], lhsT=ones_bf[:], rhs=bias_rows[:, i, half(h)],
+                        start=True, stop=True,
+                    )
+
+            def copy_bias(i):
+                nc.scalar.copy(out=bias_all[:, i, :], in_=bias_banks[i][:])
+
+            def transpose_x(b, t):
+                words = x_raw[b][:].bitcast(F32)
+                x_banks[b, t] = psum.tile([P, BANK], F32, name="bank")
+                for q in range(PASSES * 2):
+                    cols = slice(q * P, (q + 1) * P)
+                    nc.tensor.transpose(x_banks[b, t][:, cols], words[:, t, cols], ident[:])
+
+            def copy_x(b, t):
+                if t % 2 == 0:
+                    x_grps[b, t // 2] = grouped.tile([P, 2, C], BF16, align_bytes=64, name="x_grp")
+                nc.scalar.copy(
+                    out=x_grps[b, t // 2][:, t % 2, :].bitcast(F32).rearrange("p (g r u) -> p g r u", g=PASSES, u=2),
+                    in_=x_banks[b, t][:].rearrange("p (g u r) -> p g r u", g=PASSES, u=2),
+                )
+
+            def quantise_x(b, p):
+                tiles = slice(b * T + 2 * p, b * T + 2 * p + 2)
+                nc.vector.quantize_mx(
+                    out=x_codes[:, tiles, :].rearrange("p i c -> p (i c)").bitcast(FP8X4),
+                    scales=x_scales[:, tiles, :].rearrange("p i c -> p (i c)"),
+                    in_=x_grps[b, p][:].rearrange("p i c -> p (i c)"),
+                )
+
+            def regroup_w(copy, i, g, cols):
+                if (i, g) not in w_grps:
+                    w_grps[i, g] = grouped.tile([P, E, PACK], BF16, align_bytes=64, name="w_grp")
+                copy(
+                    out=w_grps[i, g][:, cols, :].rearrange("p (c i) t -> p c t i", i=4),
+                    in_=w_raw[i, g][:, :, cols].rearrange("p t (c i) -> p c t i", i=4),
+                )
+
+            def quantise_w(i, g, cols):
+                nc.vector.quantize_mx(
+                    out=w_codes[i][:, g, cols].bitcast(FP8X4), scales=w_scales[i][:, g, cols],
+                    in_=w_grps[i, g][:, cols, :].rearrange("p n t -> p (n t)"),
+                )
+
+            for g in range(PASSES):
+                regroup_w(nc.vector.tensor_copy, KEYS, g, slice(0, WK_VECTOR))
+                regroup_w(nc.scalar.copy, KEYS, g, slice(WK_VECTOR, E))
+                for h in range(HALVES):
+                    quantise_w(KEYS, g, half(h))
+                for t in (2 * g, 2 * g + 1):
+                    transpose_x(0, t)
+                    copy_x(0, t)
+                if g == 0:
+                    load_w(VALUES, 1)
+                    for p in range(2):
+                        load_x(1, p)
+                    for i in (KEYS, VALUES):
+                        multiply_bias(i)
+                        copy_bias(i)
+                quantise_x(0, g)
+
+            whole = slice(0, E)
+            regroup_w(nc.scalar.copy, VALUES, 0, whole)
+            for t in range(3):
+                project_keys(0, t)
+                add_key_bias(0, t)
+            total_rows(0, 0)
+            for t in range(2):
+                transpose_x(1, t)
+            copy_x(1, 0)
+            square_centred(0, 0)
+            copy_x(1, 1)
+            regroup_w(nc.vector.tensor_copy, VALUES, 1, slice(0, WV_VECTOR))
+            regroup_w(nc.scalar.copy, VALUES, 1, slice(WV_VECTOR, E))
+            project_keys(0, 3)
+            add_key_bias(0, 3)
+            quantise_x(1, 0)
+            quantise_w(VALUES, 0, whole)
+            total_rows(0, 1)
+            square_centred(0, 1)
+            for t in range(2, T):
+                transpose_x(1, t)
+                copy_x(1, t)
+            for t in range(2, T):
+                square_centred(0, t)
+            project_keys(1, 0)
+            add_key_bias(1, 0)
+            quantise_w(VALUES, 1, whole)
+            add_eps(0, 0)
+            project_keys(1, 1)
+            add_key_bias(1, 1)
+            quantise_x(1, 1)
+            invert_sums(0, 0)
+            total_rows(1, 0)
+        rows = ctx.enter_context(tc.tile_pool(name="rows", bufs=8))
+
+        for t in range(2):
+            scale_features(nc.gpsimd, 0, t)
+            square_features(0, t)
+            square_centred(1, t)
+            project_values(0, t)
+        add_value_bias(0, 0, 0)
+        add_value_bias(0, 0, 1)
+        add_eps(0, 1)
+        add_value_bias(0, 1, 0)
+        add_value_bias(0, 1, 1)
+        invert_sums(0, 1)
+        scale_features(nc.gpsimd, 0, 2)
+        add_squares(0, 1)
+        scale_features(nc.gpsimd, 0, 3)
+        for t in range(2, T):
+            square_features(0, t)
+        add_squares(0, 3)
+        project_keys(1, 2)
+        add_key_bias(1, 2)
+        project_values(0, 2)
+        add_value_bias(0, 2, 0)
+        add_value_bias(0, 2, 1)
+        project_keys(1, 3)
+        add_key_bias(1, 3)
+        add_eps(1, 0)
+        project_values(0, 3)
+        add_value_bias(0, 3, 0)
+        total_rows(1, 1)
+        invert_sums(1, 0)
+        add_value_bias(0, 3, 1)
+        for t in range(2):
+            square_features(1, t)
+        add_squares(1, 1)
+        for t in range(2, T):
+            square_centred(1, t)
+
+        for t in range(T):
+            project_values(1, t)
+            for h in range(HALVES):
+                add_value_bias(1, t, h)
+        sum_over_tokens(0, 1, True, False)
+        sum_over_tokens(0, 3, False, True)
+        add_eps(1, 1)
+        regroup_values(nc.vector.tensor_copy, 0, 0)
+        regroup_values(nc.scalar.copy, 0, 1)
+        invert_norms(0)
+        invert_sums(1, 1)
+        for t in range(2, T):
+            square_features(1, t)
+        for h in range(HALVES):
+            quantise_values(0, h)
+        regroup_values(nc.scalar.copy, 1, 1)
+        bound_norms(0)
+
+        def multiply_pair(b, q):
+            for j in (2 * q, 2 * q + 1):
+                multiply(b, j)
+
+        def empty_chunk(b, j):
+            for h in range(HALVES):
+                empty_bank(nc.scalar.copy, b, j, h)
+            store(b, j)
+
+        sum_over_tokens(1, 1, True, False)
+        sum_over_tokens(1, 2, False, False)
+        normalise_keys(0, 0)
+        normalise_keys(0, 1)
+        quantise_keys(0, 0)
+        multiply_pair(0, 0)
+        empty_chunk(0, 0)
+        empty_chunk(0, 1)
+        scale_features(nc.vector, 1, 0)
+        quantise_keys(0, 1)
+        multiply_pair(0, 1)
+        empty_chunk(0, 2)
+        empty_chunk(0, 3)
+        scale_features(nc.vector, 1, 1)
+        scale_features(nc.vector, 1, 2)
+        regroup_values(nc.vector.tensor_copy, 1, 0)
+        normalise_keys(0, 2)
+        scale_features(nc.vector, 1, 3)
+        quantise_keys(0, 2)
+        sum_over_tokens(1, 3, False, True)
+        multiply_pair(0, 2)
+        empty_chunk(0, 4)
+        invert_norms(1)
+        empty_chunk(0, 5)
+        normalise_keys(0, 3)
+        quantise_values(1, 0)
+        quantise_keys(0, 3)
+        multiply_pair(0, 3)
+        empty_chunk(0, 6)
+        empty_chunk(0, 7)
+        quantise_values(1, 1)
+        bound_norms(1)
+
+        pairs = E // PAIR
+        normalise_keys(1, 0)
+        for q in range(pairs):
+            if q + 1 < pairs:
+                normalise_keys(1, q + 1)
+            quantise_keys(1, q)
+            if q > 0:
+                empty_bank(nc.vector.tensor_copy, 1, 2 * q - 1, 1)
+                store(1, 2 * q - 1)
+            multiply_pair(1, q)
+            if q + 1 < pairs:
+                empty_chunk(1, 2 * q)
+            else:
+                empty_bank(nc.scalar.copy, 1, 2 * q, 0)
+            empty_bank(nc.scalar.copy, 1, 2 * q + 1, 0)
+        last = 2 * pairs - 1
+        empty_bank(nc.vector.tensor_copy, 1, last - 1, 1)
+        store(1, last - 1)
+        store(1, last, half(0))
+        empty_bank(nc.vector.tensor_copy, 1, last, 1)
+        store(1, last, half(1))

@@ -162,8 +162,9 @@ def tile_essattn_pa_kernel(tc, x, wk, bk, wv, bv, out_0, out_1):
             nc.vector.tensor_tensor(
                 out=v_all[b][:, t, half(h)], in0=v_banks[b, t][h][:], in1=bias_all[:, VALUES, half(h)], op=ALU.add
             )
-            if h == HALVES - 1:
-                nc.sync.dma_start(out=out_1[b].rearrange("(p t) e -> p t e", t=T)[:, t, :], in_=v_all[b][:, t, :])
+            if h == HALVES - 1 and t % 2 == 1:
+                pair = slice(t - 1, t + 1)
+                nc.sync.dma_start(out=out_1[b].rearrange("(p t) e -> p t e", t=T)[:, pair, :], in_=v_all[b][:, pair, :])
 
         def regroup_values(copy, b, h):
             if b not in v_grps:
@@ -240,12 +241,10 @@ def tile_essattn_pa_kernel(tc, x, wk, bk, wv, bv, out_0, out_1):
 
             def load_w(i, g):
                 w_raw[i, g] = raw.tile([P, PACK, E], BF16, name="w_raw")
-                for u in range(2):
-                    first = g * P * PACK + u * 2 * P
-                    nc.sync.dma_start(
-                        out=w_raw[i, g][:, 2 * u : 2 * u + 2, :],
-                        in_=(wk, wv)[i][first : first + 2 * P, :].rearrange("(q e) n -> q e n", e=2),
-                    )
+                channels = slice(g * P * PACK, (g + 1) * P * PACK)
+                nc.sync.dma_start(
+                    out=w_raw[i, g][:], in_=(wk, wv)[i][channels, :].rearrange("(p t) n -> p t n", t=PACK)
+                )
 
             load_w(KEYS, 0)
             load_x(0, 0)
@@ -269,11 +268,11 @@ def tile_essattn_pa_kernel(tc, x, wk, bk, wv, bv, out_0, out_1):
                 nc.scalar.copy(out=bias_all[:, i, :], in_=bias_banks[i][:])
 
             def transpose_x(b, t):
-                words = x_raw[b][:].bitcast(F32)
+                words = x_raw[b][:].bitcast(F32).rearrange("p t (g r u) -> p t g u r", g=PASSES, u=2)
                 x_banks[b, t] = psum.tile([P, BANK], F32, name="bank")
                 for q in range(PASSES * 2):
                     cols = slice(q * P, (q + 1) * P)
-                    nc.tensor.transpose(x_banks[b, t][:, cols], words[:, t, cols], ident[:])
+                    nc.tensor.transpose(x_banks[b, t][:, cols], words[:, t, q // 2, q % 2, :], ident[:])
 
             def copy_x(b, t):
                 if t % 2 == 0:

@@ -134,24 +134,23 @@ def tile_essattn_pa_kernel(tc, x, wk, bk, wv, bv, out_0, out_1):
         def add_squares(b, t):
             nc.gpsimd.tensor_tensor(out=squares[b, t][:], in0=squares[b, t - 1][:], in1=squares[b, t][:], op=ALU.add)
 
-        def sum_over_tokens(b, t, first, last):
-            if first:
-                sum_banks[b] = [psum.tile([P, BANK], F32, name="sums", bufs=HALVES) for h in range(HALVES)]
-            for h in range(HALVES):
-                nc.tensor.matmul(
-                    out=sum_banks[b][h][:], lhsT=ones_f32[:], rhs=squares[b, t][:, half(h)], start=first, stop=last
-                )
+        def open_sums(b):
+            sum_banks[b] = [psum.tile([P, BANK], F32, name="sums", bufs=HALVES) for h in range(HALVES)]
+
+        def sum_over_tokens(b, t, h, first=False, last=False):
+            nc.tensor.matmul(
+                out=sum_banks[b][h][:], lhsT=ones_f32[:], rhs=squares[b, t][:, half(h)], start=first, stop=last
+            )
 
         def invert_norms(b):
             inv_norms[b] = stage.tile([P, E], F32, name="inv_norm")
             for h in range(HALVES):
                 nc.scalar.activation(out=inv_norms[b][:, half(h)], in_=sum_banks[b][h][:], func=ACT.Abs_reciprocal_sqrt)
 
-        def bound_norms(b):
-            for h in range(HALVES):
-                nc.vector.tensor_scalar_min(
-                    out=inv_norms[b][:, half(h)], in0=inv_norms[b][:, half(h)], scalar1=1.0 / EPS_NORM
-                )
+        def bound_norms(b, h):
+            nc.vector.tensor_scalar_min(
+                out=inv_norms[b][:, half(h)], in0=inv_norms[b][:, half(h)], scalar1=1.0 / EPS_NORM
+            )
 
         v_banks, v_grps, v_quantised = {}, {}, {}
 
@@ -396,8 +395,10 @@ def tile_essattn_pa_kernel(tc, x, wk, bk, wv, bv, out_0, out_1):
             project_values(1, t)
             for h in range(HALVES):
                 add_value_bias(1, t, h)
-        sum_over_tokens(0, 1, True, False)
-        sum_over_tokens(0, 3, False, True)
+        open_sums(0)
+        for h in range(HALVES):
+            sum_over_tokens(0, 1, h, first=True)
+            sum_over_tokens(0, 3, h, last=True)
         add_eps(1, 1)
         regroup_values(nc.vector.tensor_copy, 0, 0)
         regroup_values(nc.scalar.copy, 0, 1)
@@ -408,7 +409,6 @@ def tile_essattn_pa_kernel(tc, x, wk, bk, wv, bv, out_0, out_1):
         for h in range(HALVES):
             quantise_values(0, h)
         regroup_values(nc.scalar.copy, 1, 1)
-        bound_norms(0)
 
         def multiply_pair(b, q):
             for j in (2 * q, 2 * q + 1):
@@ -419,26 +419,32 @@ def tile_essattn_pa_kernel(tc, x, wk, bk, wv, bv, out_0, out_1):
                 empty_bank(nc.scalar.copy, b, j, h)
             store(b, j)
 
-        sum_over_tokens(1, 1, True, False)
-        sum_over_tokens(1, 2, False, False)
+        open_sums(1)
+        for h in range(HALVES):
+            sum_over_tokens(1, 1, h, first=True)
+        for h in range(HALVES):
+            sum_over_tokens(1, 2, h)
+        bound_norms(0, 0)
         normalise_keys(0, 0)
-        normalise_keys(0, 1)
+        bound_norms(0, 1)
         quantise_keys(0, 0)
         multiply_pair(0, 0)
         empty_chunk(0, 0)
         empty_chunk(0, 1)
+        normalise_keys(0, 1)
         scale_features(nc.vector, 1, 0)
         quantise_keys(0, 1)
         multiply_pair(0, 1)
         empty_chunk(0, 2)
         empty_chunk(0, 3)
         scale_features(nc.vector, 1, 1)
-        scale_features(nc.vector, 1, 2)
-        regroup_values(nc.vector.tensor_copy, 1, 0)
         normalise_keys(0, 2)
-        scale_features(nc.vector, 1, 3)
+        scale_features(nc.vector, 1, 2)
         quantise_keys(0, 2)
-        sum_over_tokens(1, 3, False, True)
+        scale_features(nc.vector, 1, 3)
+        regroup_values(nc.vector.tensor_copy, 1, 0)
+        for h in range(HALVES):
+            sum_over_tokens(1, 3, h, last=True)
         multiply_pair(0, 2)
         empty_chunk(0, 4)
         invert_norms(1)
@@ -450,19 +456,19 @@ def tile_essattn_pa_kernel(tc, x, wk, bk, wv, bv, out_0, out_1):
         empty_chunk(0, 6)
         empty_chunk(0, 7)
         quantise_values(1, 1)
-        bound_norms(1)
 
         pairs = E // PAIR
+        bound_norms(1, 0)
         normalise_keys(1, 0)
+        bound_norms(1, 1)
         for q in range(pairs):
-            if q + 1 < pairs:
-                normalise_keys(1, q + 1)
             quantise_keys(1, q)
             if q > 0:
                 empty_bank(nc.vector.tensor_copy, 1, 2 * q - 1, 1)
                 store(1, 2 * q - 1)
             multiply_pair(1, q)
             if q + 1 < pairs:
+                normalise_keys(1, q + 1)
                 empty_chunk(1, 2 * q)
             else:
                 empty_bank(nc.scalar.copy, 1, 2 * q, 0)

from contextlib import ExitStack

import concourse.mybir as mybir
from concourse.masks import make_identity

F32 = mybir.dt.float32
BF16 = mybir.dt.bfloat16
U32 = mybir.dt.uint32
U8 = mybir.dt.uint8
FP8X4 = mybir.dt.float8_e4m3fn_x4
ALU = mybir.AluOpType
ACT = mybir.ActivationFunctionType
AXIS_X = mybir.AxisListType.X

P = 128
PACK = 4
B, N, C, E = 2, 512, 1024, 1024
T = N // P
PASSES = C // (P * PACK)
BANK = 512
HALVES = E // BANK
PAIR = 2 * P
LINE = 4
EPS_SUM = 1e-7
EPS_NORM = 1e-12
KEYS, VALUES = 0, 1
WK_VECTOR = 768
WV_VECTOR = 512

FLOPS = 2 * (2 * B * N * C * E) + 2 * B * N * E * E


def half(h):
    return slice(h * BANK, (h + 1) * BANK)


def tile_essattn_pa_kernel(tc, x, wk, bk, wv, bv, out_0, out_1):
    nc = tc.nc
    with ExitStack() as ctx:
        const = ctx.enter_context(tc.tile_pool(name="const", bufs=1))
        keep = ctx.enter_context(tc.tile_pool(name="keep", bufs=1))
        stage = ctx.enter_context(tc.tile_pool(name="stage", bufs=2))
        work = ctx.enter_context(tc.tile_pool(name="work", bufs=3))
        small = ctx.enter_context(tc.tile_pool(name="small", bufs=4))
        psum = ctx.enter_context(tc.psum_pool(name="psum", bufs=6))
        ctx.enter_context(tc.manual_schedule())

        ident = const.tile([P, P], F32)
        make_identity(nc, ident[:])
        ones_bf = const.tile([P, P], BF16)
        nc.vector.memset(ones_bf[:], 1.0)
        ones_f32 = const.tile([P, P], F32)
        nc.vector.memset(ones_f32[:], 1.0)
        warm = const.tile([P, 1], F32)
        nc.scalar.activation(out=warm[:], in_=ones_f32[:, 0:1], func=ACT.Abs_reciprocal_sqrt)
        bias_rows = const.tile([P, 2, E], BF16)
        nc.gpsimd.memset(bias_rows[:], 0.0)
        bias_all = const.tile([P, 2, E], BF16)
        f_sums = {(b, p): const.tile([P, 2, 2], F32, name="f_sums%d%d" % (b, p)) for b in range(B) for p in range(2)}
        for pair_sums in f_sums.values():
            nc.vector.memset(pair_sums[:], E * E * EPS_SUM)

        x_codes = keep.tile([P, B * T, PASSES * P], U32, align_bytes=64)
        x_scales = keep.tile([P, B * T, PASSES * P], U8, align_bytes=64)
        w_codes = [keep.tile([P, PASSES, E], U32, align_bytes=64, name="w_codes%d" % i) for i in (KEYS, VALUES)]
        w_scales = [keep.tile([P, PASSES, E], U8, align_bytes=64, name="w_scales%d" % i) for i in (KEYS, VALUES)]
        g_all = [keep.tile([P, T, E], F32, name="g_all%d" % b) for b in range(B)]
        v_all = [keep.tile([P, T, E], F32, name="v_all%d" % b) for b in range(B)]

        def project(weight, b, t):
            banks = []
            for h in range(HALVES):
                bank = psum.tile([P, BANK], F32, name="bank")
                for g in range(PASSES):
                    toks = slice(g * P, (g + 1) * P)
                    nc.tensor.matmul_mx(
                        out=bank[:],
                        lhsT=x_codes[:, b * T + t, toks].bitcast(FP8X4),
                        lhsT_scale=x_scales[:, b * T + t, toks],
                        rhs=w_codes[weight][:, g, half(h)].bitcast(FP8X4),
                        rhs_scale=w_scales[weight][:, g, half(h)],
                        start=(g == 0),
                        stop=(g == PASSES - 1),
                    )
                banks.append(bank)
            return banks

        k_banks, feats, row_sums, totals, inv_sums, squares = {}, {}, {}, {}, {}, {}
        sum_banks, inv_norms = {}, {}

        def project_keys(b, t):
            k_banks[b, t] = project(KEYS, b, t)

        def add_key_bias(b, t):
            if t % 2 == 0:
                row_sums[b, t // 2] = small.tile([P, 2, HALVES], F32, name="row_sums")
            feats[b, t] = work.tile([P, E], F32, name="feats", bufs=6)
            for h in range(HALVES):
                nc.vector.scalar_tensor_tensor(
                    out=feats[b, t][:, half(h)], in0=k_banks[b, t][h][:], scalar=1.0, in1=bias_all[:, KEYS, half(h)],
                    op0=ALU.mult, op1=ALU.add, accum_out=row_sums[b, t // 2][:, t % 2, h : h + 1],
                )

        def total_rows(b, p):
            totals[b, p] = small.tile([P, 2], F32, name="totals")
            nc.vector.tensor_reduce(out=totals[b, p][:], in_=row_sums[b, p][:], axis=AXIS_X, op=ALU.add)

        def square_centred(b, t):
            nc.scalar.activation(
                out=feats[b, t][:], in_=feats[b, t][:], func=ACT.Square, bias=totals[b, t // 2][:, t % 2 : t % 2 + 1],
                scale=-float(E), accum_out=f_sums[b, t // 2][:, t % 2, 0:1],
            )

        def add_eps(b, p):
            inv_sums[b, p] = small.tile([P, 2], F32, name="inv_sums")
            nc.vector.tensor_reduce(out=inv_sums[b, p][:], in_=f_sums[b, p][:], axis=AXIS_X, op=ALU.add)

        def invert_sums(b, p):
            nc.vector.reciprocal(out=inv_sums[b, p][:], in_=inv_sums[b, p][:])

        def inv_sum(b, t):
            return inv_sums[b, t // 2][:, t % 2 : t % 2 + 1]

        def scale_features(engine, b, t):
            engine.tensor_scalar(
                out=g_all[b][:, t, :], in0=feats[b, t][:], scalar1=inv_sum(b, t), scalar2=0.0,
                op0=ALU.mult, op1=ALU.add,
            )

        def square_features(b, t):
            squares[b, t] = work.tile([P, E], F32, name="squares", bufs=5)
            nc.scalar.activation(out=squares[b, t][:], in_=feats[b, t][:], func=ACT.Square, scale=inv_sum(b, t))

        def add_squares(b, t):
            nc.gpsimd.tensor_tensor(out=squares[b, t][:], in0=squares[b, t - 1][:], in1=squares[b, t][:], op=ALU.add)

        def open_sums(b):
            sum_banks[b] = [psum.tile([P, BANK], F32, name="sums", bufs=HALVES) for h in range(HALVES)]

        def sum_over_tokens(b, t, h, first=False, last=False):
            nc.tensor.matmul(
                out=sum_banks[b][h][:], lhsT=ones_f32[:], rhs=squares[b, t][:, half(h)], start=first, stop=last
            )

        def invert_norms(b):
            inv_norms[b] = stage.tile([P, E], F32, name="inv_norm")
            for h in range(HALVES):
                nc.scalar.activation(out=inv_norms[b][:, half(h)], in_=sum_banks[b][h][:], func=ACT.Abs_reciprocal_sqrt)

        def bound_norms(b, h):
            nc.vector.tensor_scalar_min(
                out=inv_norms[b][:, half(h)], in0=inv_norms[b][:, half(h)], scalar1=1.0 / EPS_NORM
            )

        v_banks, v_grps, v_quantised = {}, {}, {}

        def project_values(b, t):
            v_banks[b, t] = project(VALUES, b, t)

        def add_value_bias(b, t, h):
            nc.vector.tensor_tensor(
                out=v_all[b][:, t, half(h)], in0=v_banks[b, t][h][:], in1=bias_all[:, VALUES, half(h)], op=ALU.add
            )
            if h == HALVES - 1 and t % 2 == 1:
                pair = slice(t - 1, t + 1)
                nc.sync.dma_start(out=out_1[b].rearrange("(p t) e -> p t e", t=T)[:, pair, :], in_=v_all[b][:, pair, :])

        def regroup_values(copy, b, h):
            if b not in v_grps:
                v_grps[b] = rows.tile([P, E, PACK], BF16, align_bytes=64, name="v_grp", bufs=2)
            copy(
                out=v_grps[b][:, half(h), :].rearrange("p (c i) t -> p c t i", i=LINE),
                in_=v_all[b][:, :, half(h)].rearrange("p t (c i) -> p c t i", i=LINE),
            )

        def quantise_values(b, h):
            if b not in v_quantised:
                v_codes = stage.tile([P, E], U32, align_bytes=64, name="v_codes")
                v_scales = stage.tile([P, E], U8, align_bytes=64, name="v_scales")
                v_quantised[b] = (v_codes, v_scales)
            v_codes, v_scales = v_quantised[b]
            nc.vector.quantize_mx(
                out=v_codes[:, half(h)].bitcast(FP8X4), scales=v_scales[:, half(h)],
                in_=v_grps[b][:, half(h), :].rearrange("p e t -> p (e t)"),
            )

        k2_grps, k2_quantised, kv_banks, kv_rows = {}, {}, {}, {}

        def normalise_keys(b, q):
            cols = slice(q * PAIR, (q + 1) * PAIR)
            k2_grps[b, q] = work.tile([P, PAIR, PACK], BF16, align_bytes=64, name="k2_grp", bufs=2)
            lines = [P, PAIR // LINE, PACK, LINE]
            nc.vector.tensor_tensor(
                out=k2_grps[b, q][:].rearrange("p (c i) t -> p c t i", i=LINE),
                in0=g_all[b][:, :, cols].rearrange("p t (c i) -> p c t i", i=LINE),
                in1=inv_norms[b][:, cols].rearrange("p (c i) -> p c i", i=LINE).unsqueeze(2).to_broadcast(lines),
                op=ALU.mult,
            )

        def quantise_keys(b, q):
            k2_codes = work.tile([P, PAIR], U32, align_bytes=64, name="k2_codes")
            k2_scales = work.tile([P, PAIR], U8, align_bytes=64, name="k2_scales")
            nc.vector.quantize_mx(
                out=k2_codes[:].bitcast(FP8X4), scales=k2_scales[:], in_=k2_grps[b, q][:].rearrange("p e t -> p (e t)")
            )
            k2_quantised[b, q] = (k2_codes, k2_scales)

        def multiply(b, j):
            k2_codes, k2_scales = k2_quantised[b, j // 2]
            v_codes, v_scales = v_quantised[b]
            keys = slice(j % 2 * P, (j % 2 + 1) * P)
            for h in range(HALVES):
                bank = psum.tile([P, BANK], F32, name="bank")
                nc.tensor.matmul_mx(
                    out=bank[:], lhsT=k2_codes[:, keys].bitcast(FP8X4), lhsT_scale=k2_scales[:, keys],
                    rhs=v_codes[:, half(h)].bitcast(FP8X4), rhs_scale=v_scales[:, half(h)], start=True, stop=True,
                )
                kv_banks[b, j, h] = bank

        def empty_bank(copy, b, j, h):
            if (b, j) not in kv_rows:
                kv_rows[b, j] = rows.tile([P, E], F32, name="kv_rows")
            copy(out=kv_rows[b, j][:, half(h)], in_=kv_banks[b, j, h][:])

        def store(b, j, cols=slice(0, E)):
            nc.sync.dma_start(out=out_0[b, j * P : (j + 1) * P, cols], in_=kv_rows[b, j][:, cols])

        with tc.tile_pool(name="loaded", bufs=1) as loaded, tc.tile_pool(name="raw", bufs=3) as raw, tc.tile_pool(
            name="grouped", bufs=2
        ) as grouped:
            x_raw = [loaded.tile([P, T, C], BF16, name="x_raw%d" % b) for b in range(B)]

            def load_x(b, p):
                pair = slice(2 * p, 2 * p + 2)
                nc.sync.dma_start(
                    out=x_raw[b][:, pair, :], in_=x[b].rearrange("(p t) c -> p t c", t=T)[:, pair, :]
                )

            w_raw = {}

            def load_w(i, g):
                w_raw[i, g] = raw.tile([P, PACK, E], BF16, name="w_raw")
                channels = slice(g * P * PACK, (g + 1) * P * PACK)
                nc.sync.dma_start(
                    out=w_raw[i, g][:], in_=(wk, wv)[i][channels, :].rearrange("(p t) n -> p t n", t=PACK)
                )

            load_w(KEYS, 0)
            load_x(0, 0)
            for i in (KEYS, VALUES):
                nc.sync.dma_start(out=bias_rows[0:1, i, :], in_=(bk, bv)[i].unsqueeze(0))
            load_w(KEYS, 1)
            load_x(0, 1)
            load_w(VALUES, 0)

            x_banks, x_grps, w_grps, bias_banks = {}, {}, {}, {}

            def multiply_bias(i):
                bias_banks[i] = psum.tile([P, E], BF16, name="bank")
                for h in range(HALVES):
                    nc.tensor.matmul(
                        out=bias_banks[i][:, half(h)], lhsT=ones_bf[:], rhs=bias_rows[:, i, half(h)],
                        start=True, stop=True,
                    )

            def copy_bias(i):
                nc.scalar.copy(out=bias_all[:, i, :], in_=bias_banks[i][:])

            def transpose_x(b, t):
                words = x_raw[b][:].bitcast(F32).rearrange("p t (g r u) -> p t g u r", g=PASSES, u=2)
                x_banks[b, t] = psum.tile([P, BANK], F32, name="bank")
                for q in range(PASSES * 2):
                    cols = slice(q * P, (q + 1) * P)
                    nc.tensor.transpose(x_banks[b, t][:, cols], words[:, t, q // 2, q % 2, :], ident[:])

            def copy_x(b, t):
                if t % 2 == 0:
                    x_grps[b, t // 2] = grouped.tile([P, 2, C], BF16, align_bytes=64, name="x_grp")
                nc.scalar.copy(
                    out=x_grps[b, t // 2][:, t % 2, :].bitcast(F32).rearrange("p (g r u) -> p g r u", g=PASSES, u=2),
                    in_=x_banks[b, t][:].rearrange("p (g u r) -> p g r u", g=PASSES, u=2),
                )

            def quantise_x(b, p):
                tiles = slice(b * T + 2 * p, b * T + 2 * p + 2)
                nc.vector.quantize_mx(
                    out=x_codes[:, tiles, :].rearrange("p i c -> p (i c)").bitcast(FP8X4),
                    scales=x_scales[:, tiles, :].rearrange("p i c -> p (i c)"),
                    in_=x_grps[b, p][:].rearrange("p i c -> p (i c)"),
                )

            def regroup_w(copy, i, g, cols):
                if (i, g) not in w_grps:
                    w_grps[i, g] = grouped.tile([P, E, PACK], BF16, align_bytes=64, name="w_grp")
                copy(
                    out=w_grps[i, g][:, cols, :].rearrange("p (c i) t -> p c t i", i=4),
                    in_=w_raw[i, g][:, :, cols].rearrange("p t (c i) -> p c t i", i=4),
                )

            def quantise_w(i, g, cols):
                nc.vector.quantize_mx(
                    out=w_codes[i][:, g, cols].bitcast(FP8X4), scales=w_scales[i][:, g, cols],
                    in_=w_grps[i, g][:, cols, :].rearrange("p n t -> p (n t)"),
                )

            for g in range(PASSES):
                regroup_w(nc.vector.tensor_copy, KEYS, g, slice(0, WK_VECTOR))
                regroup_w(nc.scalar.copy, KEYS, g, slice(WK_VECTOR, E))
                for h in range(HALVES):
                    quantise_w(KEYS, g, half(h))
                for t in (2 * g, 2 * g + 1):
                    transpose_x(0, t)
                    copy_x(0, t)
                if g == 0:
                    load_w(VALUES, 1)
                    for p in range(2):
                        load_x(1, p)
                    for i in (KEYS, VALUES):
                        multiply_bias(i)
                        copy_bias(i)
                quantise_x(0, g)

            whole = slice(0, E)
            regroup_w(nc.scalar.copy, VALUES, 0, whole)
            for t in range(3):
                project_keys(0, t)
                add_key_bias(0, t)
            total_rows(0, 0)
            for t in range(2):
                transpose_x(1, t)
            copy_x(1, 0)
            square_centred(0, 0)
            copy_x(1, 1)
            regroup_w(nc.vector.tensor_copy, VALUES, 1, slice(0, WV_VECTOR))
            regroup_w(nc.scalar.copy, VALUES, 1, slice(WV_VECTOR, E))
            project_keys(0, 3)
            add_key_bias(0, 3)
            quantise_x(1, 0)
            quantise_w(VALUES, 0, whole)
            total_rows(0, 1)
            square_centred(0, 1)
            for t in range(2, T):
                transpose_x(1, t)
                copy_x(1, t)
            for t in range(2, T):
                square_centred(0, t)
            project_keys(1, 0)
            add_key_bias(1, 0)
            quantise_w(VALUES, 1, whole)
            add_eps(0, 0)
            project_keys(1, 1)
            add_key_bias(1, 1)
            quantise_x(1, 1)
            invert_sums(0, 0)
            total_rows(1, 0)
        rows = ctx.enter_context(tc.tile_pool(name="rows", bufs=8))

        for t in range(2):
            scale_features(nc.gpsimd, 0, t)
            square_features(0, t)
            square_centred(1, t)
            project_values(0, t)
        add_value_bias(0, 0, 0)
        add_value_bias(0, 0, 1)
        add_eps(0, 1)
        add_value_bias(0, 1, 0)
        add_value_bias(0, 1, 1)
        invert_sums(0, 1)
        scale_features(nc.gpsimd, 0, 2)
        add_squares(0, 1)
        scale_features(nc.gpsimd, 0, 3)
        for t in range(2, T):
            square_features(0, t)
        add_squares(0, 3)
        project_keys(1, 2)
        add_key_bias(1, 2)
        project_values(0, 2)
        add_value_bias(0, 2, 0)
        add_value_bias(0, 2, 1)
        project_keys(1, 3)
        add_key_bias(1, 3)
        add_eps(1, 0)
        project_values(0, 3)
        add_value_bias(0, 3, 0)
        total_rows(1, 1)
        invert_sums(1, 0)
        add_value_bias(0, 3, 1)
        for t in range(2):
            square_features(1, t)
        add_squares(1, 1)
        for t in range(2, T):
            square_centred(1, t)

        for t in range(T):
            project_values(1, t)
            for h in range(HALVES):
                add_value_bias(1, t, h)
        open_sums(0)
        for h in range(HALVES):
            sum_over_tokens(0, 1, h, first=True)
            sum_over_tokens(0, 3, h, last=True)
        add_eps(1, 1)
        regroup_values(nc.vector.tensor_copy, 0, 0)
        regroup_values(nc.scalar.copy, 0, 1)
        invert_norms(0)
        invert_sums(1, 1)
        for t in range(2, T):
            square_features(1, t)
        for h in range(HALVES):
            quantise_values(0, h)
        regroup_values(nc.scalar.copy, 1, 1)

        def multiply_pair(b, q):
            for j in (2 * q, 2 * q + 1):
                multiply(b, j)

        def empty_chunk(b, j):
            for h in range(HALVES):
                empty_bank(nc.scalar.copy, b, j, h)
            store(b, j)

        open_sums(1)
        for h in range(HALVES):
            sum_over_tokens(1, 1, h, first=True)
        for h in range(HALVES):
            sum_over_tokens(1, 2, h)
        bound_norms(0, 0)
        normalise_keys(0, 0)
        bound_norms(0, 1)
        quantise_keys(0, 0)
        multiply_pair(0, 0)
        empty_chunk(0, 0)
        empty_chunk(0, 1)
        normalise_keys(0, 1)
        scale_features(nc.vector, 1, 0)
        quantise_keys(0, 1)
        multiply_pair(0, 1)
        empty_chunk(0, 2)
        empty_chunk(0, 3)
        scale_features(nc.vector, 1, 1)
        normalise_keys(0, 2)
        scale_features(nc.vector, 1, 2)
        quantise_keys(0, 2)
        scale_features(nc.vector, 1, 3)
        regroup_values(nc.vector.tensor_copy, 1, 0)
        for h in range(HALVES):
            sum_over_tokens(1, 3, h, last=True)
        multiply_pair(0, 2)
        empty_chunk(0, 4)
        invert_norms(1)
        empty_chunk(0, 5)
        normalise_keys(0, 3)
        quantise_values(1, 0)
        quantise_keys(0, 3)
        multiply_pair(0, 3)
        empty_chunk(0, 6)
        empty_chunk(0, 7)
        quantise_values(1, 1)

        pairs = E // PAIR
        bound_norms(1, 0)
        normalise_keys(1, 0)
        bound_norms(1, 1)
        for q in range(pairs):
            quantise_keys(1, q)
            if q > 0:
                empty_bank(nc.vector.tensor_copy, 1, 2 * q - 1, 1)
                store(1, 2 * q - 1)
            multiply_pair(1, q)
            if q + 1 < pairs:
                normalise_keys(1, q + 1)
                empty_chunk(1, 2 * q)
            else:
                empty_bank(nc.scalar.copy, 1, 2 * q, 0)
            empty_bank(nc.scalar.copy, 1, 2 * q + 1, 0)
        last = 2 * pairs - 1
        empty_bank(nc.vector.tensor_copy, 1, last - 1, 1)
        store(1, last - 1)
        store(1, last, half(0))
        empty_bank(nc.vector.tensor_copy, 1, last, 1)
        store(1, last, half(1))
